import numpy as np
import ml_dtypes


def mxq(x, axis, fmt="e4m3"):
    dtype, down = {"e4m3": (ml_dtypes.float8_e4m3fn, 7), "e5m2": (ml_dtypes.float8_e5m2, 14)}[fmt]
    v = np.moveaxis(np.asarray(x, np.float32).astype(ml_dtypes.bfloat16).astype(np.float64), axis, -1)
    blocks = v.reshape(v.shape[:-1] + (-1, 32))
    amax = np.abs(blocks).max(-1, keepdims=True)
    byte = np.maximum(np.where(amax > 0, np.frexp(amax)[1] - 1 + 127, 0) - down, 1)
    scale = np.exp2(byte - 127.0)
    codes = (blocks / scale).astype(np.float32).astype(dtype).astype(np.float64)
    return np.moveaxis((codes * scale).reshape(v.shape), -1, axis)


WIDE = False


def mx_kscale(k):
    if not WIDE:
        return np.ones(k)
    levels = np.array([10, -10, 5, -5, 0])
    a = np.random.permutation(np.resize(levels, k // 512 * 4)).reshape(k // 512, 4)
    idx = np.arange(k)
    return np.exp2(a[idx // 512, idx % 128 // 32])


BF16 = ml_dtypes.bfloat16


def bf(x):
    return np.asarray(x, np.float32).astype(BF16)


def f64(x):
    return np.asarray(x).astype(np.float64)


B, S, D, O, G, P = 2, 2048, 1024, 128, 3, 3
NB = G + P


def silu(v):
    return v / (1.0 + np.exp(-v))


def extended_grid(d):
    pts = np.linspace(-1.0, 1.0, G + 1)
    h = 2.0 / G
    left = pts[0] + h * np.arange(-P, 0)
    right = pts[-1] + h * np.arange(1, P + 1)
    ext = np.concatenate([left, pts, right])
    return np.broadcast_to(ext, (d, ext.shape[0]))


def bspline_basis(x, grid):
    x = x[:, :, None]
    g = grid[None, :, :]
    bb = ((x >= g[..., :-1]) & (x < g[..., 1:])).astype(np.float64)
    for p in range(1, P + 1):
        left = (x - g[..., :-(p + 1)]) / (g[..., p:-1] - g[..., :-(p + 1)])
        right = (g[..., p + 1:] - x) / (g[..., p + 1:] - g[..., 1:-p])
        bb = left * bb[..., :-1] + right * bb[..., 1:]
    return bb


def setup_inputs():
    s = mx_kscale(D)
    u = s / s.max()
    return {"x": bf(np.random.standard_normal((B, S, D)) * u),
            "coef": bf(np.random.standard_normal((O, D, NB)) * 2.0 / np.sqrt(D)),
            "scale_base": bf((0.25 + (np.random.uniform(size=(O, D)) * 2.0 - 1.0) * 2.0) / np.sqrt(D) / u),
            "scale_sp": bf(1.0 + 0.1 * np.random.standard_normal((O, D))),
            "bias": bf(0.1 * np.random.standard_normal(O))}


def reference(x, coef, scale_base, scale_sp, bias):
    x = f64(x)
    b_, s_, d = x.shape
    xf = x.reshape(-1, d)
    grid = extended_grid(d)
    basis = bspline_basis(xf, grid)
    base = silu(xf)
    spline_w = f64(scale_sp)[..., None] * f64(coef)
    y_base = mxq(base, 1, "e4m3") @ mxq(f64(scale_base), 1, "e4m3").T
    bt = np.ascontiguousarray(basis.transpose(2, 0, 1))
    wt = np.ascontiguousarray(spline_w.transpose(2, 1, 0))
    y_sp = (mxq(bt, 2, "e4m3") @ mxq(wt, 1, "e4m3")).sum(0)
    y = y_base + y_sp + f64(bias)[None, :]
    return y.reshape(b_, s_, -1)

@@ -1,0 +1,174 @@
+import math
+from contextlib import ExitStack
+
+import concourse.bass as bass
+import concourse.mybir as mybir
+import concourse.tile as tile
+from concourse.masks import make_identity
+
+F32 = mybir.dt.float32
+BF16 = mybir.dt.bfloat16
+U32 = mybir.dt.uint32
+U8 = mybir.dt.uint8
+FP8X4 = mybir.dt.float8_e4m3fn_x4
+ACT = mybir.ActivationFunctionType
+ALU = mybir.AluOpType
+
+P = 128
+ROWS = 4096
+FEAT = 1024
+OUTS = 128
+NB = 6
+NFUN = NB + 1
+PASSES = 2
+CH_ROWS = 256
+BLK = CH_ROWS // P
+CHUNKS = ROWS // CH_ROWS
+W = PASSES * CH_ROWS * 4
+CW = W // 4
+FLOPS = 2 * ROWS * FEAT * OUTS * NFUN
+C6 = 1.0 / math.sqrt(6.0)
+
+
+def tile_kanoriginal_t_kernel(tc, x, coef, scale_base, scale_sp, bias, out):
+    nc = tc.nc
+    xv = x.flatten_outer_dims().rearrange("(c p j) i -> c p (j i)", p=P, j=BLK)
+    ov = out.flatten_outer_dims().rearrange("(c p j) o -> c p (j o)", p=P, j=BLK)
+    with ExitStack() as ctx:
+        const = ctx.enter_context(tc.tile_pool(name="const", bufs=1))
+        wprep = ctx.enter_context(tc.tile_pool(name="wprep", bufs=1))
+        xin = ctx.enter_context(tc.tile_pool(name="xin", bufs=3))
+        wide = ctx.enter_context(tc.tile_pool(name="wide", bufs=2))
+        half = ctx.enter_context(tc.tile_pool(name="half", bufs=2))
+        packed = ctx.enter_context(tc.tile_pool(name="packed", bufs=2))
+        pt = ctx.enter_context(tc.psum_pool(name="pt", bufs=2))
+        pa = ctx.enter_context(tc.psum_pool(name="pa", bufs=2))
+
+        ident_f = const.tile([P, P], F32)
+        make_identity(nc, ident_f[:])
+        ident_b = const.tile([P, P], BF16)
+        make_identity(nc, ident_b[:])
+
+        sb_sb = wprep.tile([P, FEAT], BF16)
+        nc.sync.dma_start(out=sb_sb[:], in_=scale_base)
+        sp_sb = wprep.tile([P, FEAT], BF16)
+        nc.sync.dma_start(out=sp_sb[:], in_=scale_sp)
+        coef_sb = wprep.tile([P, FEAT * NB], BF16)
+        nc.sync.dma_start(out=coef_sb[:], in_=coef.rearrange("o i b -> o (i b)"))
+        bias_b = const.tile([P, OUTS], BF16)
+        nc.sync.dma_start(out=bias_b[:], in_=bias.partition_broadcast(P))
+        bias_f = const.tile([P, OUTS], F32)
+        nc.vector.tensor_copy(out=bias_f[:], in_=bias_b[:])
+
+        wg = wprep.tile([P, NFUN, PASSES, OUTS, 4], BF16, align_bytes=64)
+        wt0 = pt.tile([P, PASSES, 2, OUTS], F32, tag="xt0")
+        sb_w = sb_sb[:].bitcast(F32)
+        for g in range(PASSES):
+            for u in range(2):
+                k = 2 * g + u
+                nc.tensor.transpose(wt0[:, g, u, :], sb_w[:, k * P:(k + 1) * P], ident_f[:])
+        nc.scalar.copy(
+            out=wg[:, 0].bitcast(F32),
+            in_=wt0[:].rearrange("p g u o -> p g o u"),
+        )
+        prod = wprep.tile([P, NB, 8, P], BF16)
+        coef_v = coef_sb[:].rearrange("o (w p e b) -> o b w e p", w=4, p=P, e=2, b=NB)
+        sp_v = sp_sb[:].rearrange("o (w p e) -> o w e p", w=4, p=P, e=2)
+        for b in range(NB):
+            nc.vector.tensor_tensor(
+                out=prod[:, b].rearrange("o (w e) p -> o w e p", w=4, e=2),
+                in0=coef_v[:, b],
+                in1=sp_v,
+                op=ALU.mult,
+            )
+        for b in range(NB):
+            wtb = pt.tile([P, PASSES, 4, OUTS], BF16, tag="xt1")
+            for g in range(PASSES):
+                for t in range(4):
+                    nc.tensor.transpose(wtb[:, g, t, :], prod[:, b, g * 4 + t, :], ident_b[:])
+            nc.scalar.copy(out=wg[:, 1 + b], in_=wtb[:].rearrange("p g t o -> p g o t"))
+        wcodes = const.tile([P, NFUN * PASSES * OUTS], U32, align_bytes=64)
+        wscales = const.tile([P, NFUN * PASSES * OUTS], U8, align_bytes=64)
+        wg_flat = wg[:].rearrange("p f g o t -> p (f g o t)")
+        start = 0
+        for width in (4096, 2048, 1024):
+            nc.vector.quantize_mx(
+                out=wcodes[:, start // 4:(start + width) // 4].bitcast(FP8X4),
+                scales=wscales[:, start // 4:(start + width) // 4],
+                in_=wg_flat[:, start:start + width],
+            )
+            start += width
+
+        for c in range(CHUNKS):
+            xs = xin.tile([P, BLK, FEAT], BF16)
+            nc.sync.dma_start(out=xs[:].rearrange("p j i -> p (j i)"), in_=xv[c])
+            v = half.tile([P, W], BF16, align_bytes=64)
+            v4 = v[:].rearrange("p (g n t) -> p g n t", g=PASSES, n=CH_ROWS, t=4)
+            for g in range(PASSES):
+                xt = pt.tile([P, 2, CH_ROWS], F32, tag="xt%d" % g)
+                for j in range(BLK):
+                    xw = xs[:, j, :].bitcast(F32)
+                    for u in range(2):
+                        k = 2 * g + u
+                        nc.tensor.transpose(xt[:, u, j * P:(j + 1) * P], xw[:, k * P:(k + 1) * P], ident_f[:])
+                nc.scalar.copy(out=v4[:, g].bitcast(F32), in_=xt[:].rearrange("p u n -> p n u"))
+
+            codes = packed.tile([P, NFUN, CW], U32, align_bytes=64)
+            scales = packed.tile([P, NFUN, CW], U8, align_bytes=64)
+
+            def quantise(f, src):
+                nc.vector.quantize_mx(out=codes[:, f, :].bitcast(FP8X4), scales=scales[:, f, :], in_=src)
+
+            sil = half.tile([P, W], BF16, align_bytes=64)
+            nc.scalar.activation(out=sil[:], in_=v[:], func=ACT.Silu)
+            quantise(0, sil[:])
+
+            for r in range(2):
+                e = wide.tile([P, W], F32)
+                nc.scalar.activation(out=e[:], in_=v[:], func=ACT.Abs, bias=0.5 - r, scale=1.5)
+                a2 = wide.tile([P, W], F32)
+                nc.scalar.activation(out=a2[:], in_=e[:], func=ACT.Abs, bias=-2.0, scale=1.0)
+                sq_a = wide.tile([P, W], F32)
+                nc.scalar.activation(out=sq_a[:], in_=e[:], func=ACT.Square, bias=-2.0 * C6, scale=C6)
+                sq_t = wide.tile([P, W], F32)
+                nc.scalar.activation(out=sq_t[:], in_=a2[:], func=ACT.Square, bias=-2.0 * C6, scale=C6)
+                n1u = half.tile([P, W], BF16, align_bytes=64)
+                nc.vector.scalar_tensor_tensor(out=n1u[:], in0=e[:], scalar=-2.0, in1=sq_a[:], op0=ALU.add, op1=ALU.mult)
+                n1p = half.tile([P, W], BF16, align_bytes=64)
+                nc.vector.scalar_tensor_tensor(out=n1p[:], in0=a2[:], scalar=-2.0, in1=sq_t[:], op0=ALU.add, op1=ALU.mult)
+                nc.vector.scalar_tensor_tensor(out=sq_t[:], in0=e[:], scalar=-2.0, in1=sq_t[:], op0=ALU.add, op1=ALU.mult)
+                nc.vector.scalar_tensor_tensor(out=sq_a[:], in0=a2[:], scalar=-2.0, in1=sq_a[:], op0=ALU.add, op1=ALU.mult)
+                n2u = half.tile([P, W], BF16, align_bytes=64)
+                nc.scalar.activation(out=n2u[:], in_=sq_t[:], func=ACT.Identity, bias=-2.0 / 3.0, scale=-3.0)
+                n2p = half.tile([P, W], BF16, align_bytes=64)
+                nc.scalar.activation(out=n2p[:], in_=sq_a[:], func=ACT.Identity, bias=-2.0 / 3.0, scale=-3.0)
+                nc.vector.tensor_tensor(out=n1u[:], in0=n1u[:], in1=n2u[:], op=ALU.max)
+                nc.vector.tensor_scalar(out=n1u[:], in0=n1u[:], scalar1=-1.0, scalar2=0.0, op0=ALU.mult, op1=ALU.max)
+                quantise(1 + r + 2, n1u[:])
+                nc.vector.tensor_tensor(out=n1p[:], in0=n1p[:], in1=n2p[:], op=ALU.max)
+                nc.vector.tensor_scalar(out=n1p[:], in0=n1p[:], scalar1=-1.0, scalar2=0.0, op0=ALU.mult, op1=ALU.max)
+                mask = half.tile([P, W], BF16, align_bytes=64)
+                nc.vector.tensor_scalar(out=mask[:], in0=v[:], scalar1=(2.0 * r - 1.0) / 3.0, scalar2=None, op0=ALU.is_lt)
+                nc.vector.tensor_tensor(out=mask[:], in0=n1p[:], in1=mask[:], op=ALU.mult)
+                quantise(1 + r, mask[:])
+                nc.vector.tensor_tensor(out=n1p[:], in0=n1p[:], in1=mask[:], op=ALU.subtract)
+                quantise(1 + r + 4, n1p[:])
+
+            res = xin.tile([P, BLK, OUTS], F32)
+            for j in range(BLK):
+                acc = pa.tile([P, OUTS], F32, tag="acc%d" % j)
+                for f in range(NFUN):
+                    for g in range(PASSES):
+                        lo = g * CH_ROWS + j * P
+                        wlo = (f * PASSES + g) * OUTS
+                        nc.tensor.matmul_mx(
+                            out=acc[:],
+                            lhsT=codes[:, f, lo:lo + P].bitcast(FP8X4),
+                            lhsT_scale=scales[:, f, lo:lo + P],
+                            rhs=wcodes[:, wlo:wlo + OUTS].bitcast(FP8X4),
+                            rhs_scale=wscales[:, wlo:wlo + OUTS],
+                            start=(f == 0 and g == 0),
+                            stop=(f == NFUN - 1 and g == PASSES - 1),
+                        )
+                nc.vector.tensor_tensor(out=res[:, j, :], in0=acc[:], in1=bias_f[:], op=ALU.add)
+            nc.sync.dma_start(out=ov[c], in_=res[:].rearrange("p j o -> p (j o)"))

@@ -1,9 +1,7 @@
 import math
 from contextlib import ExitStack
 
-import concourse.bass as bass
 import concourse.mybir as mybir
-import concourse.tile as tile
 from concourse.masks import make_identity
 
 F32 = mybir.dt.float32
@@ -24,10 +22,12 @@ PASSES = 2
 CH_ROWS = 256
 BLK = CH_ROWS // P
 CHUNKS = ROWS // CH_ROWS
+STEPS = 2 * CHUNKS
 W = PASSES * CH_ROWS * 4
 CW = W // 4
 FLOPS = 2 * ROWS * FEAT * OUTS * NFUN
 C6 = 1.0 / math.sqrt(6.0)
+ACT_EVERY = 4
 
 
 def tile_kanoriginal_t_kernel(tc, x, coef, scale_base, scale_sp, bias, out):
@@ -37,40 +37,196 @@ def tile_kanoriginal_t_kernel(tc, x, coef, scale_base, scale_sp, bias, out):
     with ExitStack() as ctx:
         const = ctx.enter_context(tc.tile_pool(name="const", bufs=1))
         wprep = ctx.enter_context(tc.tile_pool(name="wprep", bufs=1))
-        xin = ctx.enter_context(tc.tile_pool(name="xin", bufs=3))
+        three = ctx.enter_context(tc.tile_pool(name="three", bufs=3))
         wide = ctx.enter_context(tc.tile_pool(name="wide", bufs=2))
-        half = ctx.enter_context(tc.tile_pool(name="half", bufs=2))
-        packed = ctx.enter_context(tc.tile_pool(name="packed", bufs=2))
+        two = ctx.enter_context(tc.tile_pool(name="two", bufs=2))
+        one = ctx.enter_context(tc.tile_pool(name="one", bufs=1))
         pt = ctx.enter_context(tc.psum_pool(name="pt", bufs=2))
         pa = ctx.enter_context(tc.psum_pool(name="pa", bufs=2))
+        ctx.enter_context(tc.manual_schedule())
 
-        ident_f = const.tile([P, P], F32)
-        make_identity(nc, ident_f[:])
-        ident_b = const.tile([P, P], BF16)
-        make_identity(nc, ident_b[:])
+        xs_t = {}
+        xt_t = {}
+        v_t = {}
+        sil_t = {}
+        st = {}
+        codes_t = {}
+        scales_t = {}
+        acc_t = {}
+        done = {}
 
-        sb_sb = wprep.tile([P, FEAT], BF16)
-        nc.sync.dma_start(out=sb_sb[:], in_=scale_base)
+        def load_x(c):
+            xs = three.tile([P, BLK, FEAT], BF16, name="xs")
+            nc.sync.dma_start(out=xs[:].rearrange("p j i -> p (j i)"), in_=xv[c])
+            xs_t[c] = xs
+
+        def trans_x(c):
+            xs = xs_t[c]
+            for g in range(PASSES):
+                xt = pt.tile([P, 2, CH_ROWS], F32, tag="xt%d" % g, name="xt%d" % g)
+                for j in range(BLK):
+                    xw = xs[:, j, :].bitcast(F32)
+                    for u in range(2):
+                        k = 2 * g + u
+                        nc.tensor.transpose(xt[:, u, j * P:(j + 1) * P], xw[:, k * P:(k + 1) * P], ident_f[:])
+                xt_t[(c, g)] = xt
+
+        def copy_x(c):
+            v = three.tile([P, W], BF16, align_bytes=64, name="v")
+            v4 = v[:].rearrange("p (g n t) -> p g n t", g=PASSES, n=CH_ROWS, t=4)
+            for g in range(PASSES):
+                nc.scalar.copy(out=v4[:, g].bitcast(F32), in_=xt_t[(c, g)][:].rearrange("p u n -> p n u"))
+            v_t[c] = v
+            codes_t[c] = two.tile([P, NFUN, CW], U32, align_bytes=64, name="codes")
+            scales_t[c] = two.tile([P, NFUN, CW], U8, align_bytes=64, name="scales")
+            done[c] = 0
+
+        def silu(c):
+            sil = one.tile([P, W], BF16, align_bytes=64, name="sil")
+            nc.scalar.activation(out=sil[:], in_=v_t[c][:], func=ACT.Silu)
+            sil_t[c] = sil
+
+        def quantise(c, f, src):
+            codes = codes_t[c]
+            scales = scales_t[c]
+            nc.vector.quantize_mx(out=codes[:, f, :].bitcast(FP8X4), scales=scales[:, f, :], in_=src)
+            if done[c] == 0:
+                acc_t[c] = [pa.tile([P, OUTS], F32, tag="acc%d" % j, name="acc%d" % j) for j in range(BLK)]
+            for j in range(BLK):
+                for g in range(PASSES):
+                    lo = g * CH_ROWS + j * P
+                    wlo = (f * PASSES + g) * OUTS
+                    nc.tensor.matmul_mx(
+                        out=acc_t[c][j][:],
+                        lhsT=codes[:, f, lo:lo + P].bitcast(FP8X4),
+                        lhsT_scale=scales[:, f, lo:lo + P],
+                        rhs=wcodes[:, wlo:wlo + OUTS].bitcast(FP8X4),
+                        rhs_scale=wscales[:, wlo:wlo + OUTS],
+                        start=(done[c] == 0 and g == 0),
+                        stop=(done[c] == NFUN - 1 and g == PASSES - 1),
+                    )
+            done[c] += 1
+
+        def a_e(s):
+            c, r = divmod(s, 2)
+            e = wide.tile([P, W], F32, name="e")
+            nc.scalar.activation(out=e[:], in_=v_t[c][:], func=ACT.Abs, bias=0.5 - r, scale=1.5)
+            st[s] = {"e": e}
+
+        def a_h(s):
+            h = wide.tile([P, W], F32, name="h")
+            nc.scalar.activation(out=h[:], in_=st[s]["e"][:], func=ACT.Abs, bias=-1.0, scale=0.5)
+            st[s]["h"] = h
+
+        def a_sq_a(s):
+            sq_a = wide.tile([P, W], F32, name="sq_a")
+            nc.scalar.activation(out=sq_a[:], in_=st[s]["e"][:], func=ACT.Square, bias=-2.0 * C6, scale=C6)
+            st[s]["sq_a"] = sq_a
+
+        def a_sq_t(s):
+            sq_t = wide.tile([P, W], F32, name="sq_t")
+            nc.scalar.activation(out=sq_t[:], in_=st[s]["h"][:], func=ACT.Square, bias=-2.0, scale=2.0)
+            st[s]["sq_t"] = sq_t
+
+        def b1(s):
+            d = st[s]
+            n1u = two.tile([P, W], BF16, align_bytes=64, name="n1u")
+            nc.vector.scalar_tensor_tensor(out=n1u[:], in0=d["e"][:], scalar=-2.0, in1=d["sq_a"][:], op0=ALU.add, op1=ALU.mult)
+            d["n1u"] = n1u
+
+        def b2(s):
+            d = st[s]
+            nc.vector.scalar_tensor_tensor(out=d["sq_a"][:], in0=d["h"][:], scalar=-1.0, in1=d["sq_a"][:], op0=ALU.add, op1=ALU.mult)
+
+        def b3(s):
+            d = st[s]
+            nc.vector.scalar_tensor_tensor(out=d["h"][:], in0=d["h"][:], scalar=-1.0, in1=d["sq_t"][:], op0=ALU.add, op1=ALU.mult)
+
+        def b4(s):
+            d = st[s]
+            n2u = one.tile([P, W], BF16, align_bytes=64, name="n2u")
+            nc.vector.scalar_tensor_tensor(out=n2u[:], in0=d["sq_t"][:], scalar=-2.0 / 3.0, in1=d["h"][:], op0=ALU.add, op1=ALU.add)
+            d["n2u"] = n2u
+
+        def b5(s):
+            d = st[s]
+            nc.vector.tensor_tensor(out=d["n1u"][:], in0=d["n1u"][:], in1=d["n2u"][:], op=ALU.max)
+
+        def on_act(s):
+            c, r = divmod(s, 2)
+            return r == 0 or c % ACT_EVERY == 0
+
+        def c1(s):
+            i_p = two.tile([P, W], BF16, align_bytes=64, name="i_p")
+            nc.scalar.activation(out=i_p[:], in_=st[s]["sq_a"][:], func=ACT.Identity, bias=2.0 / 3.0, scale=6.0)
+            st[s]["i_p"] = i_p
+
+        def c2(s):
+            o_p = two.tile([P, W], BF16, align_bytes=64, name="o_p")
+            nc.scalar.activation(out=o_p[:], in_=st[s]["h"][:], func=ACT.Relu, scale=-1.0 / 3.0)
+            st[s]["o_p"] = o_p
+
+        def relu_act(s):
+            n1u = st[s]["n1u"]
+            nc.scalar.activation(out=n1u[:], in_=n1u[:], func=ACT.Relu, scale=-1.0)
+
+        def relu_dve(s):
+            n1u = st[s]["n1u"]
+            nc.vector.tensor_scalar(out=n1u[:], in0=n1u[:], scalar1=-1.0, scalar2=0.0, op0=ALU.mult, op1=ALU.max)
+
+        def d1(s):
+            d = st[s]
+            nc.vector.tensor_tensor(out=d["o_p"][:], in0=d["o_p"][:], in1=d["i_p"][:], op=ALU.min)
+
+        def d2(s):
+            c, r = divmod(s, 2)
+            mask = one.tile([P, W], BF16, align_bytes=64, name="mask")
+            nc.vector.tensor_scalar(out=mask[:], in0=v_t[c][:], scalar1=(2.0 * r - 1.0) / 3.0, scalar2=None, op0=ALU.is_lt)
+            st[s]["mask"] = mask
+
+        def d3(s):
+            d = st[s]
+            nc.vector.tensor_tensor(out=d["mask"][:], in0=d["o_p"][:], in1=d["mask"][:], op=ALU.mult)
+
+        def d6(s):
+            d = st[s]
+            nc.vector.tensor_tensor(out=d["o_p"][:], in0=d["o_p"][:], in1=d["mask"][:], op=ALU.subtract)
+
+        def q_fun(s, which):
+            c, r = divmod(s, 2)
+            quantise(c, 1 + r + {"mask": 0, "n1u": 2, "o_p": 4}[which], st[s][which][:])
+
+        def evacuate(c):
+            res = two.tile([P, BLK, OUTS], F32, name="res")
+            for j in range(BLK):
+                nc.vector.tensor_tensor(out=res[:, j, :], in0=acc_t[c][j][:], in1=bias_f[:], op=ALU.add)
+            nc.sync.dma_start(out=ov[c], in_=res[:].rearrange("p j o -> p (j o)"))
+
+        load_x(0)
         sp_sb = wprep.tile([P, FEAT], BF16)
         nc.sync.dma_start(out=sp_sb[:], in_=scale_sp)
         coef_sb = wprep.tile([P, FEAT * NB], BF16)
         nc.sync.dma_start(out=coef_sb[:], in_=coef.rearrange("o i b -> o (i b)"))
+        sb_sb = wprep.tile([P, FEAT], BF16)
+        nc.sync.dma_start(out=sb_sb[:], in_=scale_base)
         bias_b = const.tile([P, OUTS], BF16)
         nc.sync.dma_start(out=bias_b[:], in_=bias.partition_broadcast(P))
+        load_x(1)
+        load_x(2)
+        ident_f = const.tile([P, P], F32)
+        make_identity(nc, ident_f[:])
+        ident_b = const.tile([P, P], BF16)
+        make_identity(nc, ident_b[:])
+        trans_x(0)
+        copy_x(0)
+        a_e(0)
+        a_h(0)
+        a_sq_a(0)
+        a_sq_t(0)
+
         bias_f = const.tile([P, OUTS], F32)
         nc.vector.tensor_copy(out=bias_f[:], in_=bias_b[:])
-
         wg = wprep.tile([P, NFUN, PASSES, OUTS, 4], BF16, align_bytes=64)
-        wt0 = pt.tile([P, PASSES, 2, OUTS], F32, tag="xt0")
-        sb_w = sb_sb[:].bitcast(F32)
-        for g in range(PASSES):
-            for u in range(2):
-                k = 2 * g + u
-                nc.tensor.transpose(wt0[:, g, u, :], sb_w[:, k * P:(k + 1) * P], ident_f[:])
-        nc.scalar.copy(
-            out=wg[:, 0].bitcast(F32),
-            in_=wt0[:].rearrange("p g u o -> p g o u"),
-        )
         prod = wprep.tile([P, NB, 8, P], BF16)
         coef_v = coef_sb[:].rearrange("o (w p e b) -> o b w e p", w=4, p=P, e=2, b=NB)
         sp_v = sp_sb[:].rearrange("o (w p e) -> o w e p", w=4, p=P, e=2)
@@ -81,94 +237,98 @@ def tile_kanoriginal_t_kernel(tc, x, coef, scale_base, scale_sp, bias, out):
                 in1=sp_v,
                 op=ALU.mult,
             )
-        for b in range(NB):
-            wtb = pt.tile([P, PASSES, 4, OUTS], BF16, tag="xt1")
-            for g in range(PASSES):
-                for t in range(4):
-                    nc.tensor.transpose(wtb[:, g, t, :], prod[:, b, g * 4 + t, :], ident_b[:])
-            nc.scalar.copy(out=wg[:, 1 + b], in_=wtb[:].rearrange("p g t o -> p g o t"))
         wcodes = const.tile([P, NFUN * PASSES * OUTS], U32, align_bytes=64)
         wscales = const.tile([P, NFUN * PASSES * OUTS], U8, align_bytes=64)
         wg_flat = wg[:].rearrange("p f g o t -> p (f g o t)")
-        start = 0
-        for width in (4096, 2048, 1024):
-            nc.vector.quantize_mx(
-                out=wcodes[:, start // 4:(start + width) // 4].bitcast(FP8X4),
-                scales=wscales[:, start // 4:(start + width) // 4],
-                in_=wg_flat[:, start:start + width],
-            )
-            start += width
+        sb_w = sb_sb[:].bitcast(F32)
 
-        for c in range(CHUNKS):
-            xs = xin.tile([P, BLK, FEAT], BF16)
-            nc.sync.dma_start(out=xs[:].rearrange("p j i -> p (j i)"), in_=xv[c])
-            v = half.tile([P, W], BF16, align_bytes=64)
-            v4 = v[:].rearrange("p (g n t) -> p g n t", g=PASSES, n=CH_ROWS, t=4)
-            for g in range(PASSES):
-                xt = pt.tile([P, 2, CH_ROWS], F32, tag="xt%d" % g)
-                for j in range(BLK):
-                    xw = xs[:, j, :].bitcast(F32)
+        def w_copy(f):
+            if f == 0:
+                wt0 = pa.tile([P, PASSES, 2, OUTS], F32, tag="acc0", name="wt0")
+                for g in range(PASSES):
                     for u in range(2):
                         k = 2 * g + u
-                        nc.tensor.transpose(xt[:, u, j * P:(j + 1) * P], xw[:, k * P:(k + 1) * P], ident_f[:])
-                nc.scalar.copy(out=v4[:, g].bitcast(F32), in_=xt[:].rearrange("p u n -> p n u"))
+                        nc.tensor.transpose(wt0[:, g, u, :], sb_w[:, k * P:(k + 1) * P], ident_f[:])
+                nc.vector.tensor_copy(out=wg[:, 0].bitcast(F32), in_=wt0[:].rearrange("p g u o -> p g o u"))
+            else:
+                wtb = pa.tile([P, PASSES, 4, OUTS], BF16, tag="acc%d" % (f % 2), name="wtb")
+                for g in range(PASSES):
+                    for t in range(4):
+                        nc.tensor.transpose(wtb[:, g, t, :], prod[:, f - 1, g * 4 + t, :], ident_b[:])
+                nc.vector.tensor_copy(out=wg[:, f], in_=wtb[:].rearrange("p g t o -> p g o t"))
 
-            codes = packed.tile([P, NFUN, CW], U32, align_bytes=64)
-            scales = packed.tile([P, NFUN, CW], U8, align_bytes=64)
+        def w_quantise():
+            first = 0
+            for width in (4096, 2048, 1024):
+                nc.vector.quantize_mx(
+                    out=wcodes[:, first // 4:(first + width) // 4].bitcast(FP8X4),
+                    scales=wscales[:, first // 4:(first + width) // 4],
+                    in_=wg_flat[:, first:first + width],
+                )
+                first += width
 
-            def quantise(f, src):
-                nc.vector.quantize_mx(out=codes[:, f, :].bitcast(FP8X4), scales=scales[:, f, :], in_=src)
-
-            sil = half.tile([P, W], BF16, align_bytes=64)
-            nc.scalar.activation(out=sil[:], in_=v[:], func=ACT.Silu)
-            quantise(0, sil[:])
-
-            for r in range(2):
-                e = wide.tile([P, W], F32)
-                nc.scalar.activation(out=e[:], in_=v[:], func=ACT.Abs, bias=0.5 - r, scale=1.5)
-                a2 = wide.tile([P, W], F32)
-                nc.scalar.activation(out=a2[:], in_=e[:], func=ACT.Abs, bias=-2.0, scale=1.0)
-                sq_a = wide.tile([P, W], F32)
-                nc.scalar.activation(out=sq_a[:], in_=e[:], func=ACT.Square, bias=-2.0 * C6, scale=C6)
-                sq_t = wide.tile([P, W], F32)
-                nc.scalar.activation(out=sq_t[:], in_=a2[:], func=ACT.Square, bias=-2.0 * C6, scale=C6)
-                n1u = half.tile([P, W], BF16, align_bytes=64)
-                nc.vector.scalar_tensor_tensor(out=n1u[:], in0=e[:], scalar=-2.0, in1=sq_a[:], op0=ALU.add, op1=ALU.mult)
-                n1p = half.tile([P, W], BF16, align_bytes=64)
-                nc.vector.scalar_tensor_tensor(out=n1p[:], in0=a2[:], scalar=-2.0, in1=sq_t[:], op0=ALU.add, op1=ALU.mult)
-                nc.vector.scalar_tensor_tensor(out=sq_t[:], in0=e[:], scalar=-2.0, in1=sq_t[:], op0=ALU.add, op1=ALU.mult)
-                nc.vector.scalar_tensor_tensor(out=sq_a[:], in0=a2[:], scalar=-2.0, in1=sq_a[:], op0=ALU.add, op1=ALU.mult)
-                n2u = half.tile([P, W], BF16, align_bytes=64)
-                nc.scalar.activation(out=n2u[:], in_=sq_t[:], func=ACT.Identity, bias=-2.0 / 3.0, scale=-3.0)
-                n2p = half.tile([P, W], BF16, align_bytes=64)
-                nc.scalar.activation(out=n2p[:], in_=sq_a[:], func=ACT.Identity, bias=-2.0 / 3.0, scale=-3.0)
-                nc.vector.tensor_tensor(out=n1u[:], in0=n1u[:], in1=n2u[:], op=ALU.max)
-                nc.vector.tensor_scalar(out=n1u[:], in0=n1u[:], scalar1=-1.0, scalar2=0.0, op0=ALU.mult, op1=ALU.max)
-                quantise(1 + r + 2, n1u[:])
-                nc.vector.tensor_tensor(out=n1p[:], in0=n1p[:], in1=n2p[:], op=ALU.max)
-                nc.vector.tensor_scalar(out=n1p[:], in0=n1p[:], scalar1=-1.0, scalar2=0.0, op0=ALU.mult, op1=ALU.max)
-                mask = half.tile([P, W], BF16, align_bytes=64)
-                nc.vector.tensor_scalar(out=mask[:], in0=v[:], scalar1=(2.0 * r - 1.0) / 3.0, scalar2=None, op0=ALU.is_lt)
-                nc.vector.tensor_tensor(out=mask[:], in0=n1p[:], in1=mask[:], op=ALU.mult)
-                quantise(1 + r, mask[:])
-                nc.vector.tensor_tensor(out=n1p[:], in0=n1p[:], in1=mask[:], op=ALU.subtract)
-                quantise(1 + r + 4, n1p[:])
-
-            res = xin.tile([P, BLK, OUTS], F32)
-            for j in range(BLK):
-                acc = pa.tile([P, OUTS], F32, tag="acc%d" % j)
-                for f in range(NFUN):
-                    for g in range(PASSES):
-                        lo = g * CH_ROWS + j * P
-                        wlo = (f * PASSES + g) * OUTS
-                        nc.tensor.matmul_mx(
-                            out=acc[:],
-                            lhsT=codes[:, f, lo:lo + P].bitcast(FP8X4),
-                            lhsT_scale=scales[:, f, lo:lo + P],
-                            rhs=wcodes[:, wlo:wlo + OUTS].bitcast(FP8X4),
-                            rhs_scale=wscales[:, wlo:wlo + OUTS],
-                            start=(f == 0 and g == 0),
-                            stop=(f == NFUN - 1 and g == PASSES - 1),
-                        )
-                nc.vector.tensor_tensor(out=res[:, j, :], in0=acc[:], in1=bias_f[:], op=ALU.add)
-            nc.sync.dma_start(out=ov[c], in_=res[:].rearrange("p j o -> p (j o)"))
+        for t in range(STEPS + 1):
+            c, r = divmod(t, 2)
+            nxt = t + 1 < STEPS
+            cur = t < STEPS
+            prev = t >= 1
+            if r == 0 and c + 1 < CHUNKS:
+                trans_x(c + 1)
+                if c + 3 < CHUNKS:
+                    load_x(c + 3)
+            if nxt:
+                a_e(t + 1)
+            if prev and on_act(t - 1):
+                relu_act(t - 1)
+            if nxt:
+                a_h(t + 1)
+                a_sq_a(t + 1)
+                a_sq_t(t + 1)
+            if cur:
+                b1(t)
+            if prev:
+                d1(t - 1)
+            else:
+                w_copy(0)
+                w_copy(1)
+            if cur:
+                b2(t)
+            if prev:
+                d2(t - 1)
+            else:
+                w_copy(2)
+                w_copy(3)
+            if cur:
+                b3(t)
+            if prev:
+                d3(t - 1)
+                if not on_act(t - 1):
+                    relu_dve(t - 1)
+            else:
+                w_copy(4)
+                w_copy(5)
+            if cur:
+                b4(t)
+                c1(t)
+                c2(t)
+            if r == 0 and c < CHUNKS:
+                silu(c)
+                if c + 1 < CHUNKS:
+                    copy_x(c + 1)
+            if prev:
+                q_fun(t - 1, "mask")
+                d6(t - 1)
+            else:
+                w_copy(6)
+            if cur:
+                b5(t)
+            if prev:
+                q_fun(t - 1, "n1u")
+                q_fun(t - 1, "o_p")
+            else:
+                w_quantise()
+            if r == 1:
+                quantise(c, 0, sil_t[c][:])
+                if c >= 1:
+                    evacuate(c - 1)
+        evacuate(CHUNKS - 1)

@@ -27,7 +27,7 @@ W = PASSES * CH_ROWS * 4
 CW = W // 4
 FLOPS = 2 * ROWS * FEAT * OUTS * NFUN
 C6 = 1.0 / math.sqrt(6.0)
-ACT_EVERY = 4
+ACT_EVERY = 2
 
 
 def tile_kanoriginal_t_kernel(tc, x, coef, scale_base, scale_sp, bias, out):
@@ -54,6 +54,7 @@ def tile_kanoriginal_t_kernel(tc, x, coef, scale_base, scale_sp, bias, out):
         scales_t = {}
         acc_t = {}
         done = {}
+        rt_t = {}
 
         def load_x(c):
             xs = three.tile([P, BLK, FEAT], BF16, name="xs")
@@ -91,20 +92,18 @@ def tile_kanoriginal_t_kernel(tc, x, coef, scale_base, scale_sp, bias, out):
             scales = scales_t[c]
             nc.vector.quantize_mx(out=codes[:, f, :].bitcast(FP8X4), scales=scales[:, f, :], in_=src)
             if done[c] == 0:
-                acc_t[c] = [pa.tile([P, OUTS], F32, tag="acc%d" % j, name="acc%d" % j) for j in range(BLK)]
-            for j in range(BLK):
-                for g in range(PASSES):
-                    lo = g * CH_ROWS + j * P
-                    wlo = (f * PASSES + g) * OUTS
-                    nc.tensor.matmul_mx(
-                        out=acc_t[c][j][:],
-                        lhsT=codes[:, f, lo:lo + P].bitcast(FP8X4),
-                        lhsT_scale=scales[:, f, lo:lo + P],
-                        rhs=wcodes[:, wlo:wlo + OUTS].bitcast(FP8X4),
-                        rhs_scale=wscales[:, wlo:wlo + OUTS],
-                        start=(done[c] == 0 and g == 0),
-                        stop=(done[c] == NFUN - 1 and g == PASSES - 1),
-                    )
+                acc_t[c] = pa.tile([P, CH_ROWS], F32, tag="acc", name="acc")
+            for g in range(PASSES):
+                wlo = (f * PASSES + g) * OUTS
+                nc.tensor.matmul_mx(
+                    out=acc_t[c][:],
+                    lhsT=wcodes[:, wlo:wlo + OUTS].bitcast(FP8X4),
+                    lhsT_scale=wscales[:, wlo:wlo + OUTS],
+                    rhs=codes[:, f, g * CH_ROWS:(g + 1) * CH_ROWS].bitcast(FP8X4),
+                    rhs_scale=scales[:, f, g * CH_ROWS:(g + 1) * CH_ROWS],
+                    start=(done[c] == 0 and g == 0),
+                    stop=(done[c] == NFUN - 1 and g == PASSES - 1),
+                )
             done[c] += 1
 
         def a_e(s):
@@ -196,10 +195,17 @@ def tile_kanoriginal_t_kernel(tc, x, coef, scale_base, scale_sp, bias, out):
             c, r = divmod(s, 2)
             quantise(c, 1 + r + {"mask": 0, "n1u": 2, "o_p": 4}[which], st[s][which][:])
 
-        def evacuate(c):
-            res = two.tile([P, BLK, OUTS], F32, name="res")
+        def evac_bias(c):
+            o_t = one.tile([P, CH_ROWS], F32, name="o_t")
+            nc.scalar.activation(out=o_t[:], in_=acc_t[c][:], func=ACT.Identity, bias=bias_f[:, 0:1], scale=1.0)
+            rt = pa.tile([P, BLK, OUTS], F32, tag="rt", name="rt")
             for j in range(BLK):
-                nc.vector.tensor_tensor(out=res[:, j, :], in0=acc_t[c][j][:], in1=bias_f[:], op=ALU.add)
+                nc.tensor.transpose(rt[:, j, :], o_t[:, j * P:(j + 1) * P], ident_f[:])
+            rt_t[c] = rt
+
+        def evac_store(c):
+            res = two.tile([P, BLK, OUTS], F32, name="res")
+            nc.scalar.copy(out=res[:], in_=rt_t[c][:])
             nc.sync.dma_start(out=ov[c], in_=res[:].rearrange("p j o -> p (j o)"))
 
         load_x(0)
@@ -209,8 +215,8 @@ def tile_kanoriginal_t_kernel(tc, x, coef, scale_base, scale_sp, bias, out):
         nc.sync.dma_start(out=coef_sb[:], in_=coef.rearrange("o i b -> o (i b)"))
         sb_sb = wprep.tile([P, FEAT], BF16)
         nc.sync.dma_start(out=sb_sb[:], in_=scale_base)
-        bias_b = const.tile([P, OUTS], BF16)
-        nc.sync.dma_start(out=bias_b[:], in_=bias.partition_broadcast(P))
+        bias_b = const.tile([P, 1], BF16)
+        nc.sync.dma_start(out=bias_b[:], in_=bias.rearrange("(o a) -> o a", a=1))
         load_x(1)
         load_x(2)
         ident_f = const.tile([P, P], F32)
@@ -224,7 +230,7 @@ def tile_kanoriginal_t_kernel(tc, x, coef, scale_base, scale_sp, bias, out):
         a_sq_a(0)
         a_sq_t(0)
 
-        bias_f = const.tile([P, OUTS], F32)
+        bias_f = const.tile([P, 1], F32)
         nc.vector.tensor_copy(out=bias_f[:], in_=bias_b[:])
         wg = wprep.tile([P, NFUN, PASSES, OUTS, 4], BF16, align_bytes=64)
         prod = wprep.tile([P, NB, 8, P], BF16)
@@ -244,14 +250,14 @@ def tile_kanoriginal_t_kernel(tc, x, coef, scale_base, scale_sp, bias, out):
 
         def w_copy(f):
             if f == 0:
-                wt0 = pa.tile([P, PASSES, 2, OUTS], F32, tag="acc0", name="wt0")
+                wt0 = pa.tile([P, PASSES, 2, OUTS], F32, tag="acc", name="wt0")
                 for g in range(PASSES):
                     for u in range(2):
                         k = 2 * g + u
                         nc.tensor.transpose(wt0[:, g, u, :], sb_w[:, k * P:(k + 1) * P], ident_f[:])
                 nc.vector.tensor_copy(out=wg[:, 0].bitcast(F32), in_=wt0[:].rearrange("p g u o -> p g o u"))
             else:
-                wtb = pa.tile([P, PASSES, 4, OUTS], BF16, tag="acc%d" % (f % 2), name="wtb")
+                wtb = pa.tile([P, PASSES, 4, OUTS], BF16, tag=("acc", "rt")[f % 2], name="wtb")
                 for g in range(PASSES):
                     for t in range(4):
                         nc.tensor.transpose(wtb[:, g, t, :], prod[:, f - 1, g * 4 + t, :], ident_b[:])
@@ -280,6 +286,8 @@ def tile_kanoriginal_t_kernel(tc, x, coef, scale_base, scale_sp, bias, out):
                 a_e(t + 1)
             if prev and on_act(t - 1):
                 relu_act(t - 1)
+            if r == 0 and c >= 2:
+                evac_bias(c - 2)
             if nxt:
                 a_h(t + 1)
                 a_sq_a(t + 1)
@@ -315,6 +323,8 @@ def tile_kanoriginal_t_kernel(tc, x, coef, scale_base, scale_sp, bias, out):
                 silu(c)
                 if c + 1 < CHUNKS:
                     copy_x(c + 1)
+            if r == 0 and c >= 2:
+                evac_store(c - 2)
             if prev:
                 q_fun(t - 1, "mask")
                 d6(t - 1)
@@ -329,6 +339,5 @@ def tile_kanoriginal_t_kernel(tc, x, coef, scale_base, scale_sp, bias, out):
                 w_quantise()
             if r == 1:
                 quantise(c, 0, sil_t[c][:])
-                if c >= 1:
-                    evacuate(c - 1)
-        evacuate(CHUNKS - 1)
+        evac_bias(CHUNKS - 1)
+        evac_store(CHUNKS - 1)

@@ -25,9 +25,12 @@ CHUNKS = ROWS // CH_ROWS
 STEPS = 2 * CHUNKS
 W = PASSES * CH_ROWS * 4
 CW = W // 4
+HW = W // PASSES
 FLOPS = 2 * ROWS * FEAT * OUTS * NFUN
 C6 = 1.0 / math.sqrt(6.0)
-ACT_EVERY = 2
+C3 = 1.0 / math.sqrt(3.0)
+C2 = 1.0 / math.sqrt(2.0)
+SILU_KNOT = (-1.0 / 3.0 / (1.0 + math.exp(1.0 / 3.0)), 1.0 / 3.0 / (1.0 + math.exp(-1.0 / 3.0)))
 
 
 def tile_kanoriginal_t_kernel(tc, x, coef, scale_base, scale_sp, bias, out):
@@ -47,14 +50,12 @@ def tile_kanoriginal_t_kernel(tc, x, coef, scale_base, scale_sp, bias, out):
 
         xs_t = {}
         xt_t = {}
-        v_t = {}
         sil_t = {}
         st = {}
         codes_t = {}
         scales_t = {}
         acc_t = {}
         done = {}
-        rt_t = {}
 
         def load_x(c):
             xs = three.tile([P, BLK, FEAT], BF16, name="xs")
@@ -72,140 +73,126 @@ def tile_kanoriginal_t_kernel(tc, x, coef, scale_base, scale_sp, bias, out):
                         nc.tensor.transpose(xt[:, u, j * P:(j + 1) * P], xw[:, k * P:(k + 1) * P], ident_f[:])
                 xt_t[(c, g)] = xt
 
-        def copy_x(c):
-            v = three.tile([P, W], BF16, align_bytes=64, name="v")
-            v4 = v[:].rearrange("p (g n t) -> p g n t", g=PASSES, n=CH_ROWS, t=4)
-            for g in range(PASSES):
-                nc.scalar.copy(out=v4[:, g].bitcast(F32), in_=xt_t[(c, g)][:].rearrange("p u n -> p n u"))
-            v_t[c] = v
-            codes_t[c] = two.tile([P, NFUN, CW], U32, align_bytes=64, name="codes")
-            scales_t[c] = two.tile([P, NFUN, CW], U8, align_bytes=64, name="scales")
-            done[c] = 0
+        def grouped(c, g):
+            return xt_t[(c, g)][:].bitcast(BF16).rearrange("p u (n e) -> p n u e", e=2)
+
+        def split(ap, g):
+            return ap[:, g * HW:(g + 1) * HW].rearrange("p (n u e) -> p n u e", u=2, e=2)
 
         def silu(c):
-            sil = one.tile([P, W], BF16, align_bytes=64, name="sil")
-            nc.scalar.activation(out=sil[:], in_=v_t[c][:], func=ACT.Silu)
+            sil = three.tile([P, W], BF16, align_bytes=64, name="sil")
+            for g in range(PASSES):
+                nc.scalar.activation(out=split(sil, g), in_=grouped(c, g), func=ACT.Silu)
             sil_t[c] = sil
+            done[c] = 0
 
         def quantise(c, f, src):
+            if done[c] == 0:
+                codes_t[c] = two.tile([P, NFUN, CW], U32, align_bytes=64, name="codes")
+                scales_t[c] = two.tile([P, NFUN, CW], U8, align_bytes=64, name="scales")
+                acc_t[c] = [pa.tile([P, OUTS], F32, tag="acc%d" % j, name="acc%d" % j) for j in range(BLK)]
             codes = codes_t[c]
             scales = scales_t[c]
             nc.vector.quantize_mx(out=codes[:, f, :].bitcast(FP8X4), scales=scales[:, f, :], in_=src)
-            if done[c] == 0:
-                acc_t[c] = pa.tile([P, CH_ROWS], F32, tag="acc", name="acc")
-            for g in range(PASSES):
-                wlo = (f * PASSES + g) * OUTS
-                nc.tensor.matmul_mx(
-                    out=acc_t[c][:],
-                    lhsT=wcodes[:, wlo:wlo + OUTS].bitcast(FP8X4),
-                    lhsT_scale=wscales[:, wlo:wlo + OUTS],
-                    rhs=codes[:, f, g * CH_ROWS:(g + 1) * CH_ROWS].bitcast(FP8X4),
-                    rhs_scale=scales[:, f, g * CH_ROWS:(g + 1) * CH_ROWS],
-                    start=(done[c] == 0 and g == 0),
-                    stop=(done[c] == NFUN - 1 and g == PASSES - 1),
-                )
+            for j in range(BLK):
+                for g in range(PASSES):
+                    lo = g * CH_ROWS + j * P
+                    wlo = (f * PASSES + g) * OUTS
+                    nc.tensor.matmul_mx(
+                        out=acc_t[c][j][:],
+                        lhsT=codes[:, f, lo:lo + P].bitcast(FP8X4),
+                        lhsT_scale=scales[:, f, lo:lo + P],
+                        rhs=wcodes[:, wlo:wlo + OUTS].bitcast(FP8X4),
+                        rhs_scale=wscales[:, wlo:wlo + OUTS],
+                        start=(done[c] == 0 and g == 0),
+                        stop=(done[c] == NFUN - 1 and g == PASSES - 1),
+                    )
             done[c] += 1
+
+        def raw(s, pool, name, src, func, scale, shift):
+            t = pool.tile([P, W], F32, name=name)
+            nc.scalar.activation(out=t[:], in_=src[:], func=func, bias=shift, scale=scale)
+            st[s][name] = t
 
         def a_e(s):
             c, r = divmod(s, 2)
             e = wide.tile([P, W], F32, name="e")
-            nc.scalar.activation(out=e[:], in_=v_t[c][:], func=ACT.Abs, bias=0.5 - r, scale=1.5)
+            for g in range(PASSES):
+                nc.scalar.activation(out=split(e, g), in_=grouped(c, g), func=ACT.Abs, bias=0.5 - r, scale=1.5)
             st[s] = {"e": e}
 
-        def a_h(s):
-            h = wide.tile([P, W], F32, name="h")
-            nc.scalar.activation(out=h[:], in_=st[s]["e"][:], func=ACT.Abs, bias=-1.0, scale=0.5)
-            st[s]["h"] = h
+        def a_rest(s):
+            d = st[s]
+            raw(s, wide, "h", d["e"], ACT.Abs, 0.5, -1.0)
+            raw(s, wide, "sq_u", d["e"], ACT.Square, C6, -2.0 * C6)
+            if s % 2 == 0:
+                raw(s, one, "a3", d["h"], ACT.Abs, 2.0, -1.0)
+            else:
+                raw(s, one, "sq_x", st[s - 1]["a3"], ACT.Square, C2, -0.5 * C2)
+            raw(s, wide, "sq_p", d["h"], ACT.Square, 2.0 * C3, -2.0 * C3)
+            if s % 2 == 0:
+                raw(s, wide, "sq_i", d["a3"], ACT.Square, C2, -C2)
 
-        def a_sq_a(s):
-            sq_a = wide.tile([P, W], F32, name="sq_a")
-            nc.scalar.activation(out=sq_a[:], in_=st[s]["e"][:], func=ACT.Square, bias=-2.0 * C6, scale=C6)
-            st[s]["sq_a"] = sq_a
-
-        def a_sq_t(s):
-            sq_t = wide.tile([P, W], F32, name="sq_t")
-            nc.scalar.activation(out=sq_t[:], in_=st[s]["h"][:], func=ACT.Square, bias=-2.0, scale=2.0)
-            st[s]["sq_t"] = sq_t
+        def product(s, name, lin, shift, square):
+            d = st[s]
+            if name is None:
+                dst = d[square]
+            else:
+                dst = two.tile([P, W], BF16, align_bytes=64, name=name)
+                d[name] = dst
+            nc.vector.scalar_tensor_tensor(out=dst[:], in0=d[lin][:], scalar=shift, in1=d[square][:], op0=ALU.add, op1=ALU.mult)
 
         def b1(s):
-            d = st[s]
-            n1u = two.tile([P, W], BF16, align_bytes=64, name="n1u")
-            nc.vector.scalar_tensor_tensor(out=n1u[:], in0=d["e"][:], scalar=-2.0, in1=d["sq_a"][:], op0=ALU.add, op1=ALU.mult)
-            d["n1u"] = n1u
+            product(s, "n1u", "e", -2.0, "sq_u")
 
         def b2(s):
-            d = st[s]
-            nc.vector.scalar_tensor_tensor(out=d["sq_a"][:], in0=d["h"][:], scalar=-1.0, in1=d["sq_a"][:], op0=ALU.add, op1=ALU.mult)
+            product(s, "n1p", "h", -1.0, "sq_p")
 
         def b3(s):
+            if s % 2 == 0:
+                product(s, None, "a3", 1.0, "sq_i")
+            else:
+                ni = two.tile([P, W], BF16, align_bytes=64, name="ni")
+                nc.vector.scalar_tensor_tensor(
+                    out=ni[:], in0=st[s]["sq_x"][:], scalar=-7.0 / 24.0, in1=st[s - 1]["sq_i"][:], op0=ALU.add, op1=ALU.subtract
+                )
+                st[s]["ni"] = ni
+
+        def round_act(s):
+            ni = two.tile([P, W], BF16, align_bytes=64, name="ni")
+            nc.scalar.activation(out=ni[:], in_=st[s]["sq_i"][:], func=ACT.Identity, bias=-2.0 / 3.0, scale=1.0)
+            st[s]["ni"] = ni
+
+        def merge(s, name):
             d = st[s]
-            nc.vector.scalar_tensor_tensor(out=d["h"][:], in0=d["h"][:], scalar=-1.0, in1=d["sq_t"][:], op0=ALU.add, op1=ALU.mult)
+            nc.vector.tensor_tensor(out=d[name][:], in0=d[name][:], in1=d["ni"][:], op=ALU.max)
 
-        def b4(s):
-            d = st[s]
-            n2u = one.tile([P, W], BF16, align_bytes=64, name="n2u")
-            nc.vector.scalar_tensor_tensor(out=n2u[:], in0=d["sq_t"][:], scalar=-2.0 / 3.0, in1=d["h"][:], op0=ALU.add, op1=ALU.add)
-            d["n2u"] = n2u
+        def relu_neg(s, name):
+            t = st[s][name]
+            nc.vector.tensor_scalar(out=t[:], in0=t[:], scalar1=-1.0, scalar2=0.0, op0=ALU.mult, op1=ALU.max)
 
-        def b5(s):
-            d = st[s]
-            nc.vector.tensor_tensor(out=d["n1u"][:], in0=d["n1u"][:], in1=d["n2u"][:], op=ALU.max)
-
-        def on_act(s):
-            c, r = divmod(s, 2)
-            return r == 0 or c % ACT_EVERY == 0
-
-        def c1(s):
-            i_p = two.tile([P, W], BF16, align_bytes=64, name="i_p")
-            nc.scalar.activation(out=i_p[:], in_=st[s]["sq_a"][:], func=ACT.Identity, bias=2.0 / 3.0, scale=6.0)
-            st[s]["i_p"] = i_p
-
-        def c2(s):
-            o_p = two.tile([P, W], BF16, align_bytes=64, name="o_p")
-            nc.scalar.activation(out=o_p[:], in_=st[s]["h"][:], func=ACT.Relu, scale=-1.0 / 3.0)
-            st[s]["o_p"] = o_p
-
-        def relu_act(s):
-            n1u = st[s]["n1u"]
-            nc.scalar.activation(out=n1u[:], in_=n1u[:], func=ACT.Relu, scale=-1.0)
-
-        def relu_dve(s):
-            n1u = st[s]["n1u"]
-            nc.vector.tensor_scalar(out=n1u[:], in0=n1u[:], scalar1=-1.0, scalar2=0.0, op0=ALU.mult, op1=ALU.max)
-
-        def d1(s):
-            d = st[s]
-            nc.vector.tensor_tensor(out=d["o_p"][:], in0=d["o_p"][:], in1=d["i_p"][:], op=ALU.min)
-
-        def d2(s):
+        def mask_lo(s):
             c, r = divmod(s, 2)
             mask = one.tile([P, W], BF16, align_bytes=64, name="mask")
-            nc.vector.tensor_scalar(out=mask[:], in0=v_t[c][:], scalar1=(2.0 * r - 1.0) / 3.0, scalar2=None, op0=ALU.is_lt)
+            nc.vector.tensor_scalar(out=mask[:], in0=sil_t[c][:], scalar1=SILU_KNOT[r], scalar2=None, op0=ALU.is_lt)
             st[s]["mask"] = mask
 
-        def d3(s):
+        def take_lo(s):
             d = st[s]
-            nc.vector.tensor_tensor(out=d["mask"][:], in0=d["o_p"][:], in1=d["mask"][:], op=ALU.mult)
+            nc.vector.tensor_tensor(out=d["mask"][:], in0=d["n1p"][:], in1=d["mask"][:], op=ALU.mult)
 
-        def d6(s):
+        def take_hi(s):
             d = st[s]
-            nc.vector.tensor_tensor(out=d["o_p"][:], in0=d["o_p"][:], in1=d["mask"][:], op=ALU.subtract)
+            nc.vector.tensor_tensor(out=d["n1p"][:], in0=d["n1p"][:], in1=d["mask"][:], op=ALU.subtract)
 
         def q_fun(s, which):
             c, r = divmod(s, 2)
-            quantise(c, 1 + r + {"mask": 0, "n1u": 2, "o_p": 4}[which], st[s][which][:])
+            quantise(c, 1 + r + {"mask": 0, "n1u": 2, "n1p": 4}[which], st[s][which][:])
 
-        def evac_bias(c):
-            o_t = one.tile([P, CH_ROWS], F32, name="o_t")
-            nc.scalar.activation(out=o_t[:], in_=acc_t[c][:], func=ACT.Identity, bias=bias_f[:, 0:1], scale=1.0)
-            rt = pa.tile([P, BLK, OUTS], F32, tag="rt", name="rt")
-            for j in range(BLK):
-                nc.tensor.transpose(rt[:, j, :], o_t[:, j * P:(j + 1) * P], ident_f[:])
-            rt_t[c] = rt
-
-        def evac_store(c):
+        def evacuate(c):
             res = two.tile([P, BLK, OUTS], F32, name="res")
-            nc.scalar.copy(out=res[:], in_=rt_t[c][:])
+            for j in range(BLK):
+                nc.vector.tensor_tensor(out=res[:, j, :], in0=acc_t[c][j][:], in1=bias_f[:], op=ALU.add)
             nc.sync.dma_start(out=ov[c], in_=res[:].rearrange("p j o -> p (j o)"))
 
         load_x(0)
@@ -215,8 +202,8 @@ def tile_kanoriginal_t_kernel(tc, x, coef, scale_base, scale_sp, bias, out):
         nc.sync.dma_start(out=coef_sb[:], in_=coef.rearrange("o i b -> o (i b)"))
         sb_sb = wprep.tile([P, FEAT], BF16)
         nc.sync.dma_start(out=sb_sb[:], in_=scale_base)
-        bias_b = const.tile([P, 1], BF16)
-        nc.sync.dma_start(out=bias_b[:], in_=bias.rearrange("(o a) -> o a", a=1))
+        bias_b = const.tile([P, OUTS], BF16)
+        nc.sync.dma_start(out=bias_b[:], in_=bias.partition_broadcast(P))
         load_x(1)
         load_x(2)
         ident_f = const.tile([P, P], F32)
@@ -224,44 +211,35 @@ def tile_kanoriginal_t_kernel(tc, x, coef, scale_base, scale_sp, bias, out):
         ident_b = const.tile([P, P], BF16)
         make_identity(nc, ident_b[:])
         trans_x(0)
-        copy_x(0)
         a_e(0)
-        a_h(0)
-        a_sq_a(0)
-        a_sq_t(0)
 
-        bias_f = const.tile([P, 1], F32)
+        bias_f = const.tile([P, OUTS], F32)
         nc.vector.tensor_copy(out=bias_f[:], in_=bias_b[:])
         wg = wprep.tile([P, NFUN, PASSES, OUTS, 4], BF16, align_bytes=64)
-        prod = wprep.tile([P, NB, 8, P], BF16)
         coef_v = coef_sb[:].rearrange("o (w p e b) -> o b w e p", w=4, p=P, e=2, b=NB)
-        sp_v = sp_sb[:].rearrange("o (w p e) -> o w e p", w=4, p=P, e=2)
-        for b in range(NB):
-            nc.vector.tensor_tensor(
-                out=prod[:, b].rearrange("o (w e) p -> o w e p", w=4, e=2),
-                in0=coef_v[:, b],
-                in1=sp_v,
-                op=ALU.mult,
-            )
+        spg = wprep.tile([P, PASSES, OUTS, 4], BF16)
         wcodes = const.tile([P, NFUN * PASSES * OUTS], U32, align_bytes=64)
         wscales = const.tile([P, NFUN * PASSES * OUTS], U8, align_bytes=64)
         wg_flat = wg[:].rearrange("p f g o t -> p (f g o t)")
-        sb_w = sb_sb[:].bitcast(F32)
+
+        def w_words(src, dst):
+            wt0 = pa.tile([P, PASSES, 2, OUTS], F32, tag="acc0", name="wt0")
+            for g in range(PASSES):
+                for u in range(2):
+                    k = 2 * g + u
+                    nc.tensor.transpose(wt0[:, g, u, :], src[:, k * P:(k + 1) * P], ident_f[:])
+            nc.vector.tensor_copy(out=dst.bitcast(F32), in_=wt0[:].rearrange("p g u o -> p g o u"))
 
         def w_copy(f):
             if f == 0:
-                wt0 = pa.tile([P, PASSES, 2, OUTS], F32, tag="acc", name="wt0")
-                for g in range(PASSES):
-                    for u in range(2):
-                        k = 2 * g + u
-                        nc.tensor.transpose(wt0[:, g, u, :], sb_w[:, k * P:(k + 1) * P], ident_f[:])
-                nc.vector.tensor_copy(out=wg[:, 0].bitcast(F32), in_=wt0[:].rearrange("p g u o -> p g o u"))
+                w_words(sp_sb[:].bitcast(F32), spg[:])
+                w_words(sb_sb[:].bitcast(F32), wg[:, 0])
             else:
-                wtb = pa.tile([P, PASSES, 4, OUTS], BF16, tag=("acc", "rt")[f % 2], name="wtb")
+                wtb = pa.tile([P, PASSES, 4, OUTS], BF16, tag="acc1", name="wtb")
                 for g in range(PASSES):
                     for t in range(4):
-                        nc.tensor.transpose(wtb[:, g, t, :], prod[:, f - 1, g * 4 + t, :], ident_b[:])
-                nc.vector.tensor_copy(out=wg[:, f], in_=wtb[:].rearrange("p g t o -> p g o t"))
+                        nc.tensor.transpose(wtb[:, g, t, :], coef_v[:, f - 1, 2 * g + t // 2, t % 2, :], ident_b[:])
+                nc.vector.tensor_tensor(out=wg[:, f], in0=wtb[:].rearrange("p g t o -> p g o t"), in1=spg[:], op=ALU.mult)
 
         def w_quantise():
             first = 0
@@ -273,71 +251,54 @@ def tile_kanoriginal_t_kernel(tc, x, coef, scale_base, scale_sp, bias, out):
                 )
                 first += width
 
-        for t in range(STEPS + 1):
+        for f in range(3):
+            w_copy(f)
+
+        for t in range(-1, STEPS + 1):
             c, r = divmod(t, 2)
-            nxt = t + 1 < STEPS
-            cur = t < STEPS
+            cur = 0 <= t < STEPS
             prev = t >= 1
             if r == 0 and c + 1 < CHUNKS:
                 trans_x(c + 1)
                 if c + 3 < CHUNKS:
                     load_x(c + 3)
-            if nxt:
-                a_e(t + 1)
-            if prev and on_act(t - 1):
-                relu_act(t - 1)
-            if r == 0 and c >= 2:
-                evac_bias(c - 2)
-            if nxt:
-                a_h(t + 1)
-                a_sq_a(t + 1)
-                a_sq_t(t + 1)
+            if t + 1 < STEPS:
+                a_rest(t + 1)
+            if t + 2 < STEPS:
+                a_e(t + 2)
             if cur:
                 b1(t)
             if prev:
-                d1(t - 1)
-            else:
-                w_copy(0)
-                w_copy(1)
+                mask_lo(t - 1)
+            if t == 0:
+                w_copy(3)
+                w_copy(4)
             if cur:
                 b2(t)
             if prev:
-                d2(t - 1)
-            else:
-                w_copy(2)
-                w_copy(3)
-            if cur:
-                b3(t)
-            if prev:
-                d3(t - 1)
-                if not on_act(t - 1):
-                    relu_dve(t - 1)
-            else:
-                w_copy(4)
+                merge(t - 1, "n1p")
+            if t == 0:
                 w_copy(5)
-            if cur:
-                b4(t)
-                c1(t)
-                c2(t)
-            if r == 0 and c < CHUNKS:
-                silu(c)
-                if c + 1 < CHUNKS:
-                    copy_x(c + 1)
-            if r == 0 and c >= 2:
-                evac_store(c - 2)
-            if prev:
-                q_fun(t - 1, "mask")
-                d6(t - 1)
-            else:
                 w_copy(6)
             if cur:
-                b5(t)
+                b3(t)
+            if cur and r == 0:
+                round_act(t)
+            if r == 1 and c + 1 < CHUNKS:
+                silu(c + 1)
             if prev:
+                merge(t - 1, "n1u")
+                relu_neg(t - 1, "n1p")
+                relu_neg(t - 1, "n1u")
+                take_lo(t - 1)
                 q_fun(t - 1, "n1u")
-                q_fun(t - 1, "o_p")
-            else:
+                take_hi(t - 1)
+                q_fun(t - 1, "mask")
+                q_fun(t - 1, "n1p")
+            if t == 0:
                 w_quantise()
-            if r == 1:
+            if prev and r == 1:
                 quantise(c, 0, sil_t[c][:])
-        evac_bias(CHUNKS - 1)
-        evac_store(CHUNKS - 1)
+                if c >= 1:
+                    evacuate(c - 1)
+        evacuate(CHUNKS - 1)

@@ -56,6 +56,7 @@ def tile_kanoriginal_t_kernel(tc, x, coef, scale_base, scale_sp, bias, out):
         scales_t = {}
         acc_t = {}
         done = {}
+        rt_t = {}
 
         def load_x(c):
             xs = three.tile([P, BLK, FEAT], BF16, name="xs")
@@ -90,23 +91,21 @@ def tile_kanoriginal_t_kernel(tc, x, coef, scale_base, scale_sp, bias, out):
             if done[c] == 0:
                 codes_t[c] = two.tile([P, NFUN, CW], U32, align_bytes=64, name="codes")
                 scales_t[c] = two.tile([P, NFUN, CW], U8, align_bytes=64, name="scales")
-                acc_t[c] = [pa.tile([P, OUTS], F32, tag="acc%d" % j, name="acc%d" % j) for j in range(BLK)]
+                acc_t[c] = pa.tile([P, CH_ROWS], F32, tag="acc", name="acc")
             codes = codes_t[c]
             scales = scales_t[c]
             nc.vector.quantize_mx(out=codes[:, f, :].bitcast(FP8X4), scales=scales[:, f, :], in_=src)
-            for j in range(BLK):
-                for g in range(PASSES):
-                    lo = g * CH_ROWS + j * P
-                    wlo = (f * PASSES + g) * OUTS
-                    nc.tensor.matmul_mx(
-                        out=acc_t[c][j][:],
-                        lhsT=codes[:, f, lo:lo + P].bitcast(FP8X4),
-                        lhsT_scale=scales[:, f, lo:lo + P],
-                        rhs=wcodes[:, wlo:wlo + OUTS].bitcast(FP8X4),
-                        rhs_scale=wscales[:, wlo:wlo + OUTS],
-                        start=(done[c] == 0 and g == 0),
-                        stop=(done[c] == NFUN - 1 and g == PASSES - 1),
-                    )
+            for g in range(PASSES):
+                wlo = (f * PASSES + g) * OUTS
+                nc.tensor.matmul_mx(
+                    out=acc_t[c][:],
+                    lhsT=wcodes[:, wlo:wlo + OUTS].bitcast(FP8X4),
+                    lhsT_scale=wscales[:, wlo:wlo + OUTS],
+                    rhs=codes[:, f, g * CH_ROWS:(g + 1) * CH_ROWS].bitcast(FP8X4),
+                    rhs_scale=scales[:, f, g * CH_ROWS:(g + 1) * CH_ROWS],
+                    start=(done[c] == 0 and g == 0),
+                    stop=(done[c] == NFUN - 1 and g == PASSES - 1),
+                )
             done[c] += 1
 
         def raw(s, pool, name, src, func, scale, shift):
@@ -127,11 +126,11 @@ def tile_kanoriginal_t_kernel(tc, x, coef, scale_base, scale_sp, bias, out):
             raw(s, wide, "sq_u", d["e"], ACT.Square, C6, -2.0 * C6)
             if s % 2 == 0:
                 raw(s, one, "a3", d["h"], ACT.Abs, 2.0, -1.0)
-            else:
-                raw(s, one, "sq_x", st[s - 1]["a3"], ACT.Square, C2, -0.5 * C2)
             raw(s, wide, "sq_p", d["h"], ACT.Square, 2.0 * C3, -2.0 * C3)
             if s % 2 == 0:
                 raw(s, wide, "sq_i", d["a3"], ACT.Square, C2, -C2)
+            else:
+                raw(s, one, "sq_x", st[s - 1]["a3"], ACT.Square, C2, -0.5 * C2)
 
         def product(s, name, lin, shift, square):
             d = st[s]
@@ -189,21 +188,28 @@ def tile_kanoriginal_t_kernel(tc, x, coef, scale_base, scale_sp, bias, out):
             c, r = divmod(s, 2)
             quantise(c, 1 + r + {"mask": 0, "n1u": 2, "n1p": 4}[which], st[s][which][:])
 
-        def evacuate(c):
-            res = two.tile([P, BLK, OUTS], F32, name="res")
+        def evac_bias(c):
+            o_t = one.tile([P, CH_ROWS], F32, name="o_t")
+            nc.scalar.activation(out=o_t[:], in_=acc_t[c][:], func=ACT.Identity, bias=bias_f[:, 0:1], scale=1.0)
+            rt = pa.tile([P, BLK, OUTS], F32, tag="rt", name="rt")
             for j in range(BLK):
-                nc.vector.tensor_tensor(out=res[:, j, :], in0=acc_t[c][j][:], in1=bias_f[:], op=ALU.add)
+                nc.tensor.transpose(rt[:, j, :], o_t[:, j * P:(j + 1) * P], ident_f[:])
+            rt_t[c] = rt
+
+        def evac_store(c):
+            res = two.tile([P, BLK, OUTS], F32, name="res")
+            nc.scalar.copy(out=res[:], in_=rt_t[c][:])
             nc.sync.dma_start(out=ov[c], in_=res[:].rearrange("p j o -> p (j o)"))
 
         load_x(0)
         sp_sb = wprep.tile([P, FEAT], BF16)
         nc.sync.dma_start(out=sp_sb[:], in_=scale_sp)
-        coef_sb = wprep.tile([P, FEAT * NB], BF16)
-        nc.sync.dma_start(out=coef_sb[:], in_=coef.rearrange("o i b -> o (i b)"))
         sb_sb = wprep.tile([P, FEAT], BF16)
         nc.sync.dma_start(out=sb_sb[:], in_=scale_base)
-        bias_b = const.tile([P, OUTS], BF16)
-        nc.sync.dma_start(out=bias_b[:], in_=bias.partition_broadcast(P))
+        coef_sb = wprep.tile([P, FEAT * NB], BF16)
+        nc.sync.dma_start(out=coef_sb[:], in_=coef.rearrange("o i b -> o (i b)"))
+        bias_b = const.tile([P, 1], BF16)
+        nc.sync.dma_start(out=bias_b[:], in_=bias.rearrange("(o a) -> o a", a=1))
         load_x(1)
         load_x(2)
         ident_f = const.tile([P, P], F32)
@@ -213,8 +219,7 @@ def tile_kanoriginal_t_kernel(tc, x, coef, scale_base, scale_sp, bias, out):
         trans_x(0)
         a_e(0)
 
-        bias_f = const.tile([P, OUTS], F32)
-        nc.vector.tensor_copy(out=bias_f[:], in_=bias_b[:])
+        bias_f = const.tile([P, 1], F32)
         wg = wprep.tile([P, NFUN, PASSES, OUTS, 4], BF16, align_bytes=64)
         coef_v = coef_sb[:].rearrange("o (w p e b) -> o b w e p", w=4, p=P, e=2, b=NB)
         spg = wprep.tile([P, PASSES, OUTS, 4], BF16)
@@ -223,7 +228,7 @@ def tile_kanoriginal_t_kernel(tc, x, coef, scale_base, scale_sp, bias, out):
         wg_flat = wg[:].rearrange("p f g o t -> p (f g o t)")
 
         def w_words(src, dst):
-            wt0 = pa.tile([P, PASSES, 2, OUTS], F32, tag="acc0", name="wt0")
+            wt0 = pa.tile([P, PASSES, 2, OUTS], F32, tag="acc", name="wt0")
             for g in range(PASSES):
                 for u in range(2):
                     k = 2 * g + u
@@ -235,7 +240,7 @@ def tile_kanoriginal_t_kernel(tc, x, coef, scale_base, scale_sp, bias, out):
                 w_words(sp_sb[:].bitcast(F32), spg[:])
                 w_words(sb_sb[:].bitcast(F32), wg[:, 0])
             else:
-                wtb = pa.tile([P, PASSES, 4, OUTS], BF16, tag="acc1", name="wtb")
+                wtb = pa.tile([P, PASSES, 4, OUTS], BF16, tag="rt", name="wtb")
                 for g in range(PASSES):
                     for t in range(4):
                         nc.tensor.transpose(wtb[:, g, t, :], coef_v[:, f - 1, 2 * g + t // 2, t % 2, :], ident_b[:])
@@ -264,19 +269,15 @@ def tile_kanoriginal_t_kernel(tc, x, coef, scale_base, scale_sp, bias, out):
                     load_x(c + 3)
             if t + 1 < STEPS:
                 a_rest(t + 1)
-            if t + 2 < STEPS:
-                a_e(t + 2)
+            if r == 1 and c >= 1:
+                evac_bias(c - 1)
             if cur:
                 b1(t)
-            if prev:
-                mask_lo(t - 1)
             if t == 0:
                 w_copy(3)
                 w_copy(4)
             if cur:
                 b2(t)
-            if prev:
-                merge(t - 1, "n1p")
             if t == 0:
                 w_copy(5)
                 w_copy(6)
@@ -284,10 +285,18 @@ def tile_kanoriginal_t_kernel(tc, x, coef, scale_base, scale_sp, bias, out):
                 b3(t)
             if cur and r == 0:
                 round_act(t)
-            if r == 1 and c + 1 < CHUNKS:
-                silu(c + 1)
+                silu(c)
+            if t + 2 < STEPS:
+                a_e(t + 2)
+            if r == 1 and c >= 1:
+                evac_store(c - 1)
+            if t == 0:
+                w_quantise()
+                nc.vector.tensor_copy(out=bias_f[:], in_=bias_b[:])
             if prev:
+                merge(t - 1, "n1p")
                 merge(t - 1, "n1u")
+                mask_lo(t - 1)
                 relu_neg(t - 1, "n1p")
                 relu_neg(t - 1, "n1u")
                 take_lo(t - 1)
@@ -295,10 +304,7 @@ def tile_kanoriginal_t_kernel(tc, x, coef, scale_base, scale_sp, bias, out):
                 take_hi(t - 1)
                 q_fun(t - 1, "mask")
                 q_fun(t - 1, "n1p")
-            if t == 0:
-                w_quantise()
             if prev and r == 1:
                 quantise(c, 0, sil_t[c][:])
-                if c >= 1:
-                    evacuate(c - 1)
-        evacuate(CHUNKS - 1)
+        evac_bias(CHUNKS - 1)
+        evac_store(CHUNKS - 1)

@@ -22,14 +22,14 @@ PASSES = 2
 CH_ROWS = 256
 BLK = CH_ROWS // P
 CHUNKS = ROWS // CH_ROWS
-STEPS = 2 * CHUNKS
-W = PASSES * CH_ROWS * 4
+W = BLK * FEAT
 CW = W // 4
 HW = W // PASSES
+BANK = 512
 FLOPS = 2 * ROWS * FEAT * OUTS * NFUN
 C6 = 1.0 / math.sqrt(6.0)
 C3 = 1.0 / math.sqrt(3.0)
-C2 = 1.0 / math.sqrt(2.0)
+R2 = math.sqrt(2.0)
 SILU_KNOT = (-1.0 / 3.0 / (1.0 + math.exp(1.0 / 3.0)), 1.0 / 3.0 / (1.0 + math.exp(-1.0 / 3.0)))
 
 
@@ -39,196 +39,214 @@ def tile_kanoriginal_t_kernel(tc, x, coef, scale_base, scale_sp, bias, out):
     ov = out.flatten_outer_dims().rearrange("(c p j) o -> c p (j o)", p=P, j=BLK)
     with ExitStack() as ctx:
         const = ctx.enter_context(tc.tile_pool(name="const", bufs=1))
-        wprep = ctx.enter_context(tc.tile_pool(name="wprep", bufs=1))
         three = ctx.enter_context(tc.tile_pool(name="three", bufs=3))
-        wide = ctx.enter_context(tc.tile_pool(name="wide", bufs=2))
         two = ctx.enter_context(tc.tile_pool(name="two", bufs=2))
         one = ctx.enter_context(tc.tile_pool(name="one", bufs=1))
-        pt = ctx.enter_context(tc.psum_pool(name="pt", bufs=2))
-        pa = ctx.enter_context(tc.psum_pool(name="pa", bufs=2))
+        p2 = ctx.enter_context(tc.psum_pool(name="p2", bufs=2))
+        p1 = ctx.enter_context(tc.psum_pool(name="p1", bufs=1))
         ctx.enter_context(tc.manual_schedule())
 
-        xs_t = {}
-        xt_t = {}
-        sil_t = {}
-        st = {}
-        codes_t = {}
-        scales_t = {}
-        acc_t = {}
-        done = {}
-        rt_t = {}
-
-        def load_x(c):
-            xs = three.tile([P, BLK, FEAT], BF16, name="xs")
-            nc.sync.dma_start(out=xs[:].rearrange("p j i -> p (j i)"), in_=xv[c])
-            xs_t[c] = xs
-
-        def trans_x(c):
-            xs = xs_t[c]
-            for g in range(PASSES):
-                xt = pt.tile([P, 2, CH_ROWS], F32, tag="xt%d" % g, name="xt%d" % g)
-                for j in range(BLK):
-                    xw = xs[:, j, :].bitcast(F32)
-                    for u in range(2):
-                        k = 2 * g + u
-                        nc.tensor.transpose(xt[:, u, j * P:(j + 1) * P], xw[:, k * P:(k + 1) * P], ident_f[:])
-                xt_t[(c, g)] = xt
-
-        def grouped(c, g):
-            return xt_t[(c, g)][:].bitcast(BF16).rearrange("p u (n e) -> p n u e", e=2)
+        T = {}
 
         def split(ap, g):
             return ap[:, g * HW:(g + 1) * HW].rearrange("p (n u e) -> p n u e", u=2, e=2)
 
-        def silu(c):
-            sil = three.tile([P, W], BF16, align_bytes=64, name="sil")
-            for g in range(PASSES):
-                nc.scalar.activation(out=split(sil, g), in_=grouped(c, g), func=ACT.Silu)
-            sil_t[c] = sil
-            done[c] = 0
+        def bank_bf(tile):
+            return tile[:].bitcast(BF16).rearrange("p u (n e) -> p n u e", e=2)
 
-        def quantise(c, f, src):
-            if done[c] == 0:
-                codes_t[c] = two.tile([P, NFUN, CW], U32, align_bytes=64, name="codes")
-                scales_t[c] = two.tile([P, NFUN, CW], U8, align_bytes=64, name="scales")
-                acc_t[c] = pa.tile([P, CH_ROWS], F32, tag="acc", name="acc")
-            codes = codes_t[c]
-            scales = scales_t[c]
+        def load_x(c):
+            xs = three.tile([P, W], BF16, name="xs")
+            nc.sync.dma_start(out=xs[:], in_=xv[c])
+            T["xs", c] = xs
+
+        def words_t(src, g, name):
+            wv = src[:].bitcast(F32)
+            bank = p2.tile([P, 2, CH_ROWS], F32, tag=name, name="wb")
+            for j in range(BLK):
+                for u in range(2):
+                    lo = j * BANK + (2 * g + u) * P
+                    nc.tensor.transpose(bank[:, u, j * P:(j + 1) * P], wv[:, lo:lo + P], ident_f[:])
+            return bank
+
+        def nat(c, r, name, src, func, scale, shift):
+            t = two.tile([P, W], F32, name=name)
+            nc.scalar.activation(out=t[:], in_=src[:], func=func, bias=shift, scale=scale)
+            T[name, c, r] = t
+
+        def s_e(c, r):
+            nat(c, r, "e", T["xs", c], ACT.Abs, 1.5, 0.5 - r)
+
+        def s_h(c, r):
+            nat(c, r, "h", T["e", c, r], ACT.Abs, 0.5, -1.0)
+
+        def s_su(c, r):
+            nat(c, r, "su", T["e", c, r], ACT.Square, C6, -2.0 * C6)
+
+        def s_sp(c, r):
+            nat(c, r, "sp", T["h", c, r], ACT.Square, 2.0 * C3, -2.0 * C3)
+
+        def s_v(c):
+            nat(c, 0, "v", T["h", c, 0], ACT.Abs, 1.0, -0.5)
+
+        def s_sv(c):
+            nat(c, 0, "sv", T["v", c, 0], ACT.Square, R2, 0.0)
+
+        def s_silu(c):
+            sil = two.tile([P, W], BF16, align_bytes=64, name="sil")
+            for g in range(PASSES):
+                nc.scalar.activation(out=split(sil, g), in_=bank_bf(T["xt", c, g]), func=ACT.Silu)
+            T["sil", c] = sil
+
+        def t_x(c):
+            for g in range(PASSES):
+                T["xt", c, g] = words_t(T["xs", c], g, "xt")
+
+        def v_nt(c):
+            t = one.tile([P, W], F32, name="nt3")
+            nc.vector.scalar_tensor_tensor(out=t[:], in0=T["v", c, 0][:], scalar=-2.0, in1=T["sv", c, 0][:], op0=ALU.mult, op1=ALU.mult)
+            T["nt", c] = t
+
+        def cube(c, r, lin, shift, square, name):
+            t = one.tile([P, W], BF16, align_bytes=64, name="%s%d" % (name, r))
+            nc.vector.scalar_tensor_tensor(out=t[:], in0=T[lin, c, r][:], scalar=shift, in1=T[square, c, r][:], op0=ALU.add, op1=ALU.mult)
+            T[name, c, r] = t
+
+        def v_nu(c, r):
+            cube(c, r, "e", -2.0, "su", "nu")
+
+        def v_np(c, r):
+            cube(c, r, "h", -1.0, "sp", "np")
+
+        def t_n(c, r, name, g):
+            T[name + "t", c, r, g] = words_t(T[name, c, r], g, "nt")
+
+        def t_sum(c, b):
+            r, g, j = b // 4, b // 2 % 2, b % 2
+            terms = (("v", 1), ("sv", 1), ("nt", 1)) if r == 0 else (("sv", 2), ("nt", 1))
+            bank = p2.tile([P, 4, P], F32, tag="it", name="ib")
+            for t in range(4):
+                lo = j * FEAT + (2 * g + t // 2) * 2 * P + t % 2
+                parts = []
+                for name, times in terms:
+                    src = T[name, c] if name == "nt" else T[name, c, 0]
+                    parts += [src[:, lo:lo + 2 * P - 1:2]] * times
+                for i, part in enumerate(parts):
+                    nc.tensor.matmul(bank[:, t, :], lhsT=part, rhs=ident_f[:], is_transpose=True, start=(i == 0), stop=(i == len(parts) - 1))
+            T["ib", c, b] = bank
+
+        def i_part(c, b):
+            r, g, j = b // 4, b // 2 % 2, b % 2
+            if g == 0 and j == 0:
+                T["ni", c, r] = two.tile([P, W], BF16, align_bytes=64, name="ni%d" % r)
+            lo = g * HW + j * BANK
+            return r, T["ni", c, r][:, lo:lo + BANK].rearrange("p (n t) -> p n t", t=4), T["ib", c, b][:].rearrange("p t n -> p n t")
+
+        SCALE = (-1.0, 1.0)
+        SHIFT = (-1.0 / 6.0, -2.0 / 3.0)
+
+        def s_ev(c, b):
+            r, dst, src = i_part(c, b)
+            nc.scalar.activation(out=dst, in_=src, func=ACT.Identity, bias=SHIFT[r], scale=SCALE[r])
+
+        def v_ev(c, b):
+            r, dst, src = i_part(c, b)
+            nc.vector.tensor_scalar(out=dst, in0=src, scalar1=SCALE[r], scalar2=SHIFT[r], op0=ALU.mult, op1=ALU.add)
+
+        def v_merge(c, r, name, g):
+            if g == 0:
+                pool = one if name == "nu" else two
+                T[name + "m", c, r] = pool.tile([P, W], BF16, align_bytes=64, name=name + "m")
+            nc.vector.tensor_tensor(out=split(T[name + "m", c, r], g), in0=bank_bf(T[name + "t", c, r, g]), in1=split(T["ni", c, r], g), op=ALU.max)
+
+        def v_relu(c, r, name):
+            t = T[name + "m", c, r]
+            nc.vector.tensor_scalar(out=t[:], in0=t[:], scalar1=-1.0, scalar2=0.0, op0=ALU.mult, op1=ALU.max)
+
+        def v_mask(c, r):
+            mask = two.tile([P, W], BF16, align_bytes=64, name="mask")
+            nc.vector.tensor_scalar(out=mask[:], in0=T["sil", c][:], scalar1=SILU_KNOT[r], scalar2=None, op0=ALU.is_lt)
+            T["lo", c, r] = mask
+
+        def v_lo(c, r):
+            t = T["lo", c, r]
+            nc.vector.tensor_tensor(out=t[:], in0=T["npm", c, r][:], in1=t[:], op=ALU.mult)
+
+        def v_hi(c, r):
+            t = T["npm", c, r]
+            nc.vector.tensor_tensor(out=t[:], in0=t[:], in1=T["lo", c, r][:], op=ALU.subtract)
+
+        def v_q(c, f, src):
+            n = T.get(("done", c), 0)
+            if n == 0:
+                T["codes", c] = two.tile([P, NFUN, CW], U32, align_bytes=64, name="codes")
+                T["scales", c] = two.tile([P, NFUN, CW], U8, align_bytes=64, name="scales")
+                T["acc", c] = p1.tile([P, BANK], F32, tag="acc", name="acc")
+            codes = T["codes", c]
+            scales = T["scales", c]
             nc.vector.quantize_mx(out=codes[:, f, :].bitcast(FP8X4), scales=scales[:, f, :], in_=src)
             for g in range(PASSES):
                 wlo = (f * PASSES + g) * OUTS
                 nc.tensor.matmul_mx(
-                    out=acc_t[c][:],
+                    out=T["acc", c][:, 0:CH_ROWS],
                     lhsT=wcodes[:, wlo:wlo + OUTS].bitcast(FP8X4),
                     lhsT_scale=wscales[:, wlo:wlo + OUTS],
                     rhs=codes[:, f, g * CH_ROWS:(g + 1) * CH_ROWS].bitcast(FP8X4),
                     rhs_scale=scales[:, f, g * CH_ROWS:(g + 1) * CH_ROWS],
-                    start=(done[c] == 0 and g == 0),
-                    stop=(done[c] == NFUN - 1 and g == PASSES - 1),
+                    start=(n == 0 and g == 0),
+                    stop=(n == NFUN - 1 and g == PASSES - 1),
                 )
-            done[c] += 1
+            T["done", c] = n + 1
 
-        def raw(s, pool, name, src, func, scale, shift):
-            t = pool.tile([P, W], F32, name=name)
-            nc.scalar.activation(out=t[:], in_=src[:], func=func, bias=shift, scale=scale)
-            st[s][name] = t
+        def q_u(c, r):
+            v_q(c, 3 + r, T["num", c, r][:])
 
-        def a_e(s):
-            c, r = divmod(s, 2)
-            e = wide.tile([P, W], F32, name="e")
-            for g in range(PASSES):
-                nc.scalar.activation(out=split(e, g), in_=grouped(c, g), func=ACT.Abs, bias=0.5 - r, scale=1.5)
-            st[s] = {"e": e}
+        def q_lo(c, r):
+            v_q(c, 1 + r, T["lo", c, r][:])
 
-        def a_rest(s):
-            d = st[s]
-            raw(s, wide, "h", d["e"], ACT.Abs, 0.5, -1.0)
-            raw(s, wide, "sq_u", d["e"], ACT.Square, C6, -2.0 * C6)
-            if s % 2 == 0:
-                raw(s, one, "a3", d["h"], ACT.Abs, 2.0, -1.0)
-            raw(s, wide, "sq_p", d["h"], ACT.Square, 2.0 * C3, -2.0 * C3)
-            if s % 2 == 0:
-                raw(s, wide, "sq_i", d["a3"], ACT.Square, C2, -C2)
-            else:
-                raw(s, one, "sq_x", st[s - 1]["a3"], ACT.Square, C2, -0.5 * C2)
+        def q_hi(c, r):
+            v_q(c, 5 + r, T["npm", c, r][:])
 
-        def product(s, name, lin, shift, square):
-            d = st[s]
-            if name is None:
-                dst = d[square]
-            else:
-                dst = two.tile([P, W], BF16, align_bytes=64, name=name)
-                d[name] = dst
-            nc.vector.scalar_tensor_tensor(out=dst[:], in0=d[lin][:], scalar=shift, in1=d[square][:], op0=ALU.add, op1=ALU.mult)
+        def q_sil(c):
+            v_q(c, 0, T["sil", c][:])
 
-        def b1(s):
-            product(s, "n1u", "e", -2.0, "sq_u")
-
-        def b2(s):
-            product(s, "n1p", "h", -1.0, "sq_p")
-
-        def b3(s):
-            if s % 2 == 0:
-                product(s, None, "a3", 1.0, "sq_i")
-            else:
-                ni = two.tile([P, W], BF16, align_bytes=64, name="ni")
-                nc.vector.scalar_tensor_tensor(
-                    out=ni[:], in0=st[s]["sq_x"][:], scalar=-7.0 / 24.0, in1=st[s - 1]["sq_i"][:], op0=ALU.add, op1=ALU.subtract
-                )
-                st[s]["ni"] = ni
-
-        def round_act(s):
-            ni = two.tile([P, W], BF16, align_bytes=64, name="ni")
-            nc.scalar.activation(out=ni[:], in_=st[s]["sq_i"][:], func=ACT.Identity, bias=-2.0 / 3.0, scale=1.0)
-            st[s]["ni"] = ni
-
-        def merge(s, name):
-            d = st[s]
-            nc.vector.tensor_tensor(out=d[name][:], in0=d[name][:], in1=d["ni"][:], op=ALU.max)
-
-        def relu_neg(s, name):
-            t = st[s][name]
-            nc.vector.tensor_scalar(out=t[:], in0=t[:], scalar1=-1.0, scalar2=0.0, op0=ALU.mult, op1=ALU.max)
-
-        def mask_lo(s):
-            c, r = divmod(s, 2)
-            mask = one.tile([P, W], BF16, align_bytes=64, name="mask")
-            nc.vector.tensor_scalar(out=mask[:], in0=sil_t[c][:], scalar1=SILU_KNOT[r], scalar2=None, op0=ALU.is_lt)
-            st[s]["mask"] = mask
-
-        def take_lo(s):
-            d = st[s]
-            nc.vector.tensor_tensor(out=d["mask"][:], in0=d["n1p"][:], in1=d["mask"][:], op=ALU.mult)
-
-        def take_hi(s):
-            d = st[s]
-            nc.vector.tensor_tensor(out=d["n1p"][:], in0=d["n1p"][:], in1=d["mask"][:], op=ALU.subtract)
-
-        def q_fun(s, which):
-            c, r = divmod(s, 2)
-            quantise(c, 1 + r + {"mask": 0, "n1u": 2, "n1p": 4}[which], st[s][which][:])
-
-        def evac_bias(c):
+        def s_bias(c):
             o_t = one.tile([P, CH_ROWS], F32, name="o_t")
-            nc.scalar.activation(out=o_t[:], in_=acc_t[c][:], func=ACT.Identity, bias=bias_f[:, 0:1], scale=1.0)
-            rt = pa.tile([P, BLK, OUTS], F32, tag="rt", name="rt")
+            nc.scalar.activation(out=o_t[:], in_=T["acc", c][:, 0:CH_ROWS], func=ACT.Identity, bias=bias_f[:, 0:1], scale=1.0)
+            rt = p1.tile([P, BANK], F32, tag="rt", name="rt")
             for j in range(BLK):
-                nc.tensor.transpose(rt[:, j, :], o_t[:, j * P:(j + 1) * P], ident_f[:])
-            rt_t[c] = rt
+                nc.tensor.transpose(rt[:, j * OUTS:(j + 1) * OUTS], o_t[:, j * P:(j + 1) * P], ident_f[:])
+            T["rt", c] = rt
 
-        def evac_store(c):
-            res = two.tile([P, BLK, OUTS], F32, name="res")
-            nc.scalar.copy(out=res[:], in_=rt_t[c][:])
-            nc.sync.dma_start(out=ov[c], in_=res[:].rearrange("p j o -> p (j o)"))
+        def s_store(c):
+            res = two.tile([P, BLK * OUTS], F32, name="res")
+            nc.scalar.copy(out=res[:], in_=T["rt", c][:, 0:BLK * OUTS])
+            nc.sync.dma_start(out=ov[c], in_=res[:])
 
         load_x(0)
-        sp_sb = wprep.tile([P, FEAT], BF16)
+        sp_sb = const.tile([P, FEAT], BF16)
         nc.sync.dma_start(out=sp_sb[:], in_=scale_sp)
-        sb_sb = wprep.tile([P, FEAT], BF16)
+        sb_sb = const.tile([P, FEAT], BF16)
         nc.sync.dma_start(out=sb_sb[:], in_=scale_base)
-        coef_sb = wprep.tile([P, FEAT * NB], BF16)
+        coef_sb = two.tile([P, FEAT * NB], BF16, align_bytes=64, tag="codes", name="coef_sb")
         nc.sync.dma_start(out=coef_sb[:], in_=coef.rearrange("o i b -> o (i b)"))
         bias_b = const.tile([P, 1], BF16)
         nc.sync.dma_start(out=bias_b[:], in_=bias.rearrange("(o a) -> o a", a=1))
         load_x(1)
-        load_x(2)
         ident_f = const.tile([P, P], F32)
         make_identity(nc, ident_f[:])
         ident_b = const.tile([P, P], BF16)
         make_identity(nc, ident_b[:])
-        trans_x(0)
-        a_e(0)
 
         bias_f = const.tile([P, 1], F32)
-        wg = wprep.tile([P, NFUN, PASSES, OUTS, 4], BF16, align_bytes=64)
+        wg = two.tile([P, NFUN, PASSES, OUTS, 4], BF16, align_bytes=64, tag="codes", name="wg")
         coef_v = coef_sb[:].rearrange("o (w p e b) -> o b w e p", w=4, p=P, e=2, b=NB)
-        spg = wprep.tile([P, PASSES, OUTS, 4], BF16)
+        spg = const.tile([P, PASSES, OUTS, 4], BF16)
         wcodes = const.tile([P, NFUN * PASSES * OUTS], U32, align_bytes=64)
         wscales = const.tile([P, NFUN * PASSES * OUTS], U8, align_bytes=64)
         wg_flat = wg[:].rearrange("p f g o t -> p (f g o t)")
 
         def w_words(src, dst):
-            wt0 = pa.tile([P, PASSES, 2, OUTS], F32, tag="acc", name="wt0")
+            wt0 = p2.tile([P, PASSES, 2, OUTS], F32, tag="nt", name="wt0")
             for g in range(PASSES):
                 for u in range(2):
                     k = 2 * g + u
@@ -240,7 +258,7 @@ def tile_kanoriginal_t_kernel(tc, x, coef, scale_base, scale_sp, bias, out):
                 w_words(sp_sb[:].bitcast(F32), spg[:])
                 w_words(sb_sb[:].bitcast(F32), wg[:, 0])
             else:
-                wtb = pa.tile([P, PASSES, 4, OUTS], BF16, tag="rt", name="wtb")
+                wtb = p2.tile([P, PASSES, 4, OUTS], BF16, tag="nt", name="wtb")
                 for g in range(PASSES):
                     for t in range(4):
                         nc.tensor.transpose(wtb[:, g, t, :], coef_v[:, f - 1, 2 * g + t // 2, t % 2, :], ident_b[:])
@@ -258,53 +276,114 @@ def tile_kanoriginal_t_kernel(tc, x, coef, scale_base, scale_sp, bias, out):
 
         for f in range(3):
             w_copy(f)
+        s_e(0, 0)
+        s_h(0, 0)
+        s_v(0)
+        s_sv(0)
+        for f in range(3, 7):
+            w_copy(f)
+        w_quantise()
+        nc.vector.tensor_copy(out=bias_f[:], in_=bias_b[:])
 
-        for t in range(-1, STEPS + 1):
-            c, r = divmod(t, 2)
-            cur = 0 <= t < STEPS
-            prev = t >= 1
-            if r == 0 and c + 1 < CHUNKS:
-                trans_x(c + 1)
-                if c + 3 < CHUNKS:
-                    load_x(c + 3)
-            if t + 1 < STEPS:
-                a_rest(t + 1)
-            if r == 1 and c >= 1:
-                evac_bias(c - 1)
+        for c in range(CHUNKS + 1):
+            k = c - 1
+            cur = c < CHUNKS
+            fin = c >= 1
+            nxt = c + 1 < CHUNKS
+            if c + 2 < CHUNKS:
+                load_x(c + 2)
             if cur:
-                b1(t)
-            if t == 0:
-                w_copy(3)
-                w_copy(4)
+                v_nt(c)
+            if fin:
+                for g in range(PASSES):
+                    v_merge(k, 0, "nu", g)
+                    t_n(k, 0, "np", g)
             if cur:
-                b2(t)
-            if t == 0:
-                w_copy(5)
-                w_copy(6)
+                s_su(c, 0)
+            if fin:
+                v_mask(k, 0)
             if cur:
-                b3(t)
-            if cur and r == 0:
-                round_act(t)
-                silu(c)
-            if t + 2 < STEPS:
-                a_e(t + 2)
-            if r == 1 and c >= 1:
-                evac_store(c - 1)
-            if t == 0:
-                w_quantise()
-                nc.vector.tensor_copy(out=bias_f[:], in_=bias_b[:])
-            if prev:
-                merge(t - 1, "n1p")
-                merge(t - 1, "n1u")
-                mask_lo(t - 1)
-                relu_neg(t - 1, "n1p")
-                relu_neg(t - 1, "n1u")
-                take_lo(t - 1)
-                q_fun(t - 1, "n1u")
-                take_hi(t - 1)
-                q_fun(t - 1, "mask")
-                q_fun(t - 1, "n1p")
-            if prev and r == 1:
-                quantise(c, 0, sil_t[c][:])
-        evac_bias(CHUNKS - 1)
-        evac_store(CHUNKS - 1)
+                t_sum(c, 0)
+                t_sum(c, 1)
+            if fin:
+                for g in range(PASSES):
+                    v_merge(k, 0, "np", g)
+                    t_n(k, 1, "nu", g)
+            if cur:
+                s_sp(c, 0)
+            if c >= 2:
+                s_bias(c - 2)
+            if fin:
+                v_relu(k, 0, "nu")
+                v_mask(k, 1)
+                v_relu(k, 0, "np")
+            if cur:
+                s_e(c, 1)
+                v_nu(c, 0)
+                s_ev(c, 0)
+                t_sum(c, 2)
+            if c >= 2:
+                s_store(c - 2)
+            if fin:
+                v_lo(k, 0)
+                q_u(k, 0)
+                v_hi(k, 0)
+            if cur:
+                s_h(c, 1)
+                s_ev(c, 1)
+                t_sum(c, 3)
+            if fin:
+                for g in range(PASSES):
+                    v_merge(k, 1, "nu", g)
+                    t_n(k, 1, "np", g)
+            if cur:
+                v_np(c, 0)
+                s_su(c, 1)
+                s_ev(c, 2)
+                t_sum(c, 4)
+            if fin:
+                q_lo(k, 0)
+                for g in range(PASSES):
+                    v_merge(k, 1, "np", g)
+            if cur:
+                for g in range(PASSES):
+                    t_n(c, 0, "nu", g)
+            if fin:
+                q_hi(k, 0)
+                v_relu(k, 1, "nu")
+            if cur:
+                s_sp(c, 1)
+                s_ev(c, 3)
+                t_sum(c, 5)
+                v_nu(c, 1)
+            if fin:
+                v_relu(k, 1, "np")
+                q_u(k, 1)
+                v_lo(k, 1)
+            if nxt:
+                s_e(c + 1, 0)
+            if cur:
+                s_ev(c, 4)
+                t_sum(c, 6)
+                t_x(c)
+            if fin:
+                q_sil(k)
+                v_hi(k, 1)
+            if nxt:
+                s_h(c + 1, 0)
+            if cur:
+                s_ev(c, 5)
+                t_sum(c, 7)
+                v_np(c, 1)
+                v_ev(c, 6)
+                v_ev(c, 7)
+            if nxt:
+                s_v(c + 1)
+                s_sv(c + 1)
+            if cur:
+                s_silu(c)
+            if fin:
+                q_lo(k, 1)
+                q_hi(k, 1)
+        s_bias(CHUNKS - 1)
+        s_store(CHUNKS - 1)

@@ -19,12 +19,8 @@ OUTS = 128
 NB = 6
 NFUN = NB + 1
 PASSES = 2
-CH_ROWS = 256
-BLK = CH_ROWS // P
-CHUNKS = ROWS // CH_ROWS
-W = BLK * FEAT
-CW = W // 4
-HW = W // PASSES
+BLOCKS = (1,) + (2,) * 15 + (1,)
+CHUNKS = len(BLOCKS)
 BANK = 512
 FLOPS = 2 * ROWS * FEAT * OUTS * NFUN
 C6 = 1.0 / math.sqrt(6.0)
@@ -35,8 +31,9 @@ SILU_KNOT = (-1.0 / 3.0 / (1.0 + math.exp(1.0 / 3.0)), 1.0 / 3.0 / (1.0 + math.e
 
 def tile_kanoriginal_t_kernel(tc, x, coef, scale_base, scale_sp, bias, out):
     nc = tc.nc
-    xv = x.flatten_outer_dims().rearrange("(c p j) i -> c p (j i)", p=P, j=BLK)
-    ov = out.flatten_outer_dims().rearrange("(c p j) o -> c p (j o)", p=P, j=BLK)
+    xf = x.flatten_outer_dims()
+    of = out.flatten_outer_dims()
+    rows_of = [slice(P * sum(BLOCKS[:c]), P * sum(BLOCKS[:c + 1])) for c in range(CHUNKS)]
     with ExitStack() as ctx:
         const = ctx.enter_context(tc.tile_pool(name="const", bufs=1))
         three = ctx.enter_context(tc.tile_pool(name="three", bufs=3))
@@ -48,33 +45,47 @@ def tile_kanoriginal_t_kernel(tc, x, coef, scale_base, scale_sp, bias, out):
 
         T = {}
 
-        def split(ap, g):
-            return ap[:, g * HW:(g + 1) * HW].rearrange("p (n u e) -> p n u e", u=2, e=2)
+        def split(c, ap, g):
+            hw = BLOCKS[c] * BANK
+            return ap[:, g * hw:(g + 1) * hw].rearrange("p (n u e) -> p n u e", u=2, e=2)
 
         def bank_bf(tile):
             return tile[:].bitcast(BF16).rearrange("p u (n e) -> p n u e", e=2)
 
         def load_x(c):
-            xs = three.tile([P, W], BF16, name="xs")
-            nc.sync.dma_start(out=xs[:], in_=xv[c])
+            xs = three.tile([P, BLOCKS[c] * FEAT], BF16, name="xs")
+            nc.sync.dma_start(out=xs[:], in_=xf[rows_of[c], :].rearrange("(p j) i -> p (j i)", j=BLOCKS[c]))
             T["xs", c] = xs
 
-        def words_t(src, g, name):
+        def words_t(c, src, g, name):
             wv = src[:].bitcast(F32)
-            bank = p2.tile([P, 2, CH_ROWS], F32, tag=name, name="wb")
-            for j in range(BLK):
+            bank = p2.tile([P, 2, BLOCKS[c] * P], F32, tag=name, name="wb")
+            for j in range(BLOCKS[c]):
                 for u in range(2):
                     lo = j * BANK + (2 * g + u) * P
                     nc.tensor.transpose(bank[:, u, j * P:(j + 1) * P], wv[:, lo:lo + P], ident_f[:])
             return bank
 
         def nat(c, r, name, src, func, scale, shift):
-            t = two.tile([P, W], F32, name=name)
+            t = two.tile([P, BLOCKS[c] * FEAT], F32, name=name)
             nc.scalar.activation(out=t[:], in_=src[:], func=func, bias=shift, scale=scale)
             T[name, c, r] = t
 
         def s_e(c, r):
-            nat(c, r, "e", T["xs", c], ACT.Abs, 1.5, 0.5 - r)
+            t = two.tile([P, BLOCKS[c] * FEAT], F32, name="e")
+            xs = T["xs", c][:]
+            if r == 0:
+                nc.scalar.activation(
+                    out=t[:].rearrange("p (e m) -> p e m", e=2),
+                    in_=xs.rearrange("p (m e) -> p e m", e=2),
+                    func=ACT.Abs, bias=0.5, scale=1.5,
+                )
+            else:
+                nc.scalar.activation(out=t[:], in_=xs, func=ACT.Abs, bias=-0.5, scale=1.5)
+            T["e", c, r] = t
+
+        def by_words(r, ap):
+            return ap.rearrange("p (e m) -> p m e", e=2) if r == 0 else ap
 
         def s_h(c, r):
             nat(c, r, "h", T["e", c, r], ACT.Abs, 0.5, -1.0)
@@ -92,23 +103,26 @@ def tile_kanoriginal_t_kernel(tc, x, coef, scale_base, scale_sp, bias, out):
             nat(c, 0, "sv", T["v", c, 0], ACT.Square, R2, 0.0)
 
         def s_silu(c):
-            sil = two.tile([P, W], BF16, align_bytes=64, name="sil")
+            sil = two.tile([P, BLOCKS[c] * FEAT], BF16, align_bytes=64, name="sil")
             for g in range(PASSES):
-                nc.scalar.activation(out=split(sil, g), in_=bank_bf(T["xt", c, g]), func=ACT.Silu)
+                nc.scalar.activation(out=split(c, sil, g), in_=bank_bf(T["xt", c, g]), func=ACT.Silu)
             T["sil", c] = sil
 
         def t_x(c):
             for g in range(PASSES):
-                T["xt", c, g] = words_t(T["xs", c], g, "xt")
+                T["xt", c, g] = words_t(c, T["xs", c], g, "xt")
 
         def v_nt(c):
-            t = one.tile([P, W], F32, name="nt3")
+            t = one.tile([P, BLOCKS[c] * FEAT], F32, name="nt3")
             nc.vector.scalar_tensor_tensor(out=t[:], in0=T["v", c, 0][:], scalar=-2.0, in1=T["sv", c, 0][:], op0=ALU.mult, op1=ALU.mult)
             T["nt", c] = t
 
         def cube(c, r, lin, shift, square, name):
-            t = one.tile([P, W], BF16, align_bytes=64, name="%s%d" % (name, r))
-            nc.vector.scalar_tensor_tensor(out=t[:], in0=T[lin, c, r][:], scalar=shift, in1=T[square, c, r][:], op0=ALU.add, op1=ALU.mult)
+            t = one.tile([P, BLOCKS[c] * FEAT], BF16, align_bytes=64, name="%s%d" % (name, r))
+            dst = t[:].rearrange("p (m e) -> p m e", e=2) if r == 0 else t[:]
+            nc.vector.scalar_tensor_tensor(
+                out=dst, in0=by_words(r, T[lin, c, r][:]), scalar=shift, in1=by_words(r, T[square, c, r][:]), op0=ALU.add, op1=ALU.mult
+            )
             T[name, c, r] = t
 
         def v_nu(c, r):
@@ -118,52 +132,63 @@ def tile_kanoriginal_t_kernel(tc, x, coef, scale_base, scale_sp, bias, out):
             cube(c, r, "h", -1.0, "sp", "np")
 
         def t_n(c, r, name, g):
-            T[name + "t", c, r, g] = words_t(T[name, c, r], g, "nt")
+            T[name + "t", c, r, g] = words_t(c, T[name, c, r], g, "nt")
+
+        def bank_of(c, b):
+            j = b % BLOCKS[c]
+            r, g = divmod(b // BLOCKS[c], 2)
+            return r, g, j
 
         def t_sum(c, b):
-            r, g, j = b // 4, b // 2 % 2, b % 2
+            r, g, j = bank_of(c, b)
+            if r > 1:
+                return
             terms = (("v", 1), ("sv", 1), ("nt", 1)) if r == 0 else (("sv", 2), ("nt", 1))
             bank = p2.tile([P, 4, P], F32, tag="it", name="ib")
             for t in range(4):
-                lo = j * FEAT + (2 * g + t // 2) * 2 * P + t % 2
+                lo = ((t % 2) * BLOCKS[c] + j) * BANK + (2 * g + t // 2) * P
                 parts = []
                 for name, times in terms:
                     src = T[name, c] if name == "nt" else T[name, c, 0]
-                    parts += [src[:, lo:lo + 2 * P - 1:2]] * times
+                    parts += [src[:, lo:lo + P]] * times
                 for i, part in enumerate(parts):
                     nc.tensor.matmul(bank[:, t, :], lhsT=part, rhs=ident_f[:], is_transpose=True, start=(i == 0), stop=(i == len(parts) - 1))
             T["ib", c, b] = bank
 
         def i_part(c, b):
-            r, g, j = b // 4, b // 2 % 2, b % 2
+            r, g, j = bank_of(c, b)
             if g == 0 and j == 0:
-                T["ni", c, r] = two.tile([P, W], BF16, align_bytes=64, name="ni%d" % r)
-            lo = g * HW + j * BANK
+                T["ni", c, r] = two.tile([P, BLOCKS[c] * FEAT], BF16, align_bytes=64, name="ni%d" % r)
+            lo = (g * BLOCKS[c] + j) * BANK
             return r, T["ni", c, r][:, lo:lo + BANK].rearrange("p (n t) -> p n t", t=4), T["ib", c, b][:].rearrange("p t n -> p n t")
 
         SCALE = (-1.0, 1.0)
         SHIFT = (-1.0 / 6.0, -2.0 / 3.0)
 
         def s_ev(c, b):
+            if b >= 4 * BLOCKS[c]:
+                return
             r, dst, src = i_part(c, b)
             nc.scalar.activation(out=dst, in_=src, func=ACT.Identity, bias=SHIFT[r], scale=SCALE[r])
 
         def v_ev(c, b):
+            if b >= 4 * BLOCKS[c]:
+                return
             r, dst, src = i_part(c, b)
             nc.vector.tensor_scalar(out=dst, in0=src, scalar1=SCALE[r], scalar2=SHIFT[r], op0=ALU.mult, op1=ALU.add)
 
         def v_merge(c, r, name, g):
             if g == 0:
                 pool = one if name == "nu" else two
-                T[name + "m", c, r] = pool.tile([P, W], BF16, align_bytes=64, name=name + "m")
-            nc.vector.tensor_tensor(out=split(T[name + "m", c, r], g), in0=bank_bf(T[name + "t", c, r, g]), in1=split(T["ni", c, r], g), op=ALU.max)
+                T[name + "m", c, r] = pool.tile([P, BLOCKS[c] * FEAT], BF16, align_bytes=64, name=name + "m")
+            nc.vector.tensor_tensor(out=split(c, T[name + "m", c, r], g), in0=bank_bf(T[name + "t", c, r, g]), in1=split(c, T["ni", c, r], g), op=ALU.max)
 
         def v_relu(c, r, name):
             t = T[name + "m", c, r]
             nc.vector.tensor_scalar(out=t[:], in0=t[:], scalar1=-1.0, scalar2=0.0, op0=ALU.mult, op1=ALU.max)
 
         def v_mask(c, r):
-            mask = two.tile([P, W], BF16, align_bytes=64, name="mask")
+            mask = two.tile([P, BLOCKS[c] * FEAT], BF16, align_bytes=64, name="mask")
             nc.vector.tensor_scalar(out=mask[:], in0=T["sil", c][:], scalar1=SILU_KNOT[r], scalar2=None, op0=ALU.is_lt)
             T["lo", c, r] = mask
 
@@ -177,9 +202,10 @@ def tile_kanoriginal_t_kernel(tc, x, coef, scale_base, scale_sp, bias, out):
 
         def v_q(c, f, src):
             n = T.get(("done", c), 0)
+            rows = BLOCKS[c] * P
             if n == 0:
-                T["codes", c] = two.tile([P, NFUN, CW], U32, align_bytes=64, name="codes")
-                T["scales", c] = two.tile([P, NFUN, CW], U8, align_bytes=64, name="scales")
+                T["codes", c] = two.tile([P, NFUN, 2 * rows], U32, align_bytes=64, name="codes")
+                T["scales", c] = two.tile([P, NFUN, 2 * rows], U8, align_bytes=64, name="scales")
                 T["acc", c] = p1.tile([P, BANK], F32, tag="acc", name="acc")
             codes = T["codes", c]
             scales = T["scales", c]
@@ -187,11 +213,11 @@ def tile_kanoriginal_t_kernel(tc, x, coef, scale_base, scale_sp, bias, out):
             for g in range(PASSES):
                 wlo = (f * PASSES + g) * OUTS
                 nc.tensor.matmul_mx(
-                    out=T["acc", c][:, 0:CH_ROWS],
+                    out=T["acc", c][:, 0:rows],
                     lhsT=wcodes[:, wlo:wlo + OUTS].bitcast(FP8X4),
                     lhsT_scale=wscales[:, wlo:wlo + OUTS],
-                    rhs=codes[:, f, g * CH_ROWS:(g + 1) * CH_ROWS].bitcast(FP8X4),
-                    rhs_scale=scales[:, f, g * CH_ROWS:(g + 1) * CH_ROWS],
+                    rhs=codes[:, f, g * rows:(g + 1) * rows].bitcast(FP8X4),
+                    rhs_scale=scales[:, f, g * rows:(g + 1) * rows],
                     start=(n == 0 and g == 0),
                     stop=(n == NFUN - 1 and g == PASSES - 1),
                 )
@@ -210,17 +236,18 @@ def tile_kanoriginal_t_kernel(tc, x, coef, scale_base, scale_sp, bias, out):
             v_q(c, 0, T["sil", c][:])
 
         def s_bias(c):
-            o_t = one.tile([P, CH_ROWS], F32, name="o_t")
-            nc.scalar.activation(out=o_t[:], in_=T["acc", c][:, 0:CH_ROWS], func=ACT.Identity, bias=bias_f[:, 0:1], scale=1.0)
+            rows = BLOCKS[c] * P
+            o_t = one.tile([P, rows], F32, name="o_t")
+            nc.scalar.activation(out=o_t[:], in_=T["acc", c][:, 0:rows], func=ACT.Identity, bias=bias_f[:, 0:1], scale=1.0)
             rt = p1.tile([P, BANK], F32, tag="rt", name="rt")
-            for j in range(BLK):
+            for j in range(BLOCKS[c]):
                 nc.tensor.transpose(rt[:, j * OUTS:(j + 1) * OUTS], o_t[:, j * P:(j + 1) * P], ident_f[:])
             T["rt", c] = rt
 
         def s_store(c):
-            res = two.tile([P, BLK * OUTS], F32, name="res")
-            nc.scalar.copy(out=res[:], in_=T["rt", c][:, 0:BLK * OUTS])
-            nc.sync.dma_start(out=ov[c], in_=res[:])
+            res = two.tile([P, BLOCKS[c] * OUTS], F32, name="res")
+            nc.scalar.copy(out=res[:], in_=T["rt", c][:, 0:BLOCKS[c] * OUTS])
+            nc.sync.dma_start(out=of[rows_of[c], :].rearrange("(p j) o -> p (j o)", j=BLOCKS[c]), in_=res[:])
 
         load_x(0)
         sp_sb = const.tile([P, FEAT], BF16)
@@ -274,16 +301,12 @@ def tile_kanoriginal_t_kernel(tc, x, coef, scale_base, scale_sp, bias, out):
                 )
                 first += width
 
-        for f in range(3):
-            w_copy(f)
         s_e(0, 0)
         s_h(0, 0)
         s_v(0)
         s_sv(0)
-        for f in range(3, 7):
+        for f in range(3):
             w_copy(f)
-        w_quantise()
-        nc.vector.tensor_copy(out=bias_f[:], in_=bias_b[:])
 
         for c in range(CHUNKS + 1):
             k = c - 1
@@ -320,6 +343,10 @@ def tile_kanoriginal_t_kernel(tc, x, coef, scale_base, scale_sp, bias, out):
             if cur:
                 s_e(c, 1)
                 v_nu(c, 0)
+            if c == 0:
+                w_copy(3)
+                w_copy(4)
+            if cur:
                 s_ev(c, 0)
                 t_sum(c, 2)
             if c >= 2:
@@ -338,6 +365,10 @@ def tile_kanoriginal_t_kernel(tc, x, coef, scale_base, scale_sp, bias, out):
                     t_n(k, 1, "np", g)
             if cur:
                 v_np(c, 0)
+            if c == 0:
+                w_copy(5)
+                w_copy(6)
+            if cur:
                 s_su(c, 1)
                 s_ev(c, 2)
                 t_sum(c, 4)
@@ -356,6 +387,9 @@ def tile_kanoriginal_t_kernel(tc, x, coef, scale_base, scale_sp, bias, out):
                 s_ev(c, 3)
                 t_sum(c, 5)
                 v_nu(c, 1)
+            if c == 0:
+                w_quantise()
+                nc.vector.tensor_copy(out=bias_f[:], in_=bias_b[:])
             if fin:
                 v_relu(k, 1, "np")
                 q_u(k, 1)

@@ -25,7 +25,6 @@ BANK = 512
 FLOPS = 2 * ROWS * FEAT * OUTS * NFUN
 C6 = 1.0 / math.sqrt(6.0)
 C3 = 1.0 / math.sqrt(3.0)
-R2 = math.sqrt(2.0)
 SILU_KNOT = (-1.0 / 3.0 / (1.0 + math.exp(1.0 / 3.0)), 1.0 / 3.0 / (1.0 + math.exp(-1.0 / 3.0)))
 
 
@@ -36,9 +35,9 @@ def tile_kanoriginal_t_kernel(tc, x, coef, scale_base, scale_sp, bias, out):
     rows_of = [slice(P * sum(BLOCKS[:c]), P * sum(BLOCKS[:c + 1])) for c in range(CHUNKS)]
     with ExitStack() as ctx:
         const = ctx.enter_context(tc.tile_pool(name="const", bufs=1))
-        three = ctx.enter_context(tc.tile_pool(name="three", bufs=3))
         two = ctx.enter_context(tc.tile_pool(name="two", bufs=2))
         one = ctx.enter_context(tc.tile_pool(name="one", bufs=1))
+        p4 = ctx.enter_context(tc.psum_pool(name="p4", bufs=4))
         p2 = ctx.enter_context(tc.psum_pool(name="p2", bufs=2))
         p1 = ctx.enter_context(tc.psum_pool(name="p1", bufs=1))
         ctx.enter_context(tc.manual_schedule())
@@ -53,54 +52,50 @@ def tile_kanoriginal_t_kernel(tc, x, coef, scale_base, scale_sp, bias, out):
             return tile[:].bitcast(BF16).rearrange("p u (n e) -> p n u e", e=2)
 
         def load_x(c):
-            xs = three.tile([P, BLOCKS[c] * FEAT], BF16, name="xs")
+            xs = two.tile([P, BLOCKS[c] * FEAT], BF16, name="xs")
             nc.sync.dma_start(out=xs[:], in_=xf[rows_of[c], :].rearrange("(p j) i -> p (j i)", j=BLOCKS[c]))
             T["xs", c] = xs
 
-        def words_t(c, src, g, name):
+        def words_t(c, src, g):
             wv = src[:].bitcast(F32)
-            bank = p2.tile([P, 2, BLOCKS[c] * P], F32, tag=name, name="wb")
+            bank = p2.tile([P, 2, BLOCKS[c] * P], F32, tag="nt", name="wb")
             for j in range(BLOCKS[c]):
                 for u in range(2):
                     lo = j * BANK + (2 * g + u) * P
                     nc.tensor.transpose(bank[:, u, j * P:(j + 1) * P], wv[:, lo:lo + P], ident_f[:])
             return bank
 
-        def nat(c, r, name, src, func, scale, shift):
-            t = two.tile([P, BLOCKS[c] * FEAT], F32, name=name)
-            nc.scalar.activation(out=t[:], in_=src[:], func=func, bias=shift, scale=scale)
-            T[name, c, r] = t
+        def nat(pool, c, name, src, func, scale, shift):
+            t = pool.tile([P, BLOCKS[c] * FEAT], F32, name=name)
+            nc.scalar.activation(out=t[:], in_=T[src, c][:], func=func, bias=shift, scale=scale)
+            T[name, c] = t
 
-        def s_e(c, r):
-            t = two.tile([P, BLOCKS[c] * FEAT], F32, name="e")
-            xs = T["xs", c][:]
-            if r == 0:
-                nc.scalar.activation(
-                    out=t[:].rearrange("p (e m) -> p e m", e=2),
-                    in_=xs.rearrange("p (m e) -> p e m", e=2),
-                    func=ACT.Abs, bias=0.5, scale=1.5,
-                )
-            else:
-                nc.scalar.activation(out=t[:], in_=xs, func=ACT.Abs, bias=-0.5, scale=1.5)
-            T["e", c, r] = t
+        def s_e0(c):
+            t = two.tile([P, BLOCKS[c] * FEAT], F32, name="e0")
+            nc.scalar.activation(
+                out=t[:].rearrange("p (e m) -> p e m", e=2),
+                in_=T["xs", c][:].rearrange("p (m e) -> p e m", e=2),
+                func=ACT.Abs, bias=0.5, scale=1.5,
+            )
+            T["e0", c] = t
 
-        def by_words(r, ap):
-            return ap.rearrange("p (e m) -> p m e", e=2) if r == 0 else ap
+        def s_h0(c):
+            nat(two, c, "h0", "e0", ACT.Abs, 0.5, -1.0)
 
-        def s_h(c, r):
-            nat(c, r, "h", T["e", c, r], ACT.Abs, 0.5, -1.0)
+        def s_sq(c):
+            nat(two, c, "sq", "h0", ACT.Square, 2.0, -1.0)
 
-        def s_su(c, r):
-            nat(c, r, "su", T["e", c, r], ACT.Square, C6, -2.0 * C6)
+        def s_e1(c):
+            nat(one, c, "e1", "xs", ACT.Abs, 1.5, -0.5)
 
-        def s_sp(c, r):
-            nat(c, r, "sp", T["h", c, r], ACT.Square, 2.0 * C3, -2.0 * C3)
+        def s_h1(c):
+            nat(one, c, "h1", "e1", ACT.Abs, 0.5, -1.0)
 
-        def s_v(c):
-            nat(c, 0, "v", T["h", c, 0], ACT.Abs, 1.0, -0.5)
+        def s_su(c):
+            nat(one, c, "su", "e1", ACT.Square, C6, -2.0 * C6)
 
-        def s_sv(c):
-            nat(c, 0, "sv", T["v", c, 0], ACT.Square, R2, 0.0)
+        def s_sp(c):
+            nat(one, c, "sp", "h1", ACT.Square, 2.0 * C3, -2.0 * C3)
 
         def s_silu(c):
             sil = two.tile([P, BLOCKS[c] * FEAT], BF16, align_bytes=64, name="sil")
@@ -110,82 +105,103 @@ def tile_kanoriginal_t_kernel(tc, x, coef, scale_base, scale_sp, bias, out):
 
         def t_x(c):
             for g in range(PASSES):
-                T["xt", c, g] = words_t(c, T["xs", c], g, "xt")
+                T["xt", c, g] = words_t(c, T["xs", c], g)
 
-        def v_nt(c):
-            t = one.tile([P, BLOCKS[c] * FEAT], F32, name="nt3")
-            nc.vector.scalar_tensor_tensor(out=t[:], in0=T["v", c, 0][:], scalar=-2.0, in1=T["sv", c, 0][:], op0=ALU.mult, op1=ALU.mult)
-            T["nt", c] = t
+        def stt(c, dst, lin, shift, square):
+            nc.vector.scalar_tensor_tensor(out=dst[:], in0=T[lin, c][:], scalar=shift, in1=T[square, c][:], op0=ALU.add, op1=ALU.mult)
 
-        def cube(c, r, lin, shift, square, name):
-            t = one.tile([P, BLOCKS[c] * FEAT], BF16, align_bytes=64, name="%s%d" % (name, r))
-            dst = t[:].rearrange("p (m e) -> p m e", e=2) if r == 0 else t[:]
-            nc.vector.scalar_tensor_tensor(
-                out=dst, in0=by_words(r, T[lin, c, r][:]), scalar=shift, in1=by_words(r, T[square, c, r][:]), op0=ALU.add, op1=ALU.mult
-            )
-            T[name, c, r] = t
+        def v_qh(c):
+            T["qh", c] = one.tile([P, BLOCKS[c] * FEAT], F32, name="qh")
+            stt(c, T["qh", c], "h0", -0.5, "sq")
 
-        def v_nu(c, r):
-            cube(c, r, "e", -2.0, "su", "nu")
+        def ts(c, name, src, op0, s1, op1, s2):
+            T[name, c] = one.tile([P, BLOCKS[c] * FEAT], F32, name=name)
+            nc.vector.tensor_scalar(out=T[name, c][:], in0=T[src, c][:], scalar1=s1, scalar2=s2, op0=op0, op1=op1)
 
-        def v_np(c, r):
-            cube(c, r, "h", -1.0, "sp", "np")
+        def v_s15(c):
+            ts(c, "s15", "sq", ALU.mult, 1.5, ALU.add, 0.0)
 
-        def t_n(c, r, name, g):
-            T[name + "t", c, r, g] = words_t(c, T[name, c, r], g, "nt")
+        def v_nq(c):
+            ts(c, "nq", "qh", ALU.mult, -1.0, ALU.add, 0.0)
 
-        def bank_of(c, b):
-            j = b % BLOCKS[c]
-            r, g = divmod(b // BLOCKS[c], 2)
-            return r, g, j
+        def v_rp(c):
+            ts(c, "rp", "qh", ALU.max, 0.0, ALU.mult, -2.0)
 
-        def t_sum(c, b):
-            r, g, j = bank_of(c, b)
-            if r > 1:
-                return
-            terms = (("v", 1), ("sv", 1), ("nt", 1)) if r == 0 else (("sv", 2), ("nt", 1))
-            bank = p2.tile([P, 4, P], F32, tag="it", name="ib")
+        def v_rm(c):
+            ts(c, "rm", "qh", ALU.min, 0.0, ALU.mult, 2.0)
+
+        def v_lc(c):
+            t = T["e0", c]
+            nc.vector.tensor_scalar(out=t[:], in0=t[:], scalar1=-1.5, scalar2=2.0, op0=ALU.mult, op1=ALU.add)
+
+        def v_lp(c):
+            t = T["h0", c]
+            nc.vector.tensor_scalar(out=t[:], in0=t[:], scalar1=-3.0, scalar2=2.0, op0=ALU.mult, op1=ALU.add)
+
+        def v_nu(c):
+            T["nu", c] = one.tile([P, BLOCKS[c] * FEAT], BF16, align_bytes=64, name="nu")
+            stt(c, T["nu", c], "e1", -2.0, "su")
+
+        def v_np(c):
+            T["np", c] = one.tile([P, BLOCKS[c] * FEAT], BF16, align_bytes=64, name="np")
+            stt(c, T["np", c], "h1", -1.0, "sp")
+
+        def t_n(c, name, g):
+            T[name + "t", c, g] = words_t(c, T[name, c], g)
+
+        TERMS = {
+            "c": ("e0", "s15", "qh", "rp", "rp"),
+            "p": ("h0", "s15", "nq", "rm", "rm"),
+            "i": ("sq", "qh", "rp"),
+        }
+
+        def t_sum(c, kind, b):
+            g, j = divmod(b, BLOCKS[c])
+            bank = p4.tile([P, 4, P], F32, tag="it", name="ib")
+            terms = TERMS[kind]
             for t in range(4):
                 lo = ((t % 2) * BLOCKS[c] + j) * BANK + (2 * g + t // 2) * P
-                parts = []
-                for name, times in terms:
-                    src = T[name, c] if name == "nt" else T[name, c, 0]
-                    parts += [src[:, lo:lo + P]] * times
-                for i, part in enumerate(parts):
-                    nc.tensor.matmul(bank[:, t, :], lhsT=part, rhs=ident_f[:], is_transpose=True, start=(i == 0), stop=(i == len(parts) - 1))
-            T["ib", c, b] = bank
+                for i, name in enumerate(terms):
+                    nc.tensor.matmul(bank[:, t, :], lhsT=T[name, c][:, lo:lo + P], rhs=ident_f[:], is_transpose=True, start=(i == 0), stop=(i == len(terms) - 1))
+            T["ib", c, kind, b] = bank
 
-        def i_part(c, b):
-            r, g, j = bank_of(c, b)
-            if g == 0 and j == 0:
-                T["ni", c, r] = two.tile([P, BLOCKS[c] * FEAT], BF16, align_bytes=64, name="ni%d" % r)
+        def s_ev(c, kind, b):
+            g, j = divmod(b, BLOCKS[c])
+            if b == 0:
+                T["o" + kind, c] = one.tile([P, BLOCKS[c] * FEAT], BF16, align_bytes=64, name="o" + kind)
             lo = (g * BLOCKS[c] + j) * BANK
-            return r, T["ni", c, r][:, lo:lo + BANK].rearrange("p (n t) -> p n t", t=4), T["ib", c, b][:].rearrange("p t n -> p n t")
+            dst = T["o" + kind, c][:, lo:lo + BANK].rearrange("p (n t) -> p n t", t=4)
+            src = T["ib", c, kind, b][:].rearrange("p t n -> p n t")
+            if kind == "i":
+                nc.scalar.activation(out=dst, in_=src, func=ACT.Identity, bias=-2.0 / 3.0, scale=1.0)
+            else:
+                nc.scalar.activation(out=dst, in_=src, func=ACT.Relu, bias=0.0, scale=1.0 / 3.0)
 
-        SCALE = (-1.0, 1.0)
-        SHIFT = (-1.0 / 6.0, -2.0 / 3.0)
+        def half(c, h):
+            return range(h * BLOCKS[c], (h + 1) * BLOCKS[c])
 
-        def s_ev(c, b):
-            if b >= 4 * BLOCKS[c]:
-                return
-            r, dst, src = i_part(c, b)
-            nc.scalar.activation(out=dst, in_=src, func=ACT.Identity, bias=SHIFT[r], scale=SCALE[r])
+        def sums(c, kind, h):
+            for b in half(c, h):
+                t_sum(c, kind, b)
 
-        def v_ev(c, b):
-            if b >= 4 * BLOCKS[c]:
-                return
-            r, dst, src = i_part(c, b)
-            nc.vector.tensor_scalar(out=dst, in0=src, scalar1=SCALE[r], scalar2=SHIFT[r], op0=ALU.mult, op1=ALU.add)
+        def evs(c, kind, h):
+            for b in half(c, h):
+                s_ev(c, kind, b)
 
-        def v_merge(c, r, name, g):
+        def v_merge(c, name, g):
             if g == 0:
-                pool = one if name == "nu" else two
-                T[name + "m", c, r] = pool.tile([P, BLOCKS[c] * FEAT], BF16, align_bytes=64, name=name + "m")
-            nc.vector.tensor_tensor(out=split(c, T[name + "m", c, r], g), in0=bank_bf(T[name + "t", c, r, g]), in1=split(c, T["ni", c, r], g), op=ALU.max)
+                T[name + "m", c] = one.tile([P, BLOCKS[c] * FEAT], BF16, align_bytes=64, name=name + "m")
+            nc.vector.tensor_tensor(out=split(c, T[name + "m", c], g), in0=bank_bf(T[name + "t", c, g]), in1=split(c, T["oi", c], g), op=ALU.max)
 
-        def v_relu(c, r, name):
-            t = T[name + "m", c, r]
+        def v_relu(c, name):
+            t = T[name + "m", c]
             nc.vector.tensor_scalar(out=t[:], in0=t[:], scalar1=-1.0, scalar2=0.0, op0=ALU.mult, op1=ALU.max)
+
+        def centre(c, r):
+            return T["oc", c] if r == 0 else T["num", c]
+
+        def pair(c, r):
+            return T["op", c] if r == 0 else T["npm", c]
 
         def v_mask(c, r):
             mask = two.tile([P, BLOCKS[c] * FEAT], BF16, align_bytes=64, name="mask")
@@ -194,10 +210,10 @@ def tile_kanoriginal_t_kernel(tc, x, coef, scale_base, scale_sp, bias, out):
 
         def v_lo(c, r):
             t = T["lo", c, r]
-            nc.vector.tensor_tensor(out=t[:], in0=T["npm", c, r][:], in1=t[:], op=ALU.mult)
+            nc.vector.tensor_tensor(out=t[:], in0=pair(c, r)[:], in1=t[:], op=ALU.mult)
 
         def v_hi(c, r):
-            t = T["npm", c, r]
+            t = pair(c, r)
             nc.vector.tensor_tensor(out=t[:], in0=t[:], in1=T["lo", c, r][:], op=ALU.subtract)
 
         def v_q(c, f, src):
@@ -224,13 +240,13 @@ def tile_kanoriginal_t_kernel(tc, x, coef, scale_base, scale_sp, bias, out):
             T["done", c] = n + 1
 
         def q_u(c, r):
-            v_q(c, 3 + r, T["num", c, r][:])
+            v_q(c, 3 + r, centre(c, r)[:])
 
         def q_lo(c, r):
             v_q(c, 1 + r, T["lo", c, r][:])
 
         def q_hi(c, r):
-            v_q(c, 5 + r, T["npm", c, r][:])
+            v_q(c, 5 + r, pair(c, r)[:])
 
         def q_sil(c):
             v_q(c, 0, T["sil", c][:])
@@ -301,10 +317,9 @@ def tile_kanoriginal_t_kernel(tc, x, coef, scale_base, scale_sp, bias, out):
                 )
                 first += width
 
-        s_e(0, 0)
-        s_h(0, 0)
-        s_v(0)
-        s_sv(0)
+        s_e0(0)
+        s_h0(0)
+        s_sq(0)
         for f in range(3):
             w_copy(f)
 
@@ -313,111 +328,93 @@ def tile_kanoriginal_t_kernel(tc, x, coef, scale_base, scale_sp, bias, out):
             cur = c < CHUNKS
             fin = c >= 1
             nxt = c + 1 < CHUNKS
-            if c + 2 < CHUNKS:
-                load_x(c + 2)
             if cur:
-                v_nt(c)
-            if fin:
-                for g in range(PASSES):
-                    v_merge(k, 0, "nu", g)
-                    t_n(k, 0, "np", g)
-            if cur:
-                s_su(c, 0)
-            if fin:
-                v_mask(k, 0)
-            if cur:
-                t_sum(c, 0)
-                t_sum(c, 1)
-            if fin:
-                for g in range(PASSES):
-                    v_merge(k, 0, "np", g)
-                    t_n(k, 1, "nu", g)
-            if cur:
-                s_sp(c, 0)
+                s_e1(c)
+                v_qh(c)
+            if nxt and c >= 1:
+                load_x(c + 1)
             if c >= 2:
                 s_bias(c - 2)
             if fin:
-                v_relu(k, 0, "nu")
-                v_mask(k, 1)
-                v_relu(k, 0, "np")
+                for g in range(PASSES):
+                    t_n(k, "nu", g)
+                q_u(k, 0)
             if cur:
-                s_e(c, 1)
-                v_nu(c, 0)
+                s_h1(c)
+            if c >= 2:
+                s_store(c - 2)
+            if cur:
+                v_s15(c)
+                v_rp(c)
+                v_lc(c)
+                sums(c, "c", 0)
+                sums(c, "c", 1)
+            if fin:
+                v_mask(k, 0)
+            if cur:
+                v_nq(c)
+                s_su(c)
+                s_sp(c)
+            if fin:
+                v_lo(k, 0)
+            if cur:
+                v_rm(c)
+                v_lp(c)
+                evs(c, "c", 0)
+                sums(c, "p", 0)
             if c == 0:
                 w_copy(3)
                 w_copy(4)
-            if cur:
-                s_ev(c, 0)
-                t_sum(c, 2)
-            if c >= 2:
-                s_store(c - 2)
+            if nxt:
+                s_e0(c + 1)
             if fin:
-                v_lo(k, 0)
-                q_u(k, 0)
                 v_hi(k, 0)
-            if cur:
-                s_h(c, 1)
-                s_ev(c, 1)
-                t_sum(c, 3)
-            if fin:
+                q_lo(k, 0)
                 for g in range(PASSES):
-                    v_merge(k, 1, "nu", g)
-                    t_n(k, 1, "np", g)
+                    v_merge(k, "nu", g)
+                    t_n(k, "np", g)
             if cur:
-                v_np(c, 0)
+                evs(c, "c", 1)
+                sums(c, "p", 1)
+            if fin:
+                q_hi(k, 0)
+                v_relu(k, "nu")
             if c == 0:
                 w_copy(5)
                 w_copy(6)
-            if cur:
-                s_su(c, 1)
-                s_ev(c, 2)
-                t_sum(c, 4)
+            if nxt:
+                s_h0(c + 1)
             if fin:
-                q_lo(k, 0)
                 for g in range(PASSES):
-                    v_merge(k, 1, "np", g)
+                    v_merge(k, "np", g)
             if cur:
-                for g in range(PASSES):
-                    t_n(c, 0, "nu", g)
+                t_x(c)
+                evs(c, "p", 0)
+                sums(c, "i", 0)
             if fin:
-                q_hi(k, 0)
-                v_relu(k, 1, "nu")
+                v_mask(k, 1)
+                v_relu(k, "np")
+                q_u(k, 1)
+                v_lo(k, 1)
+            if nxt:
+                s_sq(c + 1)
             if cur:
-                s_sp(c, 1)
-                s_ev(c, 3)
-                t_sum(c, 5)
-                v_nu(c, 1)
+                evs(c, "p", 1)
+                sums(c, "i", 1)
+                v_nu(c)
+                s_silu(c)
             if c == 0:
                 w_quantise()
                 nc.vector.tensor_copy(out=bias_f[:], in_=bias_b[:])
             if fin:
-                v_relu(k, 1, "np")
-                q_u(k, 1)
-                v_lo(k, 1)
-            if nxt:
-                s_e(c + 1, 0)
+                v_hi(k, 1)
+                q_lo(k, 1)
             if cur:
-                s_ev(c, 4)
-                t_sum(c, 6)
-                t_x(c)
+                evs(c, "i", 0)
+                evs(c, "i", 1)
+                v_np(c)
             if fin:
                 q_sil(k)
-                v_hi(k, 1)
-            if nxt:
-                s_h(c + 1, 0)
-            if cur:
-                s_ev(c, 5)
-                t_sum(c, 7)
-                v_np(c, 1)
-                v_ev(c, 6)
-                v_ev(c, 7)
-            if nxt:
-                s_v(c + 1)
-                s_sv(c + 1)
-            if cur:
-                s_silu(c)
-            if fin:
-                q_lo(k, 1)
                 q_hi(k, 1)
         s_bias(CHUNKS - 1)
         s_store(CHUNKS - 1)

@@ -85,6 +85,11 @@ def tile_kanoriginal_t_kernel(tc, x, coef, scale_base, scale_sp, bias, out):
         def s_sq(c):
             nat(two, c, "sq", "h0", ACT.Square, 2.0, -1.0)
 
+        def s_v(c):
+            t = one.tile([P, BLOCKS[c] * FEAT], F32, name="v")
+            nc.scalar.activation(out=t[:], in_=T["h0", c][:], func=ACT.Abs, bias=-1.0, scale=2.0)
+            T["v", c] = t
+
         def s_e1(c):
             nat(one, c, "e1", "xs", ACT.Abs, 1.5, -0.5)
 
@@ -114,29 +119,27 @@ def tile_kanoriginal_t_kernel(tc, x, coef, scale_base, scale_sp, bias, out):
             T["qh", c] = one.tile([P, BLOCKS[c] * FEAT], F32, name="qh")
             stt(c, T["qh", c], "h0", -0.5, "sq")
 
+        def v_ng(c):
+            T["ng", c] = two.tile([P, BLOCKS[c] * FEAT], F32, name="ng")
+            stt(c, T["ng", c], "v", -3.0, "sq")
+
         def ts(c, name, src, op0, s1, op1, s2):
             T[name, c] = one.tile([P, BLOCKS[c] * FEAT], F32, name=name)
             nc.vector.tensor_scalar(out=T[name, c][:], in0=T[src, c][:], scalar1=s1, scalar2=s2, op0=op0, op1=op1)
 
-        def v_s15(c):
-            ts(c, "s15", "sq", ALU.mult, 1.5, ALU.add, 0.0)
-
-        def v_nq(c):
-            ts(c, "nq", "qh", ALU.mult, -1.0, ALU.add, 0.0)
-
         def v_rp(c):
-            ts(c, "rp", "qh", ALU.max, 0.0, ALU.mult, -2.0)
+            ts(c, "rp", "qh", ALU.max, 0.0, ALU.mult, 4.0)
 
         def v_rm(c):
-            ts(c, "rm", "qh", ALU.min, 0.0, ALU.mult, 2.0)
+            ts(c, "rm", "qh", ALU.min, 0.0, ALU.mult, -4.0)
 
         def v_lc(c):
             t = T["e0", c]
-            nc.vector.tensor_scalar(out=t[:], in0=t[:], scalar1=-1.5, scalar2=2.0, op0=ALU.mult, op1=ALU.add)
+            nc.vector.tensor_scalar(out=t[:], in0=t[:], scalar1=3.0, scalar2=-4.0, op0=ALU.mult, op1=ALU.add)
 
         def v_lp(c):
             t = T["h0", c]
-            nc.vector.tensor_scalar(out=t[:], in0=t[:], scalar1=-3.0, scalar2=2.0, op0=ALU.mult, op1=ALU.add)
+            nc.vector.tensor_scalar(out=t[:], in0=t[:], scalar1=6.0, scalar2=-4.0, op0=ALU.mult, op1=ALU.add)
 
         def v_nu(c):
             T["nu", c] = one.tile([P, BLOCKS[c] * FEAT], BF16, align_bytes=64, name="nu")
@@ -150,9 +153,9 @@ def tile_kanoriginal_t_kernel(tc, x, coef, scale_base, scale_sp, bias, out):
             T[name + "t", c, g] = words_t(c, T[name, c], g)
 
         TERMS = {
-            "c": ("e0", "s15", "qh", "rp", "rp"),
-            "p": ("h0", "s15", "nq", "rm", "rm"),
-            "i": ("sq", "qh", "rp"),
+            "c": ("e0", "ng", "rp"),
+            "p": ("h0", "ng", "rm"),
+            "i": ("sq", "ng"),
         }
 
         def t_sum(c, kind, b):
@@ -168,14 +171,14 @@ def tile_kanoriginal_t_kernel(tc, x, coef, scale_base, scale_sp, bias, out):
         def s_ev(c, kind, b):
             g, j = divmod(b, BLOCKS[c])
             if b == 0:
-                T["o" + kind, c] = one.tile([P, BLOCKS[c] * FEAT], BF16, align_bytes=64, name="o" + kind)
+                T["o" + kind, c] = (two if kind == "p" else one).tile([P, BLOCKS[c] * FEAT], BF16, align_bytes=64, name="o" + kind)
             lo = (g * BLOCKS[c] + j) * BANK
             dst = T["o" + kind, c][:, lo:lo + BANK].rearrange("p (n t) -> p n t", t=4)
             src = T["ib", c, kind, b][:].rearrange("p t n -> p n t")
             if kind == "i":
-                nc.scalar.activation(out=dst, in_=src, func=ACT.Identity, bias=-2.0 / 3.0, scale=1.0)
+                nc.scalar.activation(out=dst, in_=src, func=ACT.Identity, bias=-2.0 / 3.0, scale=-0.5)
             else:
-                nc.scalar.activation(out=dst, in_=src, func=ACT.Relu, bias=0.0, scale=1.0 / 3.0)
+                nc.scalar.activation(out=dst, in_=src, func=ACT.Relu, bias=0.0, scale=-1.0 / 6.0)
 
         def half(c, h):
             return range(h * BLOCKS[c], (h + 1) * BLOCKS[c])
@@ -320,6 +323,7 @@ def tile_kanoriginal_t_kernel(tc, x, coef, scale_base, scale_sp, bias, out):
         s_e0(0)
         s_h0(0)
         s_sq(0)
+        s_v(0)
         for f in range(3):
             w_copy(f)
 
@@ -329,92 +333,89 @@ def tile_kanoriginal_t_kernel(tc, x, coef, scale_base, scale_sp, bias, out):
             fin = c >= 1
             nxt = c + 1 < CHUNKS
             if cur:
-                s_e1(c)
                 v_qh(c)
-            if nxt and c >= 1:
-                load_x(c + 1)
-            if c >= 2:
-                s_bias(c - 2)
+                s_e1(c)
             if fin:
+                sums(k, "i", 0)
+                sums(k, "i", 1)
                 for g in range(PASSES):
                     t_n(k, "nu", g)
-                q_u(k, 0)
+                evs(k, "i", 0)
+            if nxt and c >= 1:
+                load_x(c + 1)
             if cur:
                 s_h1(c)
             if c >= 2:
+                s_bias(c - 2)
+            if fin:
+                evs(k, "i", 1)
+                q_u(k, 0)
+            if cur:
+                v_ng(c)
+                v_lc(c)
+                v_rp(c)
+                sums(c, "c", 0)
+                s_su(c)
+            if c >= 2:
                 s_store(c - 2)
             if cur:
-                v_s15(c)
-                v_rp(c)
-                v_lc(c)
-                sums(c, "c", 0)
+                v_lp(c)
+                v_rm(c)
                 sums(c, "c", 1)
+                s_sp(c)
+            if c == 0:
+                for f in range(3, NFUN):
+                    w_copy(f)
             if fin:
+                for g in range(PASSES):
+                    v_merge(k, "nu", g)
+                    t_n(k, "np", g)
                 v_mask(k, 0)
             if cur:
-                v_nq(c)
-                s_su(c)
-                s_sp(c)
-            if fin:
-                v_lo(k, 0)
-            if cur:
-                v_rm(c)
-                v_lp(c)
                 evs(c, "c", 0)
                 sums(c, "p", 0)
-            if c == 0:
-                w_copy(3)
-                w_copy(4)
+            if fin:
+                v_relu(k, "nu")
+                v_lo(k, 0)
+                q_u(k, 1)
             if nxt:
                 s_e0(c + 1)
             if fin:
                 v_hi(k, 0)
-                q_lo(k, 0)
-                for g in range(PASSES):
-                    v_merge(k, "nu", g)
-                    t_n(k, "np", g)
-            if cur:
-                evs(c, "c", 1)
-                sums(c, "p", 1)
-            if fin:
-                q_hi(k, 0)
-                v_relu(k, "nu")
-            if c == 0:
-                w_copy(5)
-                w_copy(6)
-            if nxt:
-                s_h0(c + 1)
-            if fin:
                 for g in range(PASSES):
                     v_merge(k, "np", g)
             if cur:
+                evs(c, "c", 1)
+                sums(c, "p", 1)
                 t_x(c)
-                evs(c, "p", 0)
-                sums(c, "i", 0)
             if fin:
-                v_mask(k, 1)
+                q_lo(k, 0)
                 v_relu(k, "np")
-                q_u(k, 1)
-                v_lo(k, 1)
+            if nxt:
+                s_h0(c + 1)
+            if fin:
+                q_hi(k, 0)
+                v_mask(k, 1)
+            if cur:
+                evs(c, "p", 0)
+                v_nu(c)
             if nxt:
                 s_sq(c + 1)
-            if cur:
-                evs(c, "p", 1)
-                sums(c, "i", 1)
-                v_nu(c)
-                s_silu(c)
+            if fin:
+                v_lo(k, 1)
+                q_sil(k)
+                v_hi(k, 1)
             if c == 0:
                 w_quantise()
                 nc.vector.tensor_copy(out=bias_f[:], in_=bias_b[:])
-            if fin:
-                v_hi(k, 1)
-                q_lo(k, 1)
+            if nxt:
+                s_v(c + 1)
             if cur:
-                evs(c, "i", 0)
-                evs(c, "i", 1)
+                evs(c, "p", 1)
                 v_np(c)
+                s_silu(c)
             if fin:
-                q_sil(k)
+                q_lo(k, 1)
                 q_hi(k, 1)
         s_bias(CHUNKS - 1)
         s_store(CHUNKS - 1)

@@ -39,7 +39,6 @@ def tile_kanoriginal_t_kernel(tc, x, coef, scale_base, scale_sp, bias, out):
         one = ctx.enter_context(tc.tile_pool(name="one", bufs=1))
         p4 = ctx.enter_context(tc.psum_pool(name="p4", bufs=4))
         p2 = ctx.enter_context(tc.psum_pool(name="p2", bufs=2))
-        p1 = ctx.enter_context(tc.psum_pool(name="p1", bufs=1))
         ctx.enter_context(tc.manual_schedule())
 
         T = {}
@@ -225,7 +224,7 @@ def tile_kanoriginal_t_kernel(tc, x, coef, scale_base, scale_sp, bias, out):
             if n == 0:
                 T["codes", c] = two.tile([P, NFUN, 2 * rows], U32, align_bytes=64, name="codes")
                 T["scales", c] = two.tile([P, NFUN, 2 * rows], U8, align_bytes=64, name="scales")
-                T["acc", c] = p1.tile([P, BANK], F32, tag="acc", name="acc")
+                T["acc", c] = p2.tile([P, BANK], F32, tag="acc", name="acc")
             codes = T["codes", c]
             scales = T["scales", c]
             nc.vector.quantize_mx(out=codes[:, f, :].bitcast(FP8X4), scales=scales[:, f, :], in_=src)
@@ -258,7 +257,7 @@ def tile_kanoriginal_t_kernel(tc, x, coef, scale_base, scale_sp, bias, out):
             rows = BLOCKS[c] * P
             o_t = one.tile([P, rows], F32, name="o_t")
             nc.scalar.activation(out=o_t[:], in_=T["acc", c][:, 0:rows], func=ACT.Identity, bias=bias_f[:, 0:1], scale=1.0)
-            rt = p1.tile([P, BANK], F32, tag="rt", name="rt")
+            rt = p2.tile([P, BANK], F32, tag="nt", name="rt")
             for j in range(BLOCKS[c]):
                 nc.tensor.transpose(rt[:, j * OUTS:(j + 1) * OUTS], o_t[:, j * P:(j + 1) * P], ident_f[:])
             T["rt", c] = rt
@@ -336,18 +335,14 @@ def tile_kanoriginal_t_kernel(tc, x, coef, scale_base, scale_sp, bias, out):
                 v_qh(c)
                 s_e1(c)
             if fin:
-                sums(k, "i", 0)
-                sums(k, "i", 1)
-                for g in range(PASSES):
-                    t_n(k, "nu", g)
                 evs(k, "i", 0)
             if nxt and c >= 1:
                 load_x(c + 1)
             if cur:
                 s_h1(c)
-            if c >= 2:
-                s_bias(c - 2)
             if fin:
+                for g in range(PASSES):
+                    t_n(k, "nu", g)
                 evs(k, "i", 1)
                 q_u(k, 0)
             if cur:
@@ -356,13 +351,12 @@ def tile_kanoriginal_t_kernel(tc, x, coef, scale_base, scale_sp, bias, out):
                 v_rp(c)
                 sums(c, "c", 0)
                 s_su(c)
-            if c >= 2:
-                s_store(c - 2)
-            if cur:
                 v_lp(c)
                 v_rm(c)
                 sums(c, "c", 1)
                 s_sp(c)
+            if c >= 2:
+                s_bias(c - 2)
             if c == 0:
                 for f in range(3, NFUN):
                     w_copy(f)
@@ -371,6 +365,10 @@ def tile_kanoriginal_t_kernel(tc, x, coef, scale_base, scale_sp, bias, out):
                     v_merge(k, "nu", g)
                     t_n(k, "np", g)
                 v_mask(k, 0)
+            if nxt:
+                s_e0(c + 1)
+            if c >= 2:
+                s_store(c - 2)
             if cur:
                 evs(c, "c", 0)
                 sums(c, "p", 0)
@@ -379,7 +377,7 @@ def tile_kanoriginal_t_kernel(tc, x, coef, scale_base, scale_sp, bias, out):
                 v_lo(k, 0)
                 q_u(k, 1)
             if nxt:
-                s_e0(c + 1)
+                s_h0(c + 1)
             if fin:
                 v_hi(k, 0)
                 for g in range(PASSES):
@@ -392,15 +390,16 @@ def tile_kanoriginal_t_kernel(tc, x, coef, scale_base, scale_sp, bias, out):
                 q_lo(k, 0)
                 v_relu(k, "np")
             if nxt:
-                s_h0(c + 1)
+                s_sq(c + 1)
             if fin:
                 q_hi(k, 0)
                 v_mask(k, 1)
             if cur:
                 evs(c, "p", 0)
+                sums(c, "i", 0)
                 v_nu(c)
             if nxt:
-                s_sq(c + 1)
+                s_v(c + 1)
             if fin:
                 v_lo(k, 1)
                 q_sil(k)
@@ -408,10 +407,9 @@ def tile_kanoriginal_t_kernel(tc, x, coef, scale_base, scale_sp, bias, out):
             if c == 0:
                 w_quantise()
                 nc.vector.tensor_copy(out=bias_f[:], in_=bias_b[:])
-            if nxt:
-                s_v(c + 1)
             if cur:
                 evs(c, "p", 1)
+                sums(c, "i", 1)
                 v_np(c)
                 s_silu(c)
             if fin:

@@ -79,14 +79,14 @@ def tile_kanoriginal_t_kernel(tc, x, coef, scale_base, scale_sp, bias, out):
             T["e0", c] = t
 
         def s_h0(c):
-            nat(two, c, "h0", "e0", ACT.Abs, 0.5, -1.0)
+            nat(two, c, "h0", "e0", ACT.Abs, 2.0, -4.0)
 
         def s_sq(c):
-            nat(two, c, "sq", "h0", ACT.Square, 2.0, -1.0)
+            nat(two, c, "sq", "h0", ACT.Square, 0.5, -1.0)
 
         def s_v(c):
             t = one.tile([P, BLOCKS[c] * FEAT], F32, name="v")
-            nc.scalar.activation(out=t[:], in_=T["h0", c][:], func=ACT.Abs, bias=-1.0, scale=2.0)
+            nc.scalar.activation(out=t[:], in_=T["h0", c][:], func=ACT.Abs, bias=-1.0, scale=0.5)
             T["v", c] = t
 
         def s_e1(c):
@@ -114,9 +114,9 @@ def tile_kanoriginal_t_kernel(tc, x, coef, scale_base, scale_sp, bias, out):
         def stt(c, dst, lin, shift, square):
             nc.vector.scalar_tensor_tensor(out=dst[:], in0=T[lin, c][:], scalar=shift, in1=T[square, c][:], op0=ALU.add, op1=ALU.mult)
 
-        def v_qh(c):
-            T["qh", c] = one.tile([P, BLOCKS[c] * FEAT], F32, name="qh")
-            stt(c, T["qh", c], "h0", -0.5, "sq")
+        def v_q2(c):
+            T["q2", c] = one.tile([P, BLOCKS[c] * FEAT], F32, name="q2")
+            stt(c, T["q2", c], "h0", -2.0, "sq")
 
         def v_ng(c):
             T["ng", c] = two.tile([P, BLOCKS[c] * FEAT], F32, name="ng")
@@ -126,11 +126,8 @@ def tile_kanoriginal_t_kernel(tc, x, coef, scale_base, scale_sp, bias, out):
             T[name, c] = one.tile([P, BLOCKS[c] * FEAT], F32, name=name)
             nc.vector.tensor_scalar(out=T[name, c][:], in0=T[src, c][:], scalar1=s1, scalar2=s2, op0=op0, op1=op1)
 
-        def v_rp(c):
-            ts(c, "rp", "qh", ALU.max, 0.0, ALU.mult, 4.0)
-
         def v_rm(c):
-            ts(c, "rm", "qh", ALU.min, 0.0, ALU.mult, -4.0)
+            ts(c, "rm", "q2", ALU.min, 0.0, ALU.mult, -1.0)
 
         def v_lc(c):
             t = T["e0", c]
@@ -138,7 +135,7 @@ def tile_kanoriginal_t_kernel(tc, x, coef, scale_base, scale_sp, bias, out):
 
         def v_lp(c):
             t = T["h0", c]
-            nc.vector.tensor_scalar(out=t[:], in0=t[:], scalar1=6.0, scalar2=-4.0, op0=ALU.mult, op1=ALU.add)
+            nc.vector.tensor_scalar(out=t[:], in0=t[:], scalar1=1.5, scalar2=-4.0, op0=ALU.mult, op1=ALU.add)
 
         def v_nu(c):
             T["nu", c] = one.tile([P, BLOCKS[c] * FEAT], BF16, align_bytes=64, name="nu")
@@ -152,7 +149,7 @@ def tile_kanoriginal_t_kernel(tc, x, coef, scale_base, scale_sp, bias, out):
             T[name + "t", c, g] = words_t(c, T[name, c], g)
 
         TERMS = {
-            "c": ("e0", "ng", "rp"),
+            "c": ("rm", "q2", "e0", "ng"),
             "p": ("h0", "ng", "rm"),
             "i": ("sq", "ng"),
         }
@@ -167,17 +164,30 @@ def tile_kanoriginal_t_kernel(tc, x, coef, scale_base, scale_sp, bias, out):
                     nc.tensor.matmul(bank[:, t, :], lhsT=T[name, c][:, lo:lo + P], rhs=ident_f[:], is_transpose=True, start=(i == 0), stop=(i == len(terms) - 1))
             T["ib", c, kind, b] = bank
 
-        def s_ev(c, kind, b):
+        def ev_views(c, kind, b):
             g, j = divmod(b, BLOCKS[c])
-            if b == 0:
-                T["o" + kind, c] = (two if kind == "p" else one).tile([P, BLOCKS[c] * FEAT], BF16, align_bytes=64, name="o" + kind)
+            if b == 0 and kind == "p":
+                pair_tile(c, 0)
+            elif b == 0:
+                T["o" + kind, c] = one.tile([P, BLOCKS[c] * FEAT], BF16, align_bytes=64, name="o" + kind)
+            tile = T["pr", c, 0][:, 1, :] if kind == "p" else T["o" + kind, c][:]
             lo = (g * BLOCKS[c] + j) * BANK
-            dst = T["o" + kind, c][:, lo:lo + BANK].rearrange("p (n t) -> p n t", t=4)
-            src = T["ib", c, kind, b][:].rearrange("p t n -> p n t")
+            return tile[:, lo:lo + BANK].rearrange("p (n t) -> p n t", t=4), T["ib", c, kind, b][:].rearrange("p t n -> p n t")
+
+        def s_ev(c, kind, b):
+            dst, src = ev_views(c, kind, b)
             if kind == "i":
                 nc.scalar.activation(out=dst, in_=src, func=ACT.Identity, bias=-2.0 / 3.0, scale=-0.5)
             else:
                 nc.scalar.activation(out=dst, in_=src, func=ACT.Relu, bias=0.0, scale=-1.0 / 6.0)
+
+        def v_evi(c):
+            for b in half(c, 1):
+                dst, src = ev_views(c, "i", b)
+                nc.vector.tensor_scalar(out=dst, in0=src, scalar1=-0.5, scalar2=-2.0 / 3.0, op0=ALU.mult, op1=ALU.add)
+
+        def pair_tile(c, r):
+            T["pr", c, r] = (two if r == 0 else one).tile([P, 2, BLOCKS[c] * FEAT], BF16, align_bytes=64, name="pr%d" % r)
 
         def half(c, h):
             return range(h * BLOCKS[c], (h + 1) * BLOCKS[c])
@@ -190,68 +200,63 @@ def tile_kanoriginal_t_kernel(tc, x, coef, scale_base, scale_sp, bias, out):
             for b in half(c, h):
                 s_ev(c, kind, b)
 
-        def v_merge(c, name, g):
+        def v_merge_nu(c, g):
             if g == 0:
-                T[name + "m", c] = one.tile([P, BLOCKS[c] * FEAT], BF16, align_bytes=64, name=name + "m")
-            nc.vector.tensor_tensor(out=split(c, T[name + "m", c], g), in0=bank_bf(T[name + "t", c, g]), in1=split(c, T["oi", c], g), op=ALU.max)
+                T["num", c] = one.tile([P, BLOCKS[c] * FEAT], BF16, align_bytes=64, name="num")
+            merge(c, T["num", c][:], "nu", g)
 
-        def v_relu(c, name):
-            t = T[name + "m", c]
-            nc.vector.tensor_scalar(out=t[:], in0=t[:], scalar1=-1.0, scalar2=0.0, op0=ALU.mult, op1=ALU.max)
+        def v_merge_np(c, g):
+            if g == 0:
+                pair_tile(c, 1)
+            merge(c, T["pr", c, 1][:, 1, :], "np", g)
 
-        def centre(c, r):
-            return T["oc", c] if r == 0 else T["num", c]
+        def merge(c, dst, name, g):
+            nc.vector.tensor_tensor(out=split(c, dst, g), in0=bank_bf(T[name + "t", c, g]), in1=split(c, T["oi", c], g), op=ALU.max)
 
-        def pair(c, r):
-            return T["op", c] if r == 0 else T["npm", c]
+        def relu_neg(t):
+            nc.vector.tensor_scalar(out=t, in0=t, scalar1=-1.0, scalar2=0.0, op0=ALU.mult, op1=ALU.max)
 
         def v_mask(c, r):
-            mask = two.tile([P, BLOCKS[c] * FEAT], BF16, align_bytes=64, name="mask")
-            nc.vector.tensor_scalar(out=mask[:], in0=T["sil", c][:], scalar1=SILU_KNOT[r], scalar2=None, op0=ALU.is_lt)
-            T["lo", c, r] = mask
+            nc.vector.tensor_scalar(out=T["pr", c, r][:, 0, :], in0=T["sil", c][:], scalar1=SILU_KNOT[r], scalar2=None, op0=ALU.is_lt)
 
         def v_lo(c, r):
-            t = T["lo", c, r]
-            nc.vector.tensor_tensor(out=t[:], in0=pair(c, r)[:], in1=t[:], op=ALU.mult)
+            t = T["pr", c, r]
+            nc.vector.tensor_tensor(out=t[:, 0, :], in0=t[:, 1, :], in1=t[:, 0, :], op=ALU.mult)
 
         def v_hi(c, r):
-            t = pair(c, r)
-            nc.vector.tensor_tensor(out=t[:], in0=t[:], in1=T["lo", c, r][:], op=ALU.subtract)
+            t = T["pr", c, r]
+            nc.vector.tensor_tensor(out=t[:, 1, :], in0=t[:, 1, :], in1=t[:, 0, :], op=ALU.subtract)
 
-        def v_q(c, f, src):
-            n = T.get(("done", c), 0)
+        SLOT_FUN = (3, 4, 1, 5, 0, 2, 6)
+
+        def quant(c, slot, src, count=1):
             rows = BLOCKS[c] * P
-            if n == 0:
-                T["codes", c] = two.tile([P, NFUN, 2 * rows], U32, align_bytes=64, name="codes")
-                T["scales", c] = two.tile([P, NFUN, 2 * rows], U8, align_bytes=64, name="scales")
+            if slot == 0:
+                T["codes", c] = two.tile([P, NFUN * 2 * rows], U32, align_bytes=64, name="codes")
+                T["scales", c] = two.tile([P, NFUN * 2 * rows], U8, align_bytes=64, name="scales")
                 T["acc", c] = p2.tile([P, BANK], F32, tag="acc", name="acc")
-            codes = T["codes", c]
-            scales = T["scales", c]
-            nc.vector.quantize_mx(out=codes[:, f, :].bitcast(FP8X4), scales=scales[:, f, :], in_=src)
-            for g in range(PASSES):
-                wlo = (f * PASSES + g) * OUTS
-                nc.tensor.matmul_mx(
-                    out=T["acc", c][:, 0:rows],
-                    lhsT=wcodes[:, wlo:wlo + OUTS].bitcast(FP8X4),
-                    lhsT_scale=wscales[:, wlo:wlo + OUTS],
-                    rhs=codes[:, f, g * rows:(g + 1) * rows].bitcast(FP8X4),
-                    rhs_scale=scales[:, f, g * rows:(g + 1) * rows],
-                    start=(n == 0 and g == 0),
-                    stop=(n == NFUN - 1 and g == PASSES - 1),
-                )
-            T["done", c] = n + 1
+            lo = slot * 2 * rows
+            hi = lo + count * 2 * rows
+            nc.vector.quantize_mx(out=T["codes", c][:, lo:hi].bitcast(FP8X4), scales=T["scales", c][:, lo:hi], in_=src)
 
-        def q_u(c, r):
-            v_q(c, 3 + r, centre(c, r)[:])
+        def t_mm(c, first, last):
+            rows = BLOCKS[c] * P
+            for slot in range(first, last):
+                for g in range(PASSES):
+                    wlo = (SLOT_FUN[slot] * PASSES + g) * OUTS
+                    lo = (slot * PASSES + g) * rows
+                    nc.tensor.matmul_mx(
+                        out=T["acc", c][:, 0:rows],
+                        lhsT=wcodes[:, wlo:wlo + OUTS].bitcast(FP8X4),
+                        lhsT_scale=wscales[:, wlo:wlo + OUTS],
+                        rhs=T["codes", c][:, lo:lo + rows].bitcast(FP8X4),
+                        rhs_scale=T["scales", c][:, lo:lo + rows],
+                        start=(slot == 0 and g == 0),
+                        stop=(slot == NFUN - 1 and g == PASSES - 1),
+                    )
 
-        def q_lo(c, r):
-            v_q(c, 1 + r, T["lo", c, r][:])
-
-        def q_hi(c, r):
-            v_q(c, 5 + r, pair(c, r)[:])
-
-        def q_sil(c):
-            v_q(c, 0, T["sil", c][:])
+        def q_pair(c, r):
+            quant(c, 2 if r == 0 else 5, T["pr", c, r][:].rearrange("p s w -> p (s w)"), 2)
 
         def s_bias(c):
             rows = BLOCKS[c] * P
@@ -332,8 +337,11 @@ def tile_kanoriginal_t_kernel(tc, x, coef, scale_base, scale_sp, bias, out):
             fin = c >= 1
             nxt = c + 1 < CHUNKS
             if cur:
-                v_qh(c)
+                v_q2(c)
                 s_e1(c)
+            if c >= 2:
+                q_pair(c - 2, 1)
+                t_mm(c - 2, 4, NFUN)
             if fin:
                 evs(k, "i", 0)
             if nxt and c >= 1:
@@ -343,16 +351,14 @@ def tile_kanoriginal_t_kernel(tc, x, coef, scale_base, scale_sp, bias, out):
             if fin:
                 for g in range(PASSES):
                     t_n(k, "nu", g)
-                evs(k, "i", 1)
-                q_u(k, 0)
+                quant(k, 0, T["oc", k][:])
             if cur:
                 v_ng(c)
+                v_rm(c)
                 v_lc(c)
-                v_rp(c)
                 sums(c, "c", 0)
                 s_su(c)
                 v_lp(c)
-                v_rm(c)
                 sums(c, "c", 1)
                 s_sp(c)
             if c >= 2:
@@ -361,10 +367,11 @@ def tile_kanoriginal_t_kernel(tc, x, coef, scale_base, scale_sp, bias, out):
                 for f in range(3, NFUN):
                     w_copy(f)
             if fin:
-                for g in range(PASSES):
-                    v_merge(k, "nu", g)
-                    t_n(k, "np", g)
+                v_evi(k)
                 v_mask(k, 0)
+                for g in range(PASSES):
+                    v_merge_nu(k, g)
+                    t_n(k, "np", g)
             if nxt:
                 s_e0(c + 1)
             if c >= 2:
@@ -373,47 +380,51 @@ def tile_kanoriginal_t_kernel(tc, x, coef, scale_base, scale_sp, bias, out):
                 evs(c, "c", 0)
                 sums(c, "p", 0)
             if fin:
-                v_relu(k, "nu")
                 v_lo(k, 0)
-                q_u(k, 1)
-            if nxt:
-                s_h0(c + 1)
+                relu_neg(T["num", k][:])
+            if cur:
+                v_nu(c)
             if fin:
                 v_hi(k, 0)
-                for g in range(PASSES):
-                    v_merge(k, "np", g)
+                quant(k, 1, T["num", k][:])
+            if nxt:
+                s_h0(c + 1)
             if cur:
                 evs(c, "c", 1)
                 sums(c, "p", 1)
-                t_x(c)
             if fin:
-                q_lo(k, 0)
-                v_relu(k, "np")
+                for g in range(PASSES):
+                    v_merge_np(k, g)
+            if cur:
+                t_x(c)
             if nxt:
                 s_sq(c + 1)
             if fin:
-                q_hi(k, 0)
+                q_pair(k, 0)
+                t_mm(k, 0, 4)
+            if cur:
+                v_np(c)
+            if fin:
                 v_mask(k, 1)
+                relu_neg(T["pr", k, 1][:, 1, :])
             if cur:
                 evs(c, "p", 0)
                 sums(c, "i", 0)
-                v_nu(c)
             if nxt:
                 s_v(c + 1)
             if fin:
                 v_lo(k, 1)
-                q_sil(k)
-                v_hi(k, 1)
+                quant(k, 4, T["sil", k][:])
             if c == 0:
                 w_quantise()
                 nc.vector.tensor_copy(out=bias_f[:], in_=bias_b[:])
             if cur:
                 evs(c, "p", 1)
                 sums(c, "i", 1)
-                v_np(c)
                 s_silu(c)
             if fin:
-                q_lo(k, 1)
-                q_hi(k, 1)
+                v_hi(k, 1)
+        q_pair(CHUNKS - 1, 1)
+        t_mm(CHUNKS - 1, 4, NFUN)
         s_bias(CHUNKS - 1)
         s_store(CHUNKS - 1)

@@ -181,9 +181,9 @@ def tile_kanoriginal_t_kernel(tc, x, coef, scale_base, scale_sp, bias, out):
             else:
                 nc.scalar.activation(out=dst, in_=src, func=ACT.Relu, bias=0.0, scale=-1.0 / 6.0)
 
-        def v_evi(c):
-            for b in half(c, 1):
-                dst, src = ev_views(c, "i", b)
+        def v_ev_last(c):
+            if BLOCKS[c] == 2:
+                dst, src = ev_views(c, "i", 3)
                 nc.vector.tensor_scalar(out=dst, in0=src, scalar1=-0.5, scalar2=-2.0 / 3.0, op0=ALU.mult, op1=ALU.add)
 
         def pair_tile(c, r):
@@ -198,7 +198,8 @@ def tile_kanoriginal_t_kernel(tc, x, coef, scale_base, scale_sp, bias, out):
 
         def evs(c, kind, h):
             for b in half(c, h):
-                s_ev(c, kind, b)
+                if (kind, b) != ("i", 3):
+                    s_ev(c, kind, b)
 
         def v_merge_nu(c, g):
             if g == 0:
@@ -328,8 +329,7 @@ def tile_kanoriginal_t_kernel(tc, x, coef, scale_base, scale_sp, bias, out):
         s_h0(0)
         s_sq(0)
         s_v(0)
-        for f in range(3):
-            w_copy(f)
+        w_copy(0)
 
         for c in range(CHUNKS + 1):
             k = c - 1
@@ -351,6 +351,7 @@ def tile_kanoriginal_t_kernel(tc, x, coef, scale_base, scale_sp, bias, out):
             if fin:
                 for g in range(PASSES):
                     t_n(k, "nu", g)
+                evs(k, "i", 1)
                 quant(k, 0, T["oc", k][:])
             if cur:
                 v_ng(c)
@@ -364,10 +365,10 @@ def tile_kanoriginal_t_kernel(tc, x, coef, scale_base, scale_sp, bias, out):
             if c >= 2:
                 s_bias(c - 2)
             if c == 0:
-                for f in range(3, NFUN):
+                for f in range(1, NFUN):
                     w_copy(f)
             if fin:
-                v_evi(k)
+                v_ev_last(k)
                 v_mask(k, 0)
                 for g in range(PASSES):
                     v_merge_nu(k, g)

@@ -37,8 +37,9 @@ def tile_kanoriginal_t_kernel(tc, x, coef, scale_base, scale_sp, bias, out):
         const = ctx.enter_context(tc.tile_pool(name="const", bufs=1))
         two = ctx.enter_context(tc.tile_pool(name="two", bufs=2))
         one = ctx.enter_context(tc.tile_pool(name="one", bufs=1))
-        p4 = ctx.enter_context(tc.psum_pool(name="p4", bufs=4))
+        p5 = ctx.enter_context(tc.psum_pool(name="p5", bufs=5))
         p2 = ctx.enter_context(tc.psum_pool(name="p2", bufs=2))
+        p1 = ctx.enter_context(tc.psum_pool(name="p1", bufs=1))
         ctx.enter_context(tc.manual_schedule())
 
         T = {}
@@ -154,15 +155,18 @@ def tile_kanoriginal_t_kernel(tc, x, coef, scale_base, scale_sp, bias, out):
             "i": ("sq", "ng"),
         }
 
-        def t_sum(c, kind, b):
-            g, j = divmod(b, BLOCKS[c])
-            bank = p4.tile([P, 4, P], F32, tag="it", name="ib")
+        def sums(c, kind, h):
+            banks = []
+            for b in half(c, h):
+                T["ib", c, kind, b] = p5.tile([P, 4, P], F32, tag="it", name="ib")
+                banks.append((b, T["ib", c, kind, b]))
             terms = TERMS[kind]
             for t in range(4):
-                lo = ((t % 2) * BLOCKS[c] + j) * BANK + (2 * g + t // 2) * P
                 for i, name in enumerate(terms):
-                    nc.tensor.matmul(bank[:, t, :], lhsT=T[name, c][:, lo:lo + P], rhs=ident_f[:], is_transpose=True, start=(i == 0), stop=(i == len(terms) - 1))
-            T["ib", c, kind, b] = bank
+                    for b, bank in banks:
+                        g, j = divmod(b, BLOCKS[c])
+                        lo = ((t % 2) * BLOCKS[c] + j) * BANK + (2 * g + t // 2) * P
+                        nc.tensor.matmul(bank[:, t, :], lhsT=T[name, c][:, lo:lo + P], rhs=ident_f[:], is_transpose=True, start=(i == 0), stop=(i == len(terms) - 1))
 
         def ev_views(c, kind, b):
             g, j = divmod(b, BLOCKS[c])
@@ -191,10 +195,6 @@ def tile_kanoriginal_t_kernel(tc, x, coef, scale_base, scale_sp, bias, out):
 
         def half(c, h):
             return range(h * BLOCKS[c], (h + 1) * BLOCKS[c])
-
-        def sums(c, kind, h):
-            for b in half(c, h):
-                t_sum(c, kind, b)
 
         def evs(c, kind, h):
             for b in half(c, h):
@@ -235,13 +235,14 @@ def tile_kanoriginal_t_kernel(tc, x, coef, scale_base, scale_sp, bias, out):
             if slot == 0:
                 T["codes", c] = two.tile([P, NFUN * 2 * rows], U32, align_bytes=64, name="codes")
                 T["scales", c] = two.tile([P, NFUN * 2 * rows], U8, align_bytes=64, name="scales")
-                T["acc", c] = p2.tile([P, BANK], F32, tag="acc", name="acc")
             lo = slot * 2 * rows
             hi = lo + count * 2 * rows
             nc.vector.quantize_mx(out=T["codes", c][:, lo:hi].bitcast(FP8X4), scales=T["scales", c][:, lo:hi], in_=src)
 
         def t_mm(c, first, last):
             rows = BLOCKS[c] * P
+            if first == 0:
+                T["acc", c] = p1.tile([P, BANK], F32, tag="acc", name="acc")
             for slot in range(first, last):
                 for g in range(PASSES):
                     wlo = (SLOT_FUN[slot] * PASSES + g) * OUTS

@@ -71,7 +71,7 @@ def tile_kanoriginal_t_kernel(tc, x, coef, scale_base, scale_sp, bias, out):
             T[name, c] = t
 
         def s_e0(c):
-            t = two.tile([P, BLOCKS[c] * FEAT], F32, name="e0")
+            t = one.tile([P, BLOCKS[c] * FEAT], F32, name="e0")
             nc.scalar.activation(
                 out=t[:].rearrange("p (e m) -> p e m", e=2),
                 in_=T["xs", c][:].rearrange("p (m e) -> p e m", e=2),
@@ -80,7 +80,7 @@ def tile_kanoriginal_t_kernel(tc, x, coef, scale_base, scale_sp, bias, out):
             T["e0", c] = t
 
         def s_h0(c):
-            nat(two, c, "h0", "e0", ACT.Abs, 2.0, -4.0)
+            nat(one, c, "h0", "e0", ACT.Abs, 2.0, -4.0)
 
         def s_sq(c):
             nat(two, c, "sq", "h0", ACT.Square, 0.5, -1.0)
@@ -131,12 +131,10 @@ def tile_kanoriginal_t_kernel(tc, x, coef, scale_base, scale_sp, bias, out):
             ts(c, "rm", "q2", ALU.min, 0.0, ALU.mult, -1.0)
 
         def v_lc(c):
-            t = T["e0", c]
-            nc.vector.tensor_scalar(out=t[:], in0=t[:], scalar1=3.0, scalar2=-4.0, op0=ALU.mult, op1=ALU.add)
+            ts(c, "lc", "e0", ALU.mult, 3.0, ALU.add, -4.0)
 
         def v_lp(c):
-            t = T["h0", c]
-            nc.vector.tensor_scalar(out=t[:], in0=t[:], scalar1=1.5, scalar2=-4.0, op0=ALU.mult, op1=ALU.add)
+            ts(c, "lp", "h0", ALU.mult, 1.5, ALU.add, -4.0)
 
         def v_nu(c):
             T["nu", c] = one.tile([P, BLOCKS[c] * FEAT], BF16, align_bytes=64, name="nu")
@@ -150,8 +148,8 @@ def tile_kanoriginal_t_kernel(tc, x, coef, scale_base, scale_sp, bias, out):
             T[name + "t", c, g] = words_t(c, T[name, c], g)
 
         TERMS = {
-            "c": ("rm", "q2", "e0", "ng"),
-            "p": ("h0", "ng", "rm"),
+            "c": ("rm", "q2", "lc", "ng"),
+            "p": ("lp", "ng", "rm"),
             "i": ("sq", "ng"),
         }
 
@@ -243,35 +241,28 @@ def tile_kanoriginal_t_kernel(tc, x, coef, scale_base, scale_sp, bias, out):
             rows = BLOCKS[c] * P
             if first == 0:
                 T["acc", c] = p1.tile([P, BANK], F32, tag="acc", name="acc")
-            for slot in range(first, last):
-                for g in range(PASSES):
-                    wlo = (SLOT_FUN[slot] * PASSES + g) * OUTS
-                    lo = (slot * PASSES + g) * rows
-                    nc.tensor.matmul_mx(
-                        out=T["acc", c][:, 0:rows],
-                        lhsT=wcodes[:, wlo:wlo + OUTS].bitcast(FP8X4),
-                        lhsT_scale=wscales[:, wlo:wlo + OUTS],
-                        rhs=T["codes", c][:, lo:lo + rows].bitcast(FP8X4),
-                        rhs_scale=T["scales", c][:, lo:lo + rows],
-                        start=(slot == 0 and g == 0),
-                        stop=(slot == NFUN - 1 and g == PASSES - 1),
-                    )
+            for j in range(BLOCKS[c]):
+                for slot in range(first, last):
+                    for g in range(PASSES):
+                        wlo = (SLOT_FUN[slot] * PASSES + g) * OUTS
+                        lo = (slot * PASSES + g) * rows + j * P
+                        nc.tensor.matmul_mx(
+                            out=T["acc", c][:, j * OUTS:(j + 1) * OUTS],
+                            lhsT=T["codes", c][:, lo:lo + P].bitcast(FP8X4),
+                            lhsT_scale=T["scales", c][:, lo:lo + P],
+                            rhs=wcodes[:, wlo:wlo + OUTS].bitcast(FP8X4),
+                            rhs_scale=wscales[:, wlo:wlo + OUTS],
+                            start=(slot == 0 and g == 0),
+                            stop=(slot == NFUN - 1 and g == PASSES - 1),
+                        )
 
         def q_pair(c, r):
             quant(c, 2 if r == 0 else 5, T["pr", c, r][:].rearrange("p s w -> p (s w)"), 2)
 
-        def s_bias(c):
-            rows = BLOCKS[c] * P
-            o_t = one.tile([P, rows], F32, name="o_t")
-            nc.scalar.activation(out=o_t[:], in_=T["acc", c][:, 0:rows], func=ACT.Identity, bias=bias_f[:, 0:1], scale=1.0)
-            rt = p2.tile([P, BANK], F32, tag="nt", name="rt")
-            for j in range(BLOCKS[c]):
-                nc.tensor.transpose(rt[:, j * OUTS:(j + 1) * OUTS], o_t[:, j * P:(j + 1) * P], ident_f[:])
-            T["rt", c] = rt
-
-        def s_store(c):
-            res = two.tile([P, BLOCKS[c] * OUTS], F32, name="res")
-            nc.scalar.copy(out=res[:], in_=T["rt", c][:, 0:BLOCKS[c] * OUTS])
+        def v_out(c):
+            n = BLOCKS[c] * OUTS
+            res = two.tile([P, n], F32, name="res")
+            nc.vector.tensor_tensor(out=res[:], in0=T["acc", c][:, 0:n], in1=bias_bc[:, 0:n], op=ALU.add)
             nc.sync.dma_start(out=of[rows_of[c], :].rearrange("(p j) o -> p (j o)", j=BLOCKS[c]), in_=res[:])
 
         load_x(0)
@@ -290,6 +281,15 @@ def tile_kanoriginal_t_kernel(tc, x, coef, scale_base, scale_sp, bias, out):
         make_identity(nc, ident_b[:])
 
         bias_f = const.tile([P, 1], F32)
+        bias_bc = const.tile([P, 2 * OUTS], F32)
+
+        def w_bias():
+            bank = p2.tile([P, P], F32, tag="nt", name="bt")
+            nc.vector.tensor_copy(out=bias_f[:], in_=bias_b[:])
+            nc.tensor.transpose(bank[:], bias_f[:].to_broadcast([P, P]), ident_f[:])
+            for j in range(2):
+                nc.vector.tensor_copy(out=bias_bc[:, j * OUTS:(j + 1) * OUTS], in_=bank[:])
+
         wg = two.tile([P, NFUN, PASSES, OUTS, 4], BF16, align_bytes=64, tag="codes", name="wg")
         coef_v = coef_sb[:].rearrange("o (w p e b) -> o b w e p", w=4, p=P, e=2, b=NB)
         spg = const.tile([P, PASSES, OUTS, 4], BF16)
@@ -342,7 +342,7 @@ def tile_kanoriginal_t_kernel(tc, x, coef, scale_base, scale_sp, bias, out):
                 s_e1(c)
             if c >= 2:
                 q_pair(c - 2, 1)
-                t_mm(c - 2, 4, NFUN)
+                t_mm(c - 2, 0, NFUN)
             if fin:
                 evs(k, "i", 0)
             if nxt and c >= 1:
@@ -363,11 +363,10 @@ def tile_kanoriginal_t_kernel(tc, x, coef, scale_base, scale_sp, bias, out):
                 v_lp(c)
                 sums(c, "c", 1)
                 s_sp(c)
-            if c >= 2:
-                s_bias(c - 2)
             if c == 0:
                 for f in range(1, NFUN):
                     w_copy(f)
+                w_bias()
             if fin:
                 v_ev_last(k)
                 v_mask(k, 0)
@@ -377,7 +376,7 @@ def tile_kanoriginal_t_kernel(tc, x, coef, scale_base, scale_sp, bias, out):
             if nxt:
                 s_e0(c + 1)
             if c >= 2:
-                s_store(c - 2)
+                v_out(c - 2)
             if cur:
                 evs(c, "c", 0)
                 sums(c, "p", 0)
@@ -403,6 +402,7 @@ def tile_kanoriginal_t_kernel(tc, x, coef, scale_base, scale_sp, bias, out):
                 s_sq(c + 1)
             if fin:
                 q_pair(k, 0)
+            if c == CHUNKS:
                 t_mm(k, 0, 4)
             if cur:
                 v_np(c)
@@ -419,7 +419,6 @@ def tile_kanoriginal_t_kernel(tc, x, coef, scale_base, scale_sp, bias, out):
                 quant(k, 4, T["sil", k][:])
             if c == 0:
                 w_quantise()
-                nc.vector.tensor_copy(out=bias_f[:], in_=bias_b[:])
             if cur:
                 evs(c, "p", 1)
                 sums(c, "i", 1)
@@ -428,5 +427,4 @@ def tile_kanoriginal_t_kernel(tc, x, coef, scale_base, scale_sp, bias, out):
                 v_hi(k, 1)
         q_pair(CHUNKS - 1, 1)
         t_mm(CHUNKS - 1, 4, NFUN)
-        s_bias(CHUNKS - 1)
-        s_store(CHUNKS - 1)
+        v_out(CHUNKS - 1)

import math
from contextlib import ExitStack

import concourse.mybir as mybir
from concourse.masks import make_identity

F32 = mybir.dt.float32
BF16 = mybir.dt.bfloat16
U32 = mybir.dt.uint32
U8 = mybir.dt.uint8
FP8X4 = mybir.dt.float8_e4m3fn_x4
ACT = mybir.ActivationFunctionType
ALU = mybir.AluOpType

P = 128
ROWS = 4096
FEAT = 1024
OUTS = 128
NB = 6
NFUN = NB + 1
PASSES = 2
BLOCKS = (1,) + (2,) * 15 + (1,)
CHUNKS = len(BLOCKS)
BANK = 512
FLOPS = 2 * ROWS * FEAT * OUTS * NFUN
C6 = 1.0 / math.sqrt(6.0)
C3 = 1.0 / math.sqrt(3.0)
SILU_KNOT = (-1.0 / 3.0 / (1.0 + math.exp(1.0 / 3.0)), 1.0 / 3.0 / (1.0 + math.exp(-1.0 / 3.0)))


def tile_kanoriginal_t_kernel(tc, x, coef, scale_base, scale_sp, bias, out):
    nc = tc.nc
    xf = x.flatten_outer_dims()
    of = out.flatten_outer_dims()
    rows_of = [slice(P * sum(BLOCKS[:c]), P * sum(BLOCKS[:c + 1])) for c in range(CHUNKS)]
    with ExitStack() as ctx:
        const = ctx.enter_context(tc.tile_pool(name="const", bufs=1))
        two = ctx.enter_context(tc.tile_pool(name="two", bufs=2))
        one = ctx.enter_context(tc.tile_pool(name="one", bufs=1))
        p5 = ctx.enter_context(tc.psum_pool(name="p5", bufs=5))
        p2 = ctx.enter_context(tc.psum_pool(name="p2", bufs=2))
        p1 = ctx.enter_context(tc.psum_pool(name="p1", bufs=1))
        ctx.enter_context(tc.manual_schedule())

        T = {}

        def split(c, ap, g):
            hw = BLOCKS[c] * BANK
            return ap[:, g * hw:(g + 1) * hw].rearrange("p (n u e) -> p n u e", u=2, e=2)

        def bank_bf(tile):
            return tile[:].bitcast(BF16).rearrange("p u (n e) -> p n u e", e=2)

        def load_x(c):
            xs = two.tile([P, BLOCKS[c] * FEAT], BF16, name="xs")
            nc.sync.dma_start(out=xs[:], in_=xf[rows_of[c], :].rearrange("(p j) i -> p (j i)", j=BLOCKS[c]))
            T["xs", c] = xs

        def words_t(c, src, g):
            wv = src[:].bitcast(F32)
            bank = p2.tile([P, 2, BLOCKS[c] * P], F32, tag="nt", name="wb")
            for j in range(BLOCKS[c]):
                for u in range(2):
                    lo = j * BANK + (2 * g + u) * P
                    nc.tensor.transpose(bank[:, u, j * P:(j + 1) * P], wv[:, lo:lo + P], ident_f[:])
            return bank

        def nat(pool, c, name, src, func, scale, shift):
            t = pool.tile([P, BLOCKS[c] * FEAT], F32, name=name)
            nc.scalar.activation(out=t[:], in_=T[src, c][:], func=func, bias=shift, scale=scale)
            T[name, c] = t

        def s_e0(c):
            t = one.tile([P, BLOCKS[c] * FEAT], F32, name="e0")
            nc.scalar.activation(
                out=t[:].rearrange("p (e m) -> p e m", e=2),
                in_=T["xs", c][:].rearrange("p (m e) -> p e m", e=2),
                func=ACT.Abs, bias=0.5, scale=1.5,
            )
            T["e0", c] = t

        def s_h0(c):
            nat(one, c, "h0", "e0", ACT.Abs, 2.0, -4.0)

        def s_sq(c):
            nat(two, c, "sq", "h0", ACT.Square, 0.5, -1.0)

        def s_v(c):
            t = one.tile([P, BLOCKS[c] * FEAT], F32, name="v")
            nc.scalar.activation(out=t[:], in_=T["h0", c][:], func=ACT.Abs, bias=-1.0, scale=0.5)
            T["v", c] = t

        def s_e1(c):
            nat(one, c, "e1", "xs", ACT.Abs, 1.5, -0.5)

        def s_h1(c):
            nat(one, c, "h1", "e1", ACT.Abs, 0.5, -1.0)

        def s_su(c):
            nat(one, c, "su", "e1", ACT.Square, C6, -2.0 * C6)

        def s_sp(c):
            nat(one, c, "sp", "h1", ACT.Square, 2.0 * C3, -2.0 * C3)

        def s_silu(c):
            sil = two.tile([P, BLOCKS[c] * FEAT], BF16, align_bytes=64, name="sil")
            for g in range(PASSES):
                nc.scalar.activation(out=split(c, sil, g), in_=bank_bf(T["xt", c, g]), func=ACT.Silu)
            T["sil", c] = sil

        def t_x(c):
            for g in range(PASSES):
                T["xt", c, g] = words_t(c, T["xs", c], g)

        def stt(c, dst, lin, shift, square):
            nc.vector.scalar_tensor_tensor(out=dst[:], in0=T[lin, c][:], scalar=shift, in1=T[square, c][:], op0=ALU.add, op1=ALU.mult)

        def v_q2(c):
            T["q2", c] = one.tile([P, BLOCKS[c] * FEAT], F32, name="q2")
            stt(c, T["q2", c], "h0", -2.0, "sq")

        def v_ng(c):
            T["ng", c] = two.tile([P, BLOCKS[c] * FEAT], F32, name="ng")
            stt(c, T["ng", c], "v", -3.0, "sq")

        def ts(c, name, src, op0, s1, op1, s2):
            T[name, c] = one.tile([P, BLOCKS[c] * FEAT], F32, name=name)
            nc.vector.tensor_scalar(out=T[name, c][:], in0=T[src, c][:], scalar1=s1, scalar2=s2, op0=op0, op1=op1)

        def v_rm(c):
            ts(c, "rm", "q2", ALU.min, 0.0, ALU.mult, -1.0)

        def v_lc(c):
            ts(c, "lc", "e0", ALU.mult, 3.0, ALU.add, -4.0)

        def v_lp(c):
            ts(c, "lp", "h0", ALU.mult, 1.5, ALU.add, -4.0)

        def v_nu(c):
            T["nu", c] = one.tile([P, BLOCKS[c] * FEAT], BF16, align_bytes=64, name="nu")
            stt(c, T["nu", c], "e1", -2.0, "su")

        def v_np(c):
            T["np", c] = one.tile([P, BLOCKS[c] * FEAT], BF16, align_bytes=64, name="np")
            stt(c, T["np", c], "h1", -1.0, "sp")

        def t_n(c, name, g):
            T[name + "t", c, g] = words_t(c, T[name, c], g)

        TERMS = {
            "c": ("rm", "q2", "lc", "ng"),
            "p": ("lp", "ng", "rm"),
            "i": ("sq", "ng"),
        }

        def sums(c, kind, h):
            banks = []
            for b in half(c, h):
                T["ib", c, kind, b] = p5.tile([P, 4, P], F32, tag="it", name="ib")
                banks.append((b, T["ib", c, kind, b]))
            terms = TERMS[kind]
            for t in range(4):
                for i, name in enumerate(terms):
                    for b, bank in banks:
                        g, j = divmod(b, BLOCKS[c])
                        lo = ((t % 2) * BLOCKS[c] + j) * BANK + (2 * g + t // 2) * P
                        nc.tensor.matmul(bank[:, t, :], lhsT=T[name, c][:, lo:lo + P], rhs=ident_f[:], is_transpose=True, start=(i == 0), stop=(i == len(terms) - 1))

        def ev_views(c, kind, b):
            g, j = divmod(b, BLOCKS[c])
            if b == 0 and kind == "p":
                pair_tile(c, 0)
            elif b == 0:
                T["o" + kind, c] = one.tile([P, BLOCKS[c] * FEAT], BF16, align_bytes=64, name="o" + kind)
            tile = T["pr", c, 0][:, 1, :] if kind == "p" else T["o" + kind, c][:]
            lo = (g * BLOCKS[c] + j) * BANK
            return tile[:, lo:lo + BANK].rearrange("p (n t) -> p n t", t=4), T["ib", c, kind, b][:].rearrange("p t n -> p n t")

        def s_ev(c, kind, b):
            dst, src = ev_views(c, kind, b)
            if kind == "i":
                nc.scalar.activation(out=dst, in_=src, func=ACT.Identity, bias=-2.0 / 3.0, scale=-0.5)
            else:
                nc.scalar.activation(out=dst, in_=src, func=ACT.Relu, bias=0.0, scale=-1.0 / 6.0)

        def v_ev_last(c):
            if BLOCKS[c] == 2:
                dst, src = ev_views(c, "i", 3)
                nc.vector.tensor_scalar(out=dst, in0=src, scalar1=-0.5, scalar2=-2.0 / 3.0, op0=ALU.mult, op1=ALU.add)

        def pair_tile(c, r):
            T["pr", c, r] = (two if r == 0 else one).tile([P, 2, BLOCKS[c] * FEAT], BF16, align_bytes=64, name="pr%d" % r)

        def half(c, h):
            return range(h * BLOCKS[c], (h + 1) * BLOCKS[c])

        def evs(c, kind, h):
            for b in half(c, h):
                if (kind, b) != ("i", 3):
                    s_ev(c, kind, b)

        def v_merge_nu(c, g):
            if g == 0:
                T["num", c] = one.tile([P, BLOCKS[c] * FEAT], BF16, align_bytes=64, name="num")
            merge(c, T["num", c][:], "nu", g)

        def v_merge_np(c, g):
            if g == 0:
                pair_tile(c, 1)
            merge(c, T["pr", c, 1][:, 1, :], "np", g)

        def merge(c, dst, name, g):
            nc.vector.tensor_tensor(out=split(c, dst, g), in0=bank_bf(T[name + "t", c, g]), in1=split(c, T["oi", c], g), op=ALU.max)

        def relu_neg(t):
            nc.vector.tensor_scalar(out=t, in0=t, scalar1=-1.0, scalar2=0.0, op0=ALU.mult, op1=ALU.max)

        def v_mask(c, r):
            nc.vector.tensor_scalar(out=T["pr", c, r][:, 0, :], in0=T["sil", c][:], scalar1=SILU_KNOT[r], scalar2=None, op0=ALU.is_lt)

        def v_lo(c, r):
            t = T["pr", c, r]
            nc.vector.tensor_tensor(out=t[:, 0, :], in0=t[:, 1, :], in1=t[:, 0, :], op=ALU.mult)

        def v_hi(c, r):
            t = T["pr", c, r]
            nc.vector.tensor_tensor(out=t[:, 1, :], in0=t[:, 1, :], in1=t[:, 0, :], op=ALU.subtract)

        SLOT_FUN = (3, 4, 1, 5, 0, 2, 6)

        def quant(c, slot, src, count=1):
            rows = BLOCKS[c] * P
            if slot == 0:
                T["codes", c] = two.tile([P, NFUN * 2 * rows], U32, align_bytes=64, name="codes")
                T["scales", c] = two.tile([P, NFUN * 2 * rows], U8, align_bytes=64, name="scales")
            lo = slot * 2 * rows
            hi = lo + count * 2 * rows
            nc.vector.quantize_mx(out=T["codes", c][:, lo:hi].bitcast(FP8X4), scales=T["scales", c][:, lo:hi], in_=src)

        def t_mm(c, first, last):
            rows = BLOCKS[c] * P
            if first == 0:
                T["acc", c] = p1.tile([P, BANK], F32, tag="acc", name="acc")
            for j in range(BLOCKS[c]):
                for slot in range(first, last):
                    for g in range(PASSES):
                        wlo = (SLOT_FUN[slot] * PASSES + g) * OUTS
                        lo = (slot * PASSES + g) * rows + j * P
                        nc.tensor.matmul_mx(
                            out=T["acc", c][:, j * OUTS:(j + 1) * OUTS],
                            lhsT=T["codes", c][:, lo:lo + P].bitcast(FP8X4),
                            lhsT_scale=T["scales", c][:, lo:lo + P],
                            rhs=wcodes[:, wlo:wlo + OUTS].bitcast(FP8X4),
                            rhs_scale=wscales[:, wlo:wlo + OUTS],
                            start=(slot == 0 and g == 0),
                            stop=(slot == NFUN - 1 and g == PASSES - 1),
                        )

        def q_pair(c, r):
            quant(c, 2 if r == 0 else 5, T["pr", c, r][:].rearrange("p s w -> p (s w)"), 2)

        def v_out(c):
            n = BLOCKS[c] * OUTS
            res = two.tile([P, n], F32, name="res")
            nc.vector.tensor_tensor(out=res[:], in0=T["acc", c][:, 0:n], in1=bias_bc[:, 0:n], op=ALU.add)
            nc.sync.dma_start(out=of[rows_of[c], :].rearrange("(p j) o -> p (j o)", j=BLOCKS[c]), in_=res[:])

        load_x(0)
        sp_sb = const.tile([P, FEAT], BF16)
        nc.sync.dma_start(out=sp_sb[:], in_=scale_sp)
        sb_sb = const.tile([P, FEAT], BF16)
        nc.sync.dma_start(out=sb_sb[:], in_=scale_base)
        coef_sb = two.tile([P, FEAT * NB], BF16, align_bytes=64, tag="codes", name="coef_sb")
        nc.sync.dma_start(out=coef_sb[:], in_=coef.rearrange("o i b -> o (i b)"))
        bias_b = const.tile([P, 1], BF16)
        nc.sync.dma_start(out=bias_b[:], in_=bias.rearrange("(o a) -> o a", a=1))
        load_x(1)
        ident_f = const.tile([P, P], F32)
        make_identity(nc, ident_f[:])
        ident_b = const.tile([P, P], BF16)
        make_identity(nc, ident_b[:])

        bias_f = const.tile([P, 1], F32)
        bias_bc = const.tile([P, 2 * OUTS], F32)

        def w_bias():
            bank = p2.tile([P, P], F32, tag="nt", name="bt")
            nc.vector.tensor_copy(out=bias_f[:], in_=bias_b[:])
            nc.tensor.transpose(bank[:], bias_f[:].to_broadcast([P, P]), ident_f[:])
            for j in range(2):
                nc.vector.tensor_copy(out=bias_bc[:, j * OUTS:(j + 1) * OUTS], in_=bank[:])

        wg = two.tile([P, NFUN, PASSES, OUTS, 4], BF16, align_bytes=64, tag="codes", name="wg")
        coef_v = coef_sb[:].rearrange("o (w p e b) -> o b w e p", w=4, p=P, e=2, b=NB)
        spg = const.tile([P, PASSES, OUTS, 4], BF16)
        wcodes = const.tile([P, NFUN * PASSES * OUTS], U32, align_bytes=64)
        wscales = const.tile([P, NFUN * PASSES * OUTS], U8, align_bytes=64)
        wg_flat = wg[:].rearrange("p f g o t -> p (f g o t)")

        def w_words(src, dst):
            wt0 = p2.tile([P, PASSES, 2, OUTS], F32, tag="nt", name="wt0")
            for g in range(PASSES):
                for u in range(2):
                    k = 2 * g + u
                    nc.tensor.transpose(wt0[:, g, u, :], src[:, k * P:(k + 1) * P], ident_f[:])
            nc.vector.tensor_copy(out=dst.bitcast(F32), in_=wt0[:].rearrange("p g u o -> p g o u"))

        def w_copy(f):
            if f == 0:
                w_words(sp_sb[:].bitcast(F32), spg[:])
                w_words(sb_sb[:].bitcast(F32), wg[:, 0])
            else:
                wtb = p2.tile([P, PASSES, 4, OUTS], BF16, tag="nt", name="wtb")
                for g in range(PASSES):
                    for t in range(4):
                        nc.tensor.transpose(wtb[:, g, t, :], coef_v[:, f - 1, 2 * g + t // 2, t % 2, :], ident_b[:])
                nc.vector.tensor_tensor(out=wg[:, f], in0=wtb[:].rearrange("p g t o -> p g o t"), in1=spg[:], op=ALU.mult)

        def w_quantise():
            first = 0
            for width in (4096, 2048, 1024):
                nc.vector.quantize_mx(
                    out=wcodes[:, first // 4:(first + width) // 4].bitcast(FP8X4),
                    scales=wscales[:, first // 4:(first + width) // 4],
                    in_=wg_flat[:, first:first + width],
                )
                first += width

        s_e0(0)
        s_h0(0)
        s_sq(0)
        s_v(0)
        w_copy(0)

        for c in range(CHUNKS + 1):
            k = c - 1
            cur = c < CHUNKS
            fin = c >= 1
            nxt = c + 1 < CHUNKS
            if cur:
                v_q2(c)
                s_e1(c)
            if c >= 2:
                q_pair(c - 2, 1)
                t_mm(c - 2, 0, NFUN)
            if fin:
                evs(k, "i", 0)
            if nxt and c >= 1:
                load_x(c + 1)
            if cur:
                s_h1(c)
            if fin:
                for g in range(PASSES):
                    t_n(k, "nu", g)
                evs(k, "i", 1)
                quant(k, 0, T["oc", k][:])
            if cur:
                v_ng(c)
                v_rm(c)
                v_lc(c)
                sums(c, "c", 0)
                s_su(c)
                v_lp(c)
                sums(c, "c", 1)
                s_sp(c)
            if c == 0:
                for f in range(1, NFUN):
                    w_copy(f)
                w_bias()
            if fin:
                v_ev_last(k)
                v_mask(k, 0)
                for g in range(PASSES):
                    v_merge_nu(k, g)
                    t_n(k, "np", g)
            if nxt:
                s_e0(c + 1)
            if c >= 2:
                v_out(c - 2)
            if cur:
                evs(c, "c", 0)
                sums(c, "p", 0)
            if fin:
                v_lo(k, 0)
                relu_neg(T["num", k][:])
            if cur:
                v_nu(c)
            if fin:
                v_hi(k, 0)
                quant(k, 1, T["num", k][:])
            if nxt:
                s_h0(c + 1)
            if cur:
                evs(c, "c", 1)
                sums(c, "p", 1)
            if fin:
                for g in range(PASSES):
                    v_merge_np(k, g)
            if cur:
                t_x(c)
            if nxt:
                s_sq(c + 1)
            if fin:
                q_pair(k, 0)
            if c == CHUNKS:
                t_mm(k, 0, 4)
            if cur:
                v_np(c)
            if fin:
                v_mask(k, 1)
                relu_neg(T["pr", k, 1][:, 1, :])
            if cur:
                evs(c, "p", 0)
                sums(c, "i", 0)
            if nxt:
                s_v(c + 1)
            if fin:
                v_lo(k, 1)
                quant(k, 4, T["sil", k][:])
            if c == 0:
                w_quantise()
            if cur:
                evs(c, "p", 1)
                sums(c, "i", 1)
                s_silu(c)
            if fin:
                v_hi(k, 1)
        q_pair(CHUNKS - 1, 1)
        t_mm(CHUNKS - 1, 4, NFUN)
        v_out(CHUNKS - 1)
